import numpy as np
import ml_dtypes


def mxq(x, axis, fmt="e4m3"):
    dtype, down = {"e4m3": (ml_dtypes.float8_e4m3fn, 7), "e5m2": (ml_dtypes.float8_e5m2, 14)}[fmt]
    v = np.moveaxis(np.asarray(x, np.float32).astype(ml_dtypes.bfloat16).astype(np.float64), axis, -1)
    blocks = v.reshape(v.shape[:-1] + (-1, 32))
    amax = np.abs(blocks).max(-1, keepdims=True)
    byte = np.maximum(np.where(amax > 0, np.frexp(amax)[1] - 1 + 127, 0) - down, 1)
    scale = np.exp2(byte - 127.0)
    codes = (blocks / scale).astype(np.float32).astype(dtype).astype(np.float64)
    return np.moveaxis((codes * scale).reshape(v.shape), -1, axis)


WIDE = False


def mx_kscale(k):
    if not WIDE:
        return np.ones(k)
    levels = np.array([10, -10, 5, -5, 0])
    a = np.random.permutation(np.resize(levels, k // 512 * 4)).reshape(k // 512, 4)
    idx = np.arange(k)
    return np.exp2(a[idx // 512, idx % 128 // 32])


BF16 = ml_dtypes.bfloat16


def bf(x):
    return np.asarray(x, np.float32).astype(BF16)


def f64(x):
    return np.asarray(x).astype(np.float64)


B, H, W, C, NH, KD = 1, 32, 32, 512, 4, 128
L = H * W
DV = C // NH
SCALE = 1.0 / np.sqrt(KD)


def rel_to_abs(r):
    b, n, w, _ = r.shape
    r = np.pad(r, ((0, 0), (0, 0), (0, 0), (0, 1)))
    r = r.reshape(b, n, w * 2 * w)
    r = np.pad(r, ((0, 0), (0, 0), (0, w - 1)))
    r = r.reshape(b, n, w + 1, 2 * w - 1)
    return r[:, :, :w, w - 1:]


def setup_inputs():
    s = mx_kscale(C)
    return {"q": bf(np.random.standard_normal((B, NH, L, KD))),
            "k": bf(np.random.standard_normal((B, NH, L, KD))),
            "x": bf(np.random.standard_normal((B, H, W, C)) * s),
            "w_v": bf(np.random.standard_normal((C, C)) * 2.0 / np.sqrt(C) / s[:, None]),
            "rel_w": bf(np.random.standard_normal((B, NH, H, W, 2 * W - 1))),
            "rel_h": bf(np.random.standard_normal((B, NH, W, H, 2 * H - 1)))}


def reference(q, k, x, w_v, rel_w, rel_h):
    v = mxq(f64(x).reshape(B, L, C), 2, "e4m3") @ mxq(f64(w_v), 0, "e4m3")
    v = v.reshape(B, L, NH, DV).transpose(0, 2, 1, 3)
    rw = rel_to_abs(f64(rel_w).reshape(B, NH * H, W, 2 * W - 1)).reshape(B, NH, H, W, W)
    rh = rel_to_abs(f64(rel_h).reshape(B, NH * W, H, 2 * H - 1)).reshape(B, NH, W, H, H)
    pos = rw[:, :, :, :, None, :] + rh.swapaxes(2, 3)[:, :, :, :, :, None]
    pos = pos.reshape(B, NH, L, L)
    sc = f64(q) @ f64(k).transpose(0, 1, 3, 2) * SCALE + pos
    e = np.exp(sc - sc.max(-1, keepdims=True))
    o = (mxq(e, 3, "e4m3") @ mxq(v, 2, "e4m3")) / e.sum(-1, keepdims=True)
    return o.transpose(0, 2, 1, 3).reshape(B, H, W, C)

@@ -1,0 +1,233 @@
+from contextlib import ExitStack
+
+import concourse.mybir as mybir
+from concourse.masks import make_identity
+
+F32 = mybir.dt.float32
+BF16 = mybir.dt.bfloat16
+U32 = mybir.dt.uint32
+U8 = mybir.dt.uint8
+FP8X4 = mybir.dt.float8_e4m3fn_x4
+ALU = mybir.AluOpType
+ACT = mybir.ActivationFunctionType
+AX = mybir.AxisListType
+
+P = 128
+PACK = 4
+GRID = 32
+L = GRID * GRID
+C = 512
+NH = 4
+D = 128
+NT = L // P
+NG = L // (P * PACK)
+HALF = 512
+REL = 2 * GRID - 1
+ROWS = P // GRID
+SCALE = 1.0 / (D ** 0.5)
+
+FLOPS = 2 * L * C * C + 2 * 2 * NH * L * L * D
+LAG = 2
+
+
+def tile_relativepositionmultiheadattention_pa_kernel(tc, q, k, x, w_v, rel_w, rel_h, out):
+    nc = tc.nc
+    with ExitStack() as ctx:
+        keep = ctx.enter_context(tc.tile_pool(name="keep", bufs=1))
+        bias = ctx.enter_context(tc.tile_pool(name="bias", bufs=4))
+        work = ctx.enter_context(tc.tile_pool(name="work", bufs=3))
+        late = ctx.enter_context(tc.tile_pool(name="late", bufs=LAG + 2))
+        psum_s = ctx.enter_context(tc.psum_pool(name="psum_s", bufs=4))
+        psum_t = ctx.enter_context(tc.psum_pool(name="psum_t", bufs=2))
+        psum_o = ctx.enter_context(tc.psum_pool(name="psum_o", bufs=2))
+
+        ident_bf = keep.tile([P, P], BF16)
+        make_identity(nc, ident_bf[:])
+        ident_f32 = keep.tile([P, P], F32)
+        make_identity(nc, ident_f32[:])
+
+        col_bias = keep.tile([P, NH * NT, GRID], BF16)
+        row_bias = keep.tile([P, NH * NT, GRID], BF16)
+        skew = REL - 1
+        rw = rel_w.rearrange("b n r c m -> (b n r) (c m)")[:, GRID - 1 : GRID - 1 + skew * GRID]
+        rw = rw.rearrange("a (c j) -> a c j", j=skew)[:, :, 0:GRID]
+        rw = rw.rearrange("(i rl) c j -> rl c i j", rl=ROWS)
+        rh = rel_h.rearrange("b n c r m -> (b n c) (r m)")[:, GRID - 1 : GRID - 1 + skew * GRID]
+        rh = rh.rearrange("a (r j) -> a r j", j=skew)[:, :, 0:GRID]
+        rh = rh.rearrange("(n c) (t rl) j -> n rl c t j", c=GRID, rl=ROWS)
+
+        def load_row_bias(n):
+            for rl in range(ROWS):
+                nc.sync.dma_start(
+                    out=row_bias[GRID * rl : GRID * (rl + 1), NT * n : NT * (n + 1), :], in_=rh[n, rl]
+                )
+
+        q_rows = q.rearrange("b n (t p) d -> (b n) p t d", p=P)
+        k_rows = k.rearrange("b n (t p) d -> (b n) p t d", p=P)
+        q_sb = []
+        k_sb = []
+        for n in range(NH):
+            k_sb.append(keep.tile([P, NT, D], BF16, name="k_sb%d" % n))
+            q_sb.append(keep.tile([P, NT, D], BF16, name="q_sb%d" % n))
+        nc.sync.dma_start(out=k_sb[0][:], in_=k_rows[0])
+        nc.sync.dma_start(out=q_sb[0][:], in_=q_rows[0])
+        for rl in range(ROWS):
+            nc.sync.dma_start(out=col_bias[GRID * rl : GRID * (rl + 1), :, :], in_=rw[rl])
+        load_row_bias(0)
+        x_sb = keep.tile([P, NT * C], BF16)
+        nc.sync.dma_start(
+            out=x_sb[:].rearrange("p (t c) -> p t c", c=C),
+            in_=x.rearrange("b h w c -> (b h w) c").rearrange("(t p) c -> p t c", p=P),
+        )
+        w_sb = keep.tile([P, PACK, C], BF16)
+        nc.sync.dma_start(
+            out=w_sb[:].rearrange("p (u e) c -> p u (e c)", e=2),
+            in_=w_v.rearrange("(u p e) c -> p u (e c)", u=2, e=2),
+        )
+        for n in range(1, NH):
+            load_row_bias(n)
+            nc.sync.dma_start(out=k_sb[n][:], in_=k_rows[n])
+            nc.sync.dma_start(out=q_sb[n][:], in_=q_rows[n])
+
+        qT = keep.tile([P, NH, L], BF16)
+        kT = keep.tile([P, NH, L], BF16)
+
+        def turn_head(n):
+            k_ps = psum_t.tile([P, NT, P], BF16, tag="turned")
+            for t in range(NT):
+                nc.tensor.transpose(out=k_ps[:, t, :], in_=k_sb[n][:, t, :], identity=ident_bf[:])
+            nc.vector.tensor_copy(out=kT[:, n, :], in_=k_ps[:].rearrange("p t l -> p (t l)"))
+            q_ps = psum_t.tile([P, NT, P], BF16, tag="turned")
+            for t in range(NT):
+                nc.tensor.transpose(out=q_ps[:, t, :], in_=q_sb[n][:, t, :], identity=ident_bf[:])
+            nc.scalar.copy(out=qT[:, n, :], in_=q_ps[:].rearrange("p t l -> p (t l)"))
+
+        v_codes = keep.tile([P, NG, C], U32, align_bytes=64)
+        v_scales = keep.tile([P, NG, C], U8, align_bytes=64)
+
+        def project_values():
+            x_words = x_sb[:].bitcast(F32)
+            x_grouped = keep.tile([P, L * PACK], BF16, align_bytes=64)
+            x_grouped_words = x_grouped[:].bitcast(F32).rearrange("p (l u) -> p l u", u=2)
+            for b in range(NT // 2):
+                x_ps = psum_o.tile([P, 2, 2, P], F32, tag="acc")
+                for tt in range(2):
+                    for u in range(2):
+                        first = (C // 2) * (2 * b + tt) + P * u
+                        nc.tensor.transpose(
+                            out=x_ps[:, tt, u, :], in_=x_words[:, first : first + P], identity=ident_f32[:]
+                        )
+                nc.vector.tensor_copy(
+                    out=x_grouped_words[:, 2 * P * b : 2 * P * (b + 1), :].rearrange("p (t l) u -> p t l u", t=2),
+                    in_=x_ps[:].rearrange("p t u l -> p t l u"),
+                )
+            w_grouped = keep.tile([P, C, PACK], BF16, align_bytes=64)
+            nc.vector.tensor_copy(out=w_grouped[:], in_=w_sb[:].rearrange("p t c -> p c t"))
+            x_codes = keep.tile([P, L], U32, align_bytes=64)
+            x_scales = keep.tile([P, L], U8, align_bytes=64)
+            nc.vector.quantize_mx(out=x_codes[:].bitcast(FP8X4), scales=x_scales[:], in_=x_grouped[:])
+            w_codes = keep.tile([P, C], U32, align_bytes=64)
+            w_scales = keep.tile([P, C], U8, align_bytes=64)
+            nc.vector.quantize_mx(
+                out=w_codes[:].bitcast(FP8X4), scales=w_scales[:], in_=w_grouped[:].rearrange("p c t -> p (c t)")
+            )
+            v_grouped = keep.tile([P, NG, C, PACK], BF16, align_bytes=64)
+            for g in range(NG):
+                for n in range(NH):
+                    v_ps = psum_o.tile([P, PACK, D], F32, tag="acc")
+                    for j in range(PACK):
+                        rows = slice(P * (PACK * g + j), P * (PACK * g + j + 1))
+                        cols = slice(D * n, D * (n + 1))
+                        nc.tensor.matmul_mx(
+                            out=v_ps[:, j, :],
+                            lhsT=x_codes[:, rows].bitcast(FP8X4),
+                            lhsT_scale=x_scales[:, rows],
+                            rhs=w_codes[:, cols].bitcast(FP8X4),
+                            rhs_scale=w_scales[:, cols],
+                            start=True,
+                            stop=True,
+                        )
+                    nc.scalar.copy(
+                        out=v_grouped[:, g, D * n : D * (n + 1), :], in_=v_ps[:].rearrange("p j d -> p d j")
+                    )
+                nc.vector.quantize_mx(
+                    out=v_codes[:, g, :].bitcast(FP8X4),
+                    scales=v_scales[:, g, :],
+                    in_=v_grouped[:, g, :, :].rearrange("p c j -> p (c j)"),
+                )
+
+        def softmax_tile(i):
+            n = i // NT
+            t = i % NT
+            pos = bias.tile([P, L], F32)
+            nc.gpsimd.tensor_tensor(
+                out=pos[:].rearrange("p (a b) -> p a b", b=GRID),
+                in0=col_bias[:, i, :].unsqueeze(1).to_broadcast([P, GRID, GRID]),
+                in1=row_bias[:, i, :].unsqueeze(2).to_broadcast([P, GRID, GRID]),
+                op=ALU.add,
+            )
+            s = work.tile([P, L], F32)
+            for h in range(L // HALF):
+                cols = slice(HALF * h, HALF * (h + 1))
+                s_ps = psum_s.tile([P, HALF], F32)
+                nc.tensor.matmul(
+                    out=s_ps[:], lhsT=qT[:, n, P * t : P * (t + 1)], rhs=kT[:, n, cols], start=True, stop=True
+                )
+                nc.vector.scalar_tensor_tensor(
+                    out=s[:, cols], in0=s_ps[:], scalar=SCALE, in1=pos[:, cols], op0=ALU.mult, op1=ALU.add
+                )
+            neg_max = late.tile([P, 1], F32)
+            nc.vector.tensor_reduce(out=neg_max[:], in_=s[:], axis=AX.X, op=ALU.max, negate=True)
+            e = work.tile([P, L], BF16)
+            row_sum = late.tile([P, 1], F32)
+            nc.scalar.activation(
+                out=e[:], in_=s[:], func=ACT.Exp, bias=neg_max[:, 0:1], scale=1.0, accum_out=row_sum[:, 0:1]
+            )
+            e_ps = psum_t.tile([P, NT, P], BF16, tag="turned")
+            for b in range(NT):
+                nc.tensor.transpose(out=e_ps[:, b, :], in_=e[:, P * b : P * (b + 1)], identity=ident_bf[:])
+            e_grouped = work.tile([P, NG, P, PACK], BF16, align_bytes=64)
+            nc.scalar.copy(out=e_grouped[:], in_=e_ps[:].rearrange("p (g j) m -> p g m j", g=NG))
+            e_codes = late.tile([P, NG, P], U32, align_bytes=64)
+            e_scales = late.tile([P, NG, P], U8, align_bytes=64)
+            nc.vector.quantize_mx(
+                out=e_codes[:].rearrange("p g m -> p (g m)").bitcast(FP8X4),
+                scales=e_scales[:].rearrange("p g m -> p (g m)"),
+                in_=e_grouped[:].rearrange("p g m j -> p (g m j)"),
+            )
+            return e_codes, e_scales, row_sum
+
+        out_rows = out.rearrange("b h w c -> (b h w) c")
+
+        def output_tile(i, e_codes, e_scales, row_sum):
+            n = i // NT
+            t = i % NT
+            o_ps = psum_o.tile([P, D], F32, tag="acc")
+            for g in range(NG):
+                nc.tensor.matmul_mx(
+                    out=o_ps[:],
+                    lhsT=e_codes[:, g, :].bitcast(FP8X4),
+                    lhsT_scale=e_scales[:, g, :],
+                    rhs=v_codes[:, g, D * n : D * (n + 1)].bitcast(FP8X4),
+                    rhs_scale=v_scales[:, g, D * n : D * (n + 1)],
+                    start=(g == 0),
+                    stop=(g == NG - 1),
+                )
+            inv_sum = late.tile([P, 1], F32)
+            nc.vector.reciprocal(out=inv_sum[:], in_=row_sum[:])
+            o_sb = work.tile([P, D], F32)
+            nc.scalar.activation(out=o_sb[:], in_=o_ps[:], func=ACT.Copy, scale=inv_sum[:, 0:1])
+            nc.sync.dma_start(out=out_rows[P * t : P * (t + 1), D * n : D * (n + 1)], in_=o_sb[:])
+
+        turn_head(0)
+        waiting = []
+        for i in range(NH * NT):
+            waiting.append(softmax_tile(i))
+            if i == LAG - 1:
+                project_values()
+            if i >= LAG:
+                output_tile(i - LAG, *waiting[i - LAG])
+            if i % NT == NT // 2 and i // NT + 1 < NH:
+                turn_head(i // NT + 1)
+        for i in range(NH * NT - LAG, NH * NT):
+            output_tile(i, *waiting[i])

@@ -27,16 +27,17 @@ ROWS = P // GRID
 SCALE = 1.0 / (D ** 0.5)
 
 FLOPS = 2 * L * C * C + 2 * 2 * NH * L * L * D
-LAG = 2
+TILES = NH * NT
 
 
 def tile_relativepositionmultiheadattention_pa_kernel(tc, q, k, x, w_v, rel_w, rel_h, out):
     nc = tc.nc
     with ExitStack() as ctx:
+        ctx.enter_context(tc.manual_schedule())
         keep = ctx.enter_context(tc.tile_pool(name="keep", bufs=1))
         bias = ctx.enter_context(tc.tile_pool(name="bias", bufs=4))
         work = ctx.enter_context(tc.tile_pool(name="work", bufs=3))
-        late = ctx.enter_context(tc.tile_pool(name="late", bufs=LAG + 2))
+        late = ctx.enter_context(tc.tile_pool(name="late", bufs=8))
         psum_s = ctx.enter_context(tc.psum_pool(name="psum_s", bufs=4))
         psum_t = ctx.enter_context(tc.psum_pool(name="psum_t", bufs=2))
         psum_o = ctx.enter_context(tc.psum_pool(name="psum_o", bufs=2))
@@ -46,8 +47,8 @@ def tile_relativepositionmultiheadattention_pa_kernel(tc, q, k, x, w_v, rel_w, r
         ident_f32 = keep.tile([P, P], F32)
         make_identity(nc, ident_f32[:])
 
-        col_bias = keep.tile([P, NH * NT, GRID], BF16)
-        row_bias = keep.tile([P, NH * NT, GRID], BF16)
+        col_bias = keep.tile([P, TILES, GRID], BF16)
+        row_bias = keep.tile([P, TILES, GRID], BF16)
         skew = REL - 1
         rw = rel_w.rearrange("b n r c m -> (b n r) (c m)")[:, GRID - 1 : GRID - 1 + skew * GRID]
         rw = rw.rearrange("a (c j) -> a c j", j=skew)[:, :, 0:GRID]
@@ -56,12 +57,14 @@ def tile_relativepositionmultiheadattention_pa_kernel(tc, q, k, x, w_v, rel_w, r
         rh = rh.rearrange("a (r j) -> a r j", j=skew)[:, :, 0:GRID]
         rh = rh.rearrange("(n c) (t rl) j -> n rl c t j", c=GRID, rl=ROWS)
 
-        def load_row_bias(n):
+        def load_bias(queue, n):
+            of_head = slice(NT * n, NT * (n + 1))
             for rl in range(ROWS):
-                nc.sync.dma_start(
-                    out=row_bias[GRID * rl : GRID * (rl + 1), NT * n : NT * (n + 1), :], in_=rh[n, rl]
-                )
+                rows = slice(GRID * rl, GRID * (rl + 1))
+                queue.dma_start(out=col_bias[rows, of_head, :], in_=rw[rl][:, of_head, :])
+                queue.dma_start(out=row_bias[rows, of_head, :], in_=rh[n, rl])
 
+        load_bias(nc.scalar, 0)
         q_rows = q.rearrange("b n (t p) d -> (b n) p t d", p=P)
         k_rows = k.rearrange("b n (t p) d -> (b n) p t d", p=P)
         q_sb = []
@@ -71,9 +74,6 @@ def tile_relativepositionmultiheadattention_pa_kernel(tc, q, k, x, w_v, rel_w, r
             q_sb.append(keep.tile([P, NT, D], BF16, name="q_sb%d" % n))
         nc.sync.dma_start(out=k_sb[0][:], in_=k_rows[0])
         nc.sync.dma_start(out=q_sb[0][:], in_=q_rows[0])
-        for rl in range(ROWS):
-            nc.sync.dma_start(out=col_bias[GRID * rl : GRID * (rl + 1), :, :], in_=rw[rl])
-        load_row_bias(0)
         x_sb = keep.tile([P, NT * C], BF16)
         nc.sync.dma_start(
             out=x_sb[:].rearrange("p (t c) -> p t c", c=C),
@@ -85,7 +85,7 @@ def tile_relativepositionmultiheadattention_pa_kernel(tc, q, k, x, w_v, rel_w, r
             in_=w_v.rearrange("(u p e) c -> p u (e c)", u=2, e=2),
         )
         for n in range(1, NH):
-            load_row_bias(n)
+            load_bias(nc.sync, n)
             nc.sync.dma_start(out=k_sb[n][:], in_=k_rows[n])
             nc.sync.dma_start(out=q_sb[n][:], in_=q_rows[n])
 
@@ -96,16 +96,20 @@ def tile_relativepositionmultiheadattention_pa_kernel(tc, q, k, x, w_v, rel_w, r
             k_ps = psum_t.tile([P, NT, P], BF16, tag="turned")
             for t in range(NT):
                 nc.tensor.transpose(out=k_ps[:, t, :], in_=k_sb[n][:, t, :], identity=ident_bf[:])
-            nc.vector.tensor_copy(out=kT[:, n, :], in_=k_ps[:].rearrange("p t l -> p (t l)"))
-            q_ps = psum_t.tile([P, NT, P], BF16, tag="turned")
+            nc.scalar.copy(out=kT[:, n, :], in_=k_ps[:].rearrange("p t l -> p (t l)"))
+            q_ps = psum_o.tile([P, NT, P], BF16, tag="acc")
             for t in range(NT):
                 nc.tensor.transpose(out=q_ps[:, t, :], in_=q_sb[n][:, t, :], identity=ident_bf[:])
             nc.scalar.copy(out=qT[:, n, :], in_=q_ps[:].rearrange("p t l -> p (t l)"))
 
+        x_codes = keep.tile([P, L], U32, align_bytes=64)
+        x_scales = keep.tile([P, L], U8, align_bytes=64)
+        w_codes = keep.tile([P, C], U32, align_bytes=64)
+        w_scales = keep.tile([P, C], U8, align_bytes=64)
         v_codes = keep.tile([P, NG, C], U32, align_bytes=64)
         v_scales = keep.tile([P, NG, C], U8, align_bytes=64)
 
-        def project_values():
+        def quantise_x_and_w():
             x_words = x_sb[:].bitcast(F32)
             x_grouped = keep.tile([P, L * PACK], BF16, align_bytes=64)
             x_grouped_words = x_grouped[:].bitcast(F32).rearrange("p (l u) -> p l u", u=2)
@@ -117,20 +121,19 @@ def tile_relativepositionmultiheadattention_pa_kernel(tc, q, k, x, w_v, rel_w, r
                         nc.tensor.transpose(
                             out=x_ps[:, tt, u, :], in_=x_words[:, first : first + P], identity=ident_f32[:]
                         )
-                nc.vector.tensor_copy(
-                    out=x_grouped_words[:, 2 * P * b : 2 * P * (b + 1), :].rearrange("p (t l) u -> p t l u", t=2),
-                    in_=x_ps[:].rearrange("p t u l -> p t l u"),
-                )
+                grouped = x_grouped_words[:, 2 * P * b : 2 * P * (b + 1), :].rearrange("p (t l) u -> p t l u", t=2)
+                if b % 2 == 0:
+                    nc.vector.tensor_copy(out=grouped, in_=x_ps[:].rearrange("p t u l -> p t l u"))
+                else:
+                    nc.scalar.copy(out=grouped, in_=x_ps[:].rearrange("p t u l -> p t l u"))
             w_grouped = keep.tile([P, C, PACK], BF16, align_bytes=64)
             nc.vector.tensor_copy(out=w_grouped[:], in_=w_sb[:].rearrange("p t c -> p c t"))
-            x_codes = keep.tile([P, L], U32, align_bytes=64)
-            x_scales = keep.tile([P, L], U8, align_bytes=64)
             nc.vector.quantize_mx(out=x_codes[:].bitcast(FP8X4), scales=x_scales[:], in_=x_grouped[:])
-            w_codes = keep.tile([P, C], U32, align_bytes=64)
-            w_scales = keep.tile([P, C], U8, align_bytes=64)
             nc.vector.quantize_mx(
                 out=w_codes[:].bitcast(FP8X4), scales=w_scales[:], in_=w_grouped[:].rearrange("p c t -> p (c t)")
             )
+
+        def project_values():
             v_grouped = keep.tile([P, NG, C, PACK], BF16, align_bytes=64)
             for g in range(NG):
                 for n in range(NH):
@@ -147,18 +150,21 @@ def tile_relativepositionmultiheadattention_pa_kernel(tc, q, k, x, w_v, rel_w, r
                             start=True,
                             stop=True,
                         )
-                    nc.scalar.copy(
-                        out=v_grouped[:, g, D * n : D * (n + 1), :], in_=v_ps[:].rearrange("p j d -> p d j")
-                    )
+                    grouped = v_grouped[:, g, D * n : D * (n + 1), :]
+                    if n % 2 == 0:
+                        nc.scalar.copy(out=grouped, in_=v_ps[:].rearrange("p j d -> p d j"))
+                    else:
+                        nc.vector.tensor_copy(out=grouped, in_=v_ps[:].rearrange("p j d -> p d j"))
+            for g in range(NG):
                 nc.vector.quantize_mx(
                     out=v_codes[:, g, :].bitcast(FP8X4),
                     scales=v_scales[:, g, :],
                     in_=v_grouped[:, g, :, :].rearrange("p c j -> p (c j)"),
                 )
 
-        def softmax_tile(i):
-            n = i // NT
-            t = i % NT
+        tiles = {}
+
+        def build_pos(i):
             pos = bias.tile([P, L], F32)
             nc.gpsimd.tensor_tensor(
                 out=pos[:].rearrange("p (a b) -> p a b", b=GRID),
@@ -166,68 +172,131 @@ def tile_relativepositionmultiheadattention_pa_kernel(tc, q, k, x, w_v, rel_w, r
                 in1=row_bias[:, i, :].unsqueeze(2).to_broadcast([P, GRID, GRID]),
                 op=ALU.add,
             )
+            tiles["pos", i] = pos
+
+        def scores(i):
+            n = i // NT
+            t = i % NT
+            for h in range(L // HALF):
+                s_ps = psum_s.tile([P, HALF], F32)
+                nc.tensor.matmul(
+                    out=s_ps[:],
+                    lhsT=qT[:, n, P * t : P * (t + 1)],
+                    rhs=kT[:, n, HALF * h : HALF * (h + 1)],
+                    start=True,
+                    stop=True,
+                )
+                tiles["s_ps", i, h] = s_ps
+
+        def add_bias(i):
             s = work.tile([P, L], F32)
             for h in range(L // HALF):
                 cols = slice(HALF * h, HALF * (h + 1))
-                s_ps = psum_s.tile([P, HALF], F32)
-                nc.tensor.matmul(
-                    out=s_ps[:], lhsT=qT[:, n, P * t : P * (t + 1)], rhs=kT[:, n, cols], start=True, stop=True
-                )
                 nc.vector.scalar_tensor_tensor(
-                    out=s[:, cols], in0=s_ps[:], scalar=SCALE, in1=pos[:, cols], op0=ALU.mult, op1=ALU.add
+                    out=s[:, cols],
+                    in0=tiles["s_ps", i, h][:],
+                    scalar=SCALE,
+                    in1=tiles["pos", i][:, cols],
+                    op0=ALU.mult,
+                    op1=ALU.add,
                 )
+            tiles["s", i] = s
+
+        def row_max(i):
             neg_max = late.tile([P, 1], F32)
-            nc.vector.tensor_reduce(out=neg_max[:], in_=s[:], axis=AX.X, op=ALU.max, negate=True)
+            nc.vector.tensor_reduce(out=neg_max[:], in_=tiles["s", i][:], axis=AX.X, op=ALU.max, negate=True)
+            tiles["neg_max", i] = neg_max
+
+        def exponent(i):
             e = work.tile([P, L], BF16)
             row_sum = late.tile([P, 1], F32)
             nc.scalar.activation(
-                out=e[:], in_=s[:], func=ACT.Exp, bias=neg_max[:, 0:1], scale=1.0, accum_out=row_sum[:, 0:1]
+                out=e[:],
+                in_=tiles["s", i][:],
+                func=ACT.Exp,
+                bias=tiles["neg_max", i][:, 0:1],
+                scale=1.0,
+                accum_out=row_sum[:, 0:1],
             )
+            tiles["e", i] = e
+            tiles["row_sum", i] = row_sum
+
+        def turn_e(i):
             e_ps = psum_t.tile([P, NT, P], BF16, tag="turned")
             for b in range(NT):
-                nc.tensor.transpose(out=e_ps[:, b, :], in_=e[:, P * b : P * (b + 1)], identity=ident_bf[:])
+                nc.tensor.transpose(
+                    out=e_ps[:, b, :], in_=tiles["e", i][:, P * b : P * (b + 1)], identity=ident_bf[:]
+                )
+            tiles["e_ps", i] = e_ps
+
+        def group_e(i):
             e_grouped = work.tile([P, NG, P, PACK], BF16, align_bytes=64)
-            nc.scalar.copy(out=e_grouped[:], in_=e_ps[:].rearrange("p (g j) m -> p g m j", g=NG))
+            nc.scalar.copy(out=e_grouped[:], in_=tiles["e_ps", i][:].rearrange("p (g j) m -> p g m j", g=NG))
+            tiles["e_grouped", i] = e_grouped
+
+        def quantise_e(i):
             e_codes = late.tile([P, NG, P], U32, align_bytes=64)
             e_scales = late.tile([P, NG, P], U8, align_bytes=64)
             nc.vector.quantize_mx(
                 out=e_codes[:].rearrange("p g m -> p (g m)").bitcast(FP8X4),
                 scales=e_scales[:].rearrange("p g m -> p (g m)"),
-                in_=e_grouped[:].rearrange("p g m j -> p (g m j)"),
+                in_=tiles["e_grouped", i][:].rearrange("p g m j -> p (g m j)"),
             )
-            return e_codes, e_scales, row_sum
+            tiles["e_codes", i] = e_codes
+            tiles["e_scales", i] = e_scales
 
-        out_rows = out.rearrange("b h w c -> (b h w) c")
-
-        def output_tile(i, e_codes, e_scales, row_sum):
+        def weigh_values(i):
             n = i // NT
-            t = i % NT
             o_ps = psum_o.tile([P, D], F32, tag="acc")
             for g in range(NG):
                 nc.tensor.matmul_mx(
                     out=o_ps[:],
-                    lhsT=e_codes[:, g, :].bitcast(FP8X4),
-                    lhsT_scale=e_scales[:, g, :],
+                    lhsT=tiles["e_codes", i][:, g, :].bitcast(FP8X4),
+                    lhsT_scale=tiles["e_scales", i][:, g, :],
                     rhs=v_codes[:, g, D * n : D * (n + 1)].bitcast(FP8X4),
                     rhs_scale=v_scales[:, g, D * n : D * (n + 1)],
                     start=(g == 0),
                     stop=(g == NG - 1),
                 )
+            tiles["o_ps", i] = o_ps
+
+        def invert_sum(i):
             inv_sum = late.tile([P, 1], F32)
-            nc.vector.reciprocal(out=inv_sum[:], in_=row_sum[:])
+            nc.vector.reciprocal(out=inv_sum[:], in_=tiles["row_sum", i][:])
+            tiles["inv_sum", i] = inv_sum
+
+        out_rows = out.rearrange("b h w c -> (b h w) c")
+
+        def normalise_and_store(i):
+            n = i // NT
+            t = i % NT
             o_sb = work.tile([P, D], F32)
-            nc.scalar.activation(out=o_sb[:], in_=o_ps[:], func=ACT.Copy, scale=inv_sum[:, 0:1])
+            nc.scalar.activation(
+                out=o_sb[:], in_=tiles["o_ps", i][:], func=ACT.Copy, scale=tiles["inv_sum", i][:, 0:1]
+            )
             nc.sync.dma_start(out=out_rows[P * t : P * (t + 1), D * n : D * (n + 1)], in_=o_sb[:])
 
+        def if_tile(stage, i):
+            if 0 <= i < TILES:
+                stage(i)
+
         turn_head(0)
-        waiting = []
-        for i in range(NH * NT):
-            waiting.append(softmax_tile(i))
-            if i == LAG - 1:
+        build_pos(0)
+        for c in range(-1, TILES + 7):
+            if_tile(build_pos, c + 2)
+            if_tile(scores, c + 1)
+            if_tile(turn_e, c - 2)
+            if_tile(weigh_values, c - 5)
+            if_tile(row_max, c - 1)
+            if_tile(add_bias, c)
+            if_tile(quantise_e, c - 4)
+            if_tile(invert_sum, c - 5)
+            if_tile(group_e, c - 3)
+            if_tile(normalise_and_store, c - 6)
+            if_tile(exponent, c - 1)
+            if c == 1:
+                quantise_x_and_w()
+            if c == 2:
                 project_values()
-            if i >= LAG:
-                output_tile(i - LAG, *waiting[i - LAG])
-            if i % NT == NT // 2 and i // NT + 1 < NH:
-                turn_head(i // NT + 1)
-        for i in range(NH * NT - LAG, NH * NT):
-            output_tile(i, *waiting[i])
+            if c % NT == 3 and c // NT + 1 < NH:
+                turn_head(c // NT + 1)

@@ -25,9 +25,14 @@ HALF = 512
 REL = 2 * GRID - 1
 ROWS = P // GRID
 SCALE = 1.0 / (D ** 0.5)
+ROOT = D ** 0.5
 
 FLOPS = 2 * L * C * C + 2 * 2 * NH * L * L * D
 TILES = NH * NT
+COLS = P // (HALF // GRID)
+VECTOR, MATMUL, TURN = range(3)
+KINDS = [VECTOR] * 4 + [MATMUL] + [TURN] * 3
+ORDER = [t for t in (0, 1, 4, 2, 5, 3, 6, 7)] + [NT * n + t for n in range(1, NH) for t in (0, 4, 1, 5, 2, 6, 3, 7)]
 
 
 def tile_relativepositionmultiheadattention_pa_kernel(tc, q, k, x, w_v, rel_w, rel_h, out):
@@ -36,19 +41,31 @@ def tile_relativepositionmultiheadattention_pa_kernel(tc, q, k, x, w_v, rel_w, r
         ctx.enter_context(tc.manual_schedule())
         keep = ctx.enter_context(tc.tile_pool(name="keep", bufs=1))
         bias = ctx.enter_context(tc.tile_pool(name="bias", bufs=4))
-        work = ctx.enter_context(tc.tile_pool(name="work", bufs=3))
+        work = ctx.enter_context(tc.tile_pool(name="work", bufs=4))
         late = ctx.enter_context(tc.tile_pool(name="late", bufs=8))
         psum_s = ctx.enter_context(tc.psum_pool(name="psum_s", bufs=4))
-        psum_t = ctx.enter_context(tc.psum_pool(name="psum_t", bufs=2))
-        psum_o = ctx.enter_context(tc.psum_pool(name="psum_o", bufs=2))
+        psum_t = ctx.enter_context(tc.psum_pool(name="psum_t", bufs=4))
+        psum_o = psum_t
 
         ident_bf = keep.tile([P, P], BF16)
         make_identity(nc, ident_bf[:])
         ident_f32 = keep.tile([P, P], F32)
         make_identity(nc, ident_f32[:])
+        wrap = keep.tile([P, 2 * GRID], BF16)
+        nc.gpsimd.tensor_tensor(
+            out=wrap[:], in0=ident_bf[:, 0 : 2 * GRID], in1=ident_bf[:, 2 * GRID : 4 * GRID], op=ALU.add
+        )
+        spread = keep.tile([P, L], BF16)
+        nc.gpsimd.tensor_tensor(
+            out=spread[:].rearrange("p (a b) -> p a b", b=GRID),
+            in0=wrap[:, 0:GRID].unsqueeze(1).to_broadcast([P, GRID, GRID]),
+            in1=wrap[:, GRID : 2 * GRID].unsqueeze(2).to_broadcast([P, GRID, GRID]),
+            op=ALU.add,
+        )
 
-        col_bias = keep.tile([P, TILES, GRID], BF16)
-        row_bias = keep.tile([P, TILES, GRID], BF16)
+        bias_in = keep.tile([P, TILES, 2, GRID], BF16)
+        col_bias = bias_in[:, :, 0, :]
+        row_bias = bias_in[:, :, 1, :]
         skew = REL - 1
         rw = rel_w.rearrange("b n r c m -> (b n r) (c m)")[:, GRID - 1 : GRID - 1 + skew * GRID]
         rw = rw.rearrange("a (c j) -> a c j", j=skew)[:, :, 0:GRID]
@@ -76,8 +93,8 @@ def tile_relativepositionmultiheadattention_pa_kernel(tc, q, k, x, w_v, rel_w, r
         nc.sync.dma_start(out=q_sb[0][:], in_=q_rows[0])
         x_sb = keep.tile([P, NT * C], BF16)
         nc.sync.dma_start(
-            out=x_sb[:].rearrange("p (t c) -> p t c", c=C),
-            in_=x.rearrange("b h w c -> (b h w) c").rearrange("(t p) c -> p t c", p=P),
+            out=x_sb[:].rearrange("p (u k) -> p u k", k=2 * C),
+            in_=x.rearrange("b h w c -> (b h w) c").rearrange("(u p e) c -> p u (e c)", p=P, e=2),
         )
         w_sb = keep.tile([P, PACK, C], BF16)
         nc.sync.dma_start(
@@ -97,7 +114,7 @@ def tile_relativepositionmultiheadattention_pa_kernel(tc, q, k, x, w_v, rel_w, r
             for t in range(NT):
                 nc.tensor.transpose(out=k_ps[:, t, :], in_=k_sb[n][:, t, :], identity=ident_bf[:])
             nc.scalar.copy(out=kT[:, n, :], in_=k_ps[:].rearrange("p t l -> p (t l)"))
-            q_ps = psum_o.tile([P, NT, P], BF16, tag="acc")
+            q_ps = psum_o.tile([P, NT, P], BF16, tag="turned")
             for t in range(NT):
                 nc.tensor.transpose(out=q_ps[:, t, :], in_=q_sb[n][:, t, :], identity=ident_bf[:])
             nc.scalar.copy(out=qT[:, n, :], in_=q_ps[:].rearrange("p t l -> p (t l)"))
@@ -106,63 +123,77 @@ def tile_relativepositionmultiheadattention_pa_kernel(tc, q, k, x, w_v, rel_w, r
         x_scales = keep.tile([P, L], U8, align_bytes=64)
         w_codes = keep.tile([P, C], U32, align_bytes=64)
         w_scales = keep.tile([P, C], U8, align_bytes=64)
-        v_codes = keep.tile([P, NG, C], U32, align_bytes=64)
-        v_scales = keep.tile([P, NG, C], U8, align_bytes=64)
+        v_codes = keep.tile([P, NH, NG, D], U32, align_bytes=64)
+        v_scales = keep.tile([P, NH, NG, D], U8, align_bytes=64)
+        x_grouped = keep.tile([P, L * PACK], BF16, align_bytes=64)
+        w_grouped = keep.tile([P, C, PACK], BF16, align_bytes=64)
 
-        def quantise_x_and_w():
+        def turn_x(b):
             x_words = x_sb[:].bitcast(F32)
-            x_grouped = keep.tile([P, L * PACK], BF16, align_bytes=64)
             x_grouped_words = x_grouped[:].bitcast(F32).rearrange("p (l u) -> p l u", u=2)
-            for b in range(NT // 2):
-                x_ps = psum_o.tile([P, 2, 2, P], F32, tag="acc")
-                for tt in range(2):
-                    for u in range(2):
-                        first = (C // 2) * (2 * b + tt) + P * u
-                        nc.tensor.transpose(
-                            out=x_ps[:, tt, u, :], in_=x_words[:, first : first + P], identity=ident_f32[:]
-                        )
-                grouped = x_grouped_words[:, 2 * P * b : 2 * P * (b + 1), :].rearrange("p (t l) u -> p t l u", t=2)
-                if b % 2 == 0:
-                    nc.vector.tensor_copy(out=grouped, in_=x_ps[:].rearrange("p t u l -> p t l u"))
-                else:
-                    nc.scalar.copy(out=grouped, in_=x_ps[:].rearrange("p t u l -> p t l u"))
-            w_grouped = keep.tile([P, C, PACK], BF16, align_bytes=64)
+            x_ps = psum_o.tile([P, 2, 2, P], F32, tag="turned")
+            for tt in range(2):
+                for u in range(2):
+                    first = (C // 2) * (2 * b + tt) + P * u
+                    nc.tensor.transpose(
+                        out=x_ps[:, tt, u, :], in_=x_words[:, first : first + P], identity=ident_f32[:]
+                    )
+            grouped = x_grouped_words[:, 2 * P * b : 2 * P * (b + 1), :].rearrange("p (t l) u -> p t l u", t=2)
+            if b % 2 == 0:
+                nc.vector.tensor_copy(out=grouped, in_=x_ps[:].rearrange("p t u l -> p t l u"))
+            else:
+                nc.scalar.copy(out=grouped, in_=x_ps[:].rearrange("p t u l -> p t l u"))
+
+        def group_w():
             nc.vector.tensor_copy(out=w_grouped[:], in_=w_sb[:].rearrange("p t c -> p c t"))
-            nc.vector.quantize_mx(out=x_codes[:].bitcast(FP8X4), scales=x_scales[:], in_=x_grouped[:])
+
+        def quantise_x(half):
+            cols = slice(HALF * half, HALF * (half + 1))
+            nc.vector.quantize_mx(
+                out=x_codes[:, cols].bitcast(FP8X4),
+                scales=x_scales[:, cols],
+                in_=x_grouped[:, PACK * HALF * half : PACK * HALF * (half + 1)],
+            )
+
+        def quantise_w():
             nc.vector.quantize_mx(
                 out=w_codes[:].bitcast(FP8X4), scales=w_scales[:], in_=w_grouped[:].rearrange("p c t -> p (c t)")
             )
 
-        def project_values():
-            v_grouped = keep.tile([P, NG, C, PACK], BF16, align_bytes=64)
+        v_grouped = keep.tile([P, NH, NG, D, PACK], BF16, align_bytes=64)
+
+        def project_values(n):
             for g in range(NG):
-                for n in range(NH):
-                    v_ps = psum_o.tile([P, PACK, D], F32, tag="acc")
-                    for j in range(PACK):
-                        rows = slice(P * (PACK * g + j), P * (PACK * g + j + 1))
-                        cols = slice(D * n, D * (n + 1))
-                        nc.tensor.matmul_mx(
-                            out=v_ps[:, j, :],
-                            lhsT=x_codes[:, rows].bitcast(FP8X4),
-                            lhsT_scale=x_scales[:, rows],
-                            rhs=w_codes[:, cols].bitcast(FP8X4),
-                            rhs_scale=w_scales[:, cols],
-                            start=True,
-                            stop=True,
-                        )
-                    grouped = v_grouped[:, g, D * n : D * (n + 1), :]
-                    if n % 2 == 0:
-                        nc.scalar.copy(out=grouped, in_=v_ps[:].rearrange("p j d -> p d j"))
-                    else:
-                        nc.vector.tensor_copy(out=grouped, in_=v_ps[:].rearrange("p j d -> p d j"))
-            for g in range(NG):
-                nc.vector.quantize_mx(
-                    out=v_codes[:, g, :].bitcast(FP8X4),
-                    scales=v_scales[:, g, :],
-                    in_=v_grouped[:, g, :, :].rearrange("p c j -> p (c j)"),
-                )
+                v_ps = psum_o.tile([P, PACK, D], F32, tag="turned")
+                for j in range(PACK):
+                    rows = slice(P * (PACK * g + j), P * (PACK * g + j + 1))
+                    cols = slice(D * n, D * (n + 1))
+                    nc.tensor.matmul_mx(
+                        out=v_ps[:, j, :],
+                        lhsT=x_codes[:, rows].bitcast(FP8X4),
+                        lhsT_scale=x_scales[:, rows],
+                        rhs=w_codes[:, cols].bitcast(FP8X4),
+                        rhs_scale=w_scales[:, cols],
+                        start=True,
+                        stop=True,
+                    )
+                grouped = v_grouped[:, n, g, :, :]
+                if g == 0:
+                    nc.scalar.copy(out=grouped, in_=v_ps[:].rearrange("p j d -> p d j"))
+                else:
+                    nc.vector.tensor_copy(out=grouped, in_=v_ps[:].rearrange("p j d -> p d j"))
+
+        def quantise_v(n):
+            nc.vector.quantize_mx(
+                out=v_codes[:, n, :, :].rearrange("p g d -> p (g d)").bitcast(FP8X4),
+                scales=v_scales[:, n, :, :].rearrange("p g d -> p (g d)"),
+                in_=v_grouped[:, n, :, :, :].rearrange("p g d j -> p (g d j)"),
+            )
 
         tiles = {}
+
+        def kind(i):
+            return KINDS[i % NT]
 
         def build_pos(i):
             pos = bias.tile([P, L], F32)
@@ -174,6 +205,60 @@ def tile_relativepositionmultiheadattention_pa_kernel(tc, q, k, x, w_v, rel_w, r
             )
             tiles["pos", i] = pos
 
+        def gather_bias(i):
+            if kind(i) == VECTOR:
+                build_pos(i)
+            elif kind(i) == MATMUL:
+                halves = bias.tile([P, 2, 2 * GRID], BF16)
+                rel = bias_in[:, i, :, :].rearrange("p k j -> p (k j)")
+                nc.gpsimd.tensor_scalar(out=halves[:, 0, :], in0=rel, scalar1=ROOT, scalar2=0.0, op0=ALU.mult, op1=ALU.add)
+                tiles["halves", i] = halves
+            else:
+                flat = bias.tile([P, 3, P], BF16)
+                nc.gpsimd.tensor_scalar(
+                    out=flat[:, 0, :].rearrange("p (a b) -> p a b", b=GRID),
+                    in0=col_bias[:, i, :].unsqueeze(1).to_broadcast([P, ROWS, GRID]),
+                    scalar1=1.0, scalar2=0.0, op0=ALU.mult, op1=ALU.add,
+                )
+                nc.gpsimd.tensor_scalar(
+                    out=flat[:, 1:3, :].rearrange("p h (a b) -> p (h a) b", b=COLS),
+                    in0=row_bias[:, i, :].unsqueeze(2).to_broadcast([P, GRID, COLS]),
+                    scalar1=1.0, scalar2=0.0, op0=ALU.mult, op1=ALU.add,
+                )
+                tiles["flat", i] = flat[:].rearrange("p k j -> p (k j)")
+
+        def low_half(i):
+            if kind(i) == MATMUL:
+                halves = tiles["halves", i]
+                rel = bias_in[:, i, :, :].rearrange("p k j -> p (k j)")
+                nc.vector.scalar_tensor_tensor(
+                    out=halves[:, 1, :], in0=rel, scalar=ROOT, in1=halves[:, 0, :], op0=ALU.mult, op1=ALU.subtract
+                )
+                tiles["flat", i] = halves[:].rearrange("p k j -> p (k j)")
+
+        def turn_bias(i):
+            if kind(i) == VECTOR:
+                return
+            flat = tiles["flat", i]
+            pieces = 1 if kind(i) == MATMUL else 3
+            b_ps = psum_t.tile([P, pieces, P], BF16, tag="turned")
+            for b in range(pieces):
+                nc.tensor.transpose(out=b_ps[:, b, :], in_=flat[:, P * b : P * (b + 1)], identity=ident_bf[:])
+            tiles["b_ps", i] = b_ps
+
+        def take_bias(i):
+            if kind(i) == VECTOR:
+                return
+            b_ps = tiles["b_ps", i]
+            if kind(i) == MATMUL:
+                turned = bias.tile([P, P], BF16)
+                nc.scalar.copy(out=turned[:], in_=b_ps[:, 0, :])
+                tiles["turned", i] = turned
+            else:
+                turned = bias.tile([P, 3, P], F32)
+                nc.scalar.activation(out=turned[:], in_=b_ps[:], func=ACT.Copy, scale=ROOT)
+                tiles["turned", i] = turned
+
         def scores(i):
             n = i // NT
             t = i % NT
@@ -184,11 +269,42 @@ def tile_relativepositionmultiheadattention_pa_kernel(tc, q, k, x, w_v, rel_w, r
                     lhsT=qT[:, n, P * t : P * (t + 1)],
                     rhs=kT[:, n, HALF * h : HALF * (h + 1)],
                     start=True,
-                    stop=True,
+                    stop=kind(i) == VECTOR,
                 )
+                if kind(i) == MATMUL:
+                    nc.tensor.matmul(
+                        out=s_ps[:],
+                        lhsT=tiles["turned", i][:],
+                        rhs=spread[:, HALF * h : HALF * (h + 1)],
+                        start=False,
+                        stop=True,
+                    )
+                if kind(i) == TURN:
+                    turned = tiles["turned", i]
+                    for b in range(HALF // P):
+                        nc.tensor.matmul(
+                            out=s_ps[:, P * b : P * (b + 1)],
+                            lhsT=turned[:, 0, :],
+                            rhs=ident_f32[:],
+                            start=False,
+                            stop=False,
+                            is_transpose=True,
+                        )
+                    by_cols = s_ps[:].rearrange("p (a b c) -> p b a c", b=HALF // P, c=COLS)
+                    for b in range(HALF // P):
+                        nc.tensor.matmul(
+                            out=by_cols[:, b, :, :],
+                            lhsT=turned[:, 1 + h, :],
+                            rhs=ident_f32[:],
+                            start=False,
+                            stop=b == HALF // P - 1,
+                            is_transpose=True,
+                        )
                 tiles["s_ps", i, h] = s_ps
 
         def add_bias(i):
+            if kind(i) != VECTOR:
+                return
             s = work.tile([P, L], F32)
             for h in range(L // HALF):
                 cols = slice(HALF * h, HALF * (h + 1))
@@ -203,35 +319,80 @@ def tile_relativepositionmultiheadattention_pa_kernel(tc, q, k, x, w_v, rel_w, r
             tiles["s", i] = s
 
         def row_max(i):
-            neg_max = late.tile([P, 1], F32)
-            nc.vector.tensor_reduce(out=neg_max[:], in_=tiles["s", i][:], axis=AX.X, op=ALU.max, negate=True)
-            tiles["neg_max", i] = neg_max
+            if kind(i) == VECTOR:
+                neg_max = late.tile([P, 1], F32)
+                nc.vector.tensor_reduce(out=neg_max[:], in_=tiles["s", i][:], axis=AX.X, op=ALU.max, negate=True)
+                tiles["neg_max", i] = neg_max
+            else:
+                neg_maxes = late.tile([P, 2], F32)
+                for h in range(L // HALF):
+                    nc.vector.tensor_reduce(
+                        out=neg_maxes[:, h : h + 1], in_=tiles["s_ps", i, h][:], axis=AX.X, op=ALU.max, negate=True
+                    )
+                tiles["neg_maxes", i] = neg_maxes
+
+        def join_max(i):
+            if kind(i) != VECTOR:
+                neg_max = late.tile([P, 1], F32)
+                neg_maxes = tiles["neg_maxes", i]
+                nc.vector.tensor_scalar(
+                    out=neg_max[:],
+                    in0=neg_maxes[:, 0:1],
+                    scalar1=neg_maxes[:, 1:2],
+                    scalar2=SCALE,
+                    op0=ALU.min,
+                    op1=ALU.mult,
+                )
+                tiles["neg_max", i] = neg_max
 
         def exponent(i):
             e = work.tile([P, L], BF16)
-            row_sum = late.tile([P, 1], F32)
-            nc.scalar.activation(
-                out=e[:],
-                in_=tiles["s", i][:],
-                func=ACT.Exp,
-                bias=tiles["neg_max", i][:, 0:1],
-                scale=1.0,
-                accum_out=row_sum[:, 0:1],
-            )
+            row_sum = late.tile([P, 2], F32)
+            if kind(i) == VECTOR:
+                nc.scalar.activation(
+                    out=e[:],
+                    in_=tiles["s", i][:],
+                    func=ACT.Exp,
+                    bias=tiles["neg_max", i][:, 0:1],
+                    scale=1.0,
+                    accum_out=row_sum[:, 0:1],
+                )
+            else:
+                for h in range(L // HALF):
+                    nc.scalar.activation(
+                        out=e[:, HALF * h : HALF * (h + 1)],
+                        in_=tiles["s_ps", i, h][:],
+                        func=ACT.Exp,
+                        bias=tiles["neg_max", i][:, 0:1],
+                        scale=SCALE,
+                        accum_out=row_sum[:, h : h + 1],
+                    )
             tiles["e", i] = e
             tiles["row_sum", i] = row_sum
 
+        def join_sum(i):
+            if kind(i) != VECTOR:
+                row_sum = tiles["row_sum", i]
+                whole = late.tile([P, 1], F32)
+                nc.gpsimd.tensor_tensor(out=whole[:], in0=row_sum[:, 0:1], in1=row_sum[:, 1:2], op=ALU.add)
+                tiles["row_sum", i] = whole
+
         def turn_e(i):
-            e_ps = psum_t.tile([P, NT, P], BF16, tag="turned")
-            for b in range(NT):
+            e_ps = psum_t.tile([P, NT // 2, P], F32, tag="turned")
+            e_words = tiles["e", i][:].bitcast(F32)
+            for b in range(NT // 2):
                 nc.tensor.transpose(
-                    out=e_ps[:, b, :], in_=tiles["e", i][:, P * b : P * (b + 1)], identity=ident_bf[:]
+                    out=e_ps[:, b, :], in_=e_words[:, P * b : P * (b + 1)], identity=ident_f32[:]
                 )
             tiles["e_ps", i] = e_ps
 
         def group_e(i):
             e_grouped = work.tile([P, NG, P, PACK], BF16, align_bytes=64)
-            nc.scalar.copy(out=e_grouped[:], in_=tiles["e_ps", i][:].rearrange("p (g j) m -> p g m j", g=NG))
+            grouped_words = e_grouped[:].rearrange("p g m j -> p (g m j)").bitcast(F32)
+            nc.scalar.copy(
+                out=grouped_words.rearrange("p (g m u) -> p g m u", g=NG, u=2),
+                in_=tiles["e_ps", i][:].rearrange("p (g u) m -> p g m u", g=NG),
+            )
             tiles["e_grouped", i] = e_grouped
 
         def quantise_e(i):
@@ -247,14 +408,14 @@ def tile_relativepositionmultiheadattention_pa_kernel(tc, q, k, x, w_v, rel_w, r
 
         def weigh_values(i):
             n = i // NT
-            o_ps = psum_o.tile([P, D], F32, tag="acc")
+            o_ps = psum_o.tile([P, D], F32, tag="turned")
             for g in range(NG):
                 nc.tensor.matmul_mx(
                     out=o_ps[:],
                     lhsT=tiles["e_codes", i][:, g, :].bitcast(FP8X4),
                     lhsT_scale=tiles["e_scales", i][:, g, :],
-                    rhs=v_codes[:, g, D * n : D * (n + 1)].bitcast(FP8X4),
-                    rhs_scale=v_scales[:, g, D * n : D * (n + 1)],
+                    rhs=v_codes[:, n, g, :].bitcast(FP8X4),
+                    rhs_scale=v_scales[:, n, g, :],
                     start=(g == 0),
                     stop=(g == NG - 1),
                 )
@@ -262,7 +423,7 @@ def tile_relativepositionmultiheadattention_pa_kernel(tc, q, k, x, w_v, rel_w, r
 
         def invert_sum(i):
             inv_sum = late.tile([P, 1], F32)
-            nc.vector.reciprocal(out=inv_sum[:], in_=tiles["row_sum", i][:])
+            nc.vector.reciprocal(out=inv_sum[:], in_=tiles["row_sum", i][:, 0:1])
             tiles["inv_sum", i] = inv_sum
 
         out_rows = out.rearrange("b h w c -> (b h w) c")
@@ -276,27 +437,50 @@ def tile_relativepositionmultiheadattention_pa_kernel(tc, q, k, x, w_v, rel_w, r
             )
             nc.sync.dma_start(out=out_rows[P * t : P * (t + 1), D * n : D * (n + 1)], in_=o_sb[:])
 
-        def if_tile(stage, i):
-            if 0 <= i < TILES:
-                stage(i)
+        def if_tile(stage, j):
+            if 0 <= j < TILES:
+                stage(ORDER[j])
 
         turn_head(0)
-        build_pos(0)
-        for c in range(-1, TILES + 7):
-            if_tile(build_pos, c + 2)
+        for j in range(4):
+            gather_bias(ORDER[j])
+        for c in range(-1, TILES + 8):
+            if c + 4 >= 4:
+                if_tile(gather_bias, c + 4)
+            if_tile(join_sum, c - 3)
+            if_tile(turn_bias, c + 2)
             if_tile(scores, c + 1)
+            if_tile(weigh_values, c - 6)
             if_tile(turn_e, c - 2)
-            if_tile(weigh_values, c - 5)
             if_tile(row_max, c - 1)
-            if_tile(add_bias, c)
             if_tile(quantise_e, c - 4)
-            if_tile(invert_sum, c - 5)
-            if_tile(group_e, c - 3)
-            if_tile(normalise_and_store, c - 6)
+            if_tile(join_max, c - 1)
+            if_tile(add_bias, c + 0)
+            if_tile(invert_sum, c - 6)
+            if_tile(low_half, c + 3)
+            if_tile(take_bias, c + 2)
             if_tile(exponent, c - 1)
+            if_tile(normalise_and_store, c - 6)
+            if_tile(group_e, c - 2)
+            if c == 0:
+                turn_x(0)
+                turn_x(1)
+                group_w()
             if c == 1:
-                quantise_x_and_w()
+                turn_x(2)
+                turn_x(3)
             if c == 2:
-                project_values()
+                quantise_w()
+                quantise_x(0)
+            if c == 3:
+                quantise_x(1)
+            if c == 4:
+                project_values(0)
+            if c == 5:
+                quantise_v(0)
+            if c % NT == 0 and 1 <= c // NT < NH and c > 5:
+                project_values(c // NT)
+            if c % NT == 1 and 1 <= c // NT < NH and c > 5:
+                quantise_v(c // NT)
             if c % NT == 3 and c // NT + 1 < NH:
                 turn_head(c // NT + 1)

@@ -32,7 +32,7 @@ TILES = NH * NT
 COLS = P // (HALF // GRID)
 VECTOR, MATMUL, TURN = range(3)
 KINDS = [VECTOR] * 4 + [MATMUL] + [TURN] * 3
-ORDER = [t for t in (0, 1, 4, 2, 5, 3, 6, 7)] + [NT * n + t for n in range(1, NH) for t in (0, 4, 1, 5, 2, 6, 3, 7)]
+PAIRS = TILES // 2
 
 
 def tile_relativepositionmultiheadattention_pa_kernel(tc, q, k, x, w_v, rel_w, rel_h, out):
@@ -43,8 +43,8 @@ def tile_relativepositionmultiheadattention_pa_kernel(tc, q, k, x, w_v, rel_w, r
         bias = ctx.enter_context(tc.tile_pool(name="bias", bufs=4))
         work = ctx.enter_context(tc.tile_pool(name="work", bufs=4))
         late = ctx.enter_context(tc.tile_pool(name="late", bufs=8))
-        psum_s = ctx.enter_context(tc.psum_pool(name="psum_s", bufs=4))
-        psum_t = ctx.enter_context(tc.psum_pool(name="psum_t", bufs=4))
+        psum_s = ctx.enter_context(tc.psum_pool(name="psum_s", bufs=2))
+        psum_t = ctx.enter_context(tc.psum_pool(name="psum_t", bufs=2))
         psum_o = psum_t
 
         ident_bf = keep.tile([P, P], BF16)
@@ -62,6 +62,9 @@ def tile_relativepositionmultiheadattention_pa_kernel(tc, q, k, x, w_v, rel_w, r
             in1=wrap[:, GRID : 2 * GRID].unsqueeze(2).to_broadcast([P, GRID, GRID]),
             op=ALU.add,
         )
+
+        row_sums = keep.tile([P, TILES, 2], F32)
+        nc.gpsimd.memset(row_sums[:], 0.0)
 
         bias_in = keep.tile([P, TILES, 2, GRID], BF16)
         col_bias = bias_in[:, :, 0, :]
@@ -89,18 +92,18 @@ def tile_relativepositionmultiheadattention_pa_kernel(tc, q, k, x, w_v, rel_w, r
         for n in range(NH):
             k_sb.append(keep.tile([P, NT, D], BF16, name="k_sb%d" % n))
             q_sb.append(keep.tile([P, NT, D], BF16, name="q_sb%d" % n))
-        nc.sync.dma_start(out=k_sb[0][:], in_=k_rows[0])
-        nc.sync.dma_start(out=q_sb[0][:], in_=q_rows[0])
-        x_sb = keep.tile([P, NT * C], BF16)
-        nc.sync.dma_start(
-            out=x_sb[:].rearrange("p (u k) -> p u k", k=2 * C),
-            in_=x.rearrange("b h w c -> (b h w) c").rearrange("(u p e) c -> p u (e c)", p=P, e=2),
-        )
         w_sb = keep.tile([P, PACK, C], BF16)
+        x_sb = keep.tile([P, NT * C], BF16)
+        x_in = x_sb[:].rearrange("p (u k) -> p u k", k=2 * C)
+        x_rows = x.rearrange("b h w c -> (b h w) c").rearrange("(u p e) c -> p u (e c)", p=P, e=2)
+        nc.sync.dma_start(out=k_sb[0][:], in_=k_rows[0])
         nc.sync.dma_start(
             out=w_sb[:].rearrange("p (u e) c -> p u (e c)", e=2),
             in_=w_v.rearrange("(u p e) c -> p u (e c)", u=2, e=2),
         )
+        nc.sync.dma_start(out=q_sb[0][:], in_=q_rows[0])
+        for half in range(2):
+            nc.sync.dma_start(out=x_in[:, 2 * half : 2 * half + 2, :], in_=x_rows[:, 2 * half : 2 * half + 2, :])
         for n in range(1, NH):
             load_bias(nc.sync, n)
             nc.sync.dma_start(out=k_sb[n][:], in_=k_rows[n])
@@ -109,22 +112,23 @@ def tile_relativepositionmultiheadattention_pa_kernel(tc, q, k, x, w_v, rel_w, r
         qT = keep.tile([P, NH, L], BF16)
         kT = keep.tile([P, NH, L], BF16)
 
-        def turn_head(n):
-            k_ps = psum_t.tile([P, NT, P], BF16, tag="turned")
+        def turn_rows(n, rows_sb):
+            r_ps = psum_t.tile([P, NT, P], BF16, tag="turned")
             for t in range(NT):
-                nc.tensor.transpose(out=k_ps[:, t, :], in_=k_sb[n][:, t, :], identity=ident_bf[:])
-            nc.scalar.copy(out=kT[:, n, :], in_=k_ps[:].rearrange("p t l -> p (t l)"))
-            q_ps = psum_o.tile([P, NT, P], BF16, tag="turned")
-            for t in range(NT):
-                nc.tensor.transpose(out=q_ps[:, t, :], in_=q_sb[n][:, t, :], identity=ident_bf[:])
-            nc.scalar.copy(out=qT[:, n, :], in_=q_ps[:].rearrange("p t l -> p (t l)"))
+                nc.tensor.transpose(out=r_ps[:, t, :], in_=rows_sb[n][:, t, :], identity=ident_bf[:])
+            tiles["r_ps"] = r_ps
+
+        def take_rows(n, turned):
+            nc.scalar.copy(out=turned[:, n, :], in_=tiles["r_ps"][:].rearrange("p t l -> p (t l)"))
+
+        tiles = {}
 
         x_codes = keep.tile([P, L], U32, align_bytes=64)
         x_scales = keep.tile([P, L], U8, align_bytes=64)
         w_codes = keep.tile([P, C], U32, align_bytes=64)
         w_scales = keep.tile([P, C], U8, align_bytes=64)
-        v_codes = keep.tile([P, NH, NG, D], U32, align_bytes=64)
-        v_scales = keep.tile([P, NH, NG, D], U8, align_bytes=64)
+        v_codes = keep.tile([P, NG, NH, D], U32, align_bytes=64)
+        v_scales = keep.tile([P, NG, NH, D], U8, align_bytes=64)
         x_grouped = keep.tile([P, L * PACK], BF16, align_bytes=64)
         w_grouped = keep.tile([P, C, PACK], BF16, align_bytes=64)
 
@@ -162,35 +166,34 @@ def tile_relativepositionmultiheadattention_pa_kernel(tc, q, k, x, w_v, rel_w, r
 
         v_grouped = keep.tile([P, NH, NG, D, PACK], BF16, align_bytes=64)
 
-        def project_values(n):
-            for g in range(NG):
-                v_ps = psum_o.tile([P, PACK, D], F32, tag="turned")
-                for j in range(PACK):
-                    rows = slice(P * (PACK * g + j), P * (PACK * g + j + 1))
-                    cols = slice(D * n, D * (n + 1))
-                    nc.tensor.matmul_mx(
-                        out=v_ps[:, j, :],
-                        lhsT=x_codes[:, rows].bitcast(FP8X4),
-                        lhsT_scale=x_scales[:, rows],
-                        rhs=w_codes[:, cols].bitcast(FP8X4),
-                        rhs_scale=w_scales[:, cols],
-                        start=True,
-                        stop=True,
-                    )
-                grouped = v_grouped[:, n, g, :, :]
-                if g == 0:
-                    nc.scalar.copy(out=grouped, in_=v_ps[:].rearrange("p j d -> p d j"))
-                else:
-                    nc.vector.tensor_copy(out=grouped, in_=v_ps[:].rearrange("p j d -> p d j"))
+        def project_values(n, g):
+            v_ps = psum_o.tile([P, PACK, D], F32, tag="turned")
+            for j in range(PACK):
+                rows = slice(P * (PACK * g + j), P * (PACK * g + j + 1))
+                cols = slice(D * n, D * (n + 1))
+                nc.tensor.matmul_mx(
+                    out=v_ps[:, j, :],
+                    lhsT=x_codes[:, rows].bitcast(FP8X4),
+                    lhsT_scale=x_scales[:, rows],
+                    rhs=w_codes[:, cols].bitcast(FP8X4),
+                    rhs_scale=w_scales[:, cols],
+                    start=True,
+                    stop=True,
+                )
+            tiles["v_ps"] = v_ps
 
-        def quantise_v(n):
+        def take_values(n, g):
+            grouped = v_grouped[:, n, g, :, :]
+            by_keys = tiles["v_ps"][:].rearrange("p j d -> p d j")
+            nc.scalar.copy(out=grouped, in_=by_keys)
+
+        def quantise_v(n, g):
             nc.vector.quantize_mx(
-                out=v_codes[:, n, :, :].rearrange("p g d -> p (g d)").bitcast(FP8X4),
-                scales=v_scales[:, n, :, :].rearrange("p g d -> p (g d)"),
-                in_=v_grouped[:, n, :, :, :].rearrange("p g d j -> p (g d j)"),
+                out=v_codes[:, g, n, :].bitcast(FP8X4),
+                scales=v_scales[:, g, n, :],
+                in_=v_grouped[:, n, g, :, :].rearrange("p d j -> p (d j)"),
             )
 
-        tiles = {}
 
         def kind(i):
             return KINDS[i % NT]
@@ -241,7 +244,7 @@ def tile_relativepositionmultiheadattention_pa_kernel(tc, q, k, x, w_v, rel_w, r
                 return
             flat = tiles["flat", i]
             pieces = 1 if kind(i) == MATMUL else 3
-            b_ps = psum_t.tile([P, pieces, P], BF16, tag="turned")
+            b_ps = psum_t.tile([P, pieces, P], BF16, tag="bias", bufs=1)
             for b in range(pieces):
                 nc.tensor.transpose(out=b_ps[:, b, :], in_=flat[:, P * b : P * (b + 1)], identity=ident_bf[:])
             tiles["b_ps", i] = b_ps
@@ -255,15 +258,27 @@ def tile_relativepositionmultiheadattention_pa_kernel(tc, q, k, x, w_v, rel_w, r
                 nc.scalar.copy(out=turned[:], in_=b_ps[:, 0, :])
                 tiles["turned", i] = turned
             else:
+                thin = bias.tile([P, 3, P], BF16)
+                nc.scalar.copy(out=thin[:], in_=b_ps[:])
+                tiles["thin", i] = thin
+
+        def widen_bias(i):
+            if kind(i) == TURN:
+                thin = tiles["thin", i]
                 turned = bias.tile([P, 3, P], F32)
-                nc.scalar.activation(out=turned[:], in_=b_ps[:], func=ACT.Copy, scale=ROOT)
+                nc.gpsimd.tensor_scalar(
+                    out=turned[:], in0=thin[:], scalar1=ROOT, scalar2=0.0, op0=ALU.mult, op1=ALU.add
+                )
                 tiles["turned", i] = turned
 
-        def scores(i):
+        def scores(i, h):
             n = i // NT
             t = i % NT
-            for h in range(L // HALF):
-                s_ps = psum_s.tile([P, HALF], F32)
+            if True:
+                if kind(i) == VECTOR:
+                    s_ps = psum_s.tile([P, HALF], F32, tag="logits", bufs=1)
+                else:
+                    s_ps = psum_s.tile([P, HALF], F32, tag="biased", bufs=3)
                 nc.tensor.matmul(
                     out=s_ps[:],
                     lhsT=qT[:, n, P * t : P * (t + 1)],
@@ -302,11 +317,14 @@ def tile_relativepositionmultiheadattention_pa_kernel(tc, q, k, x, w_v, rel_w, r
                         )
                 tiles["s_ps", i, h] = s_ps
 
-        def add_bias(i):
+        def add_bias(i, h):
             if kind(i) != VECTOR:
                 return
-            s = work.tile([P, L], F32)
-            for h in range(L // HALF):
+            if h == 0:
+                s = work.tile([P, L], F32)
+                tiles["s", i] = s
+            s = tiles["s", i]
+            if True:
                 cols = slice(HALF * h, HALF * (h + 1))
                 nc.vector.scalar_tensor_tensor(
                     out=s[:, cols],
@@ -316,20 +334,20 @@ def tile_relativepositionmultiheadattention_pa_kernel(tc, q, k, x, w_v, rel_w, r
                     op0=ALU.mult,
                     op1=ALU.add,
                 )
-            tiles["s", i] = s
 
         def row_max(i):
             if kind(i) == VECTOR:
                 neg_max = late.tile([P, 1], F32)
                 nc.vector.tensor_reduce(out=neg_max[:], in_=tiles["s", i][:], axis=AX.X, op=ALU.max, negate=True)
                 tiles["neg_max", i] = neg_max
-            else:
+
+        def half_max(i, h):
+            if h == 0:
                 neg_maxes = late.tile([P, 2], F32)
-                for h in range(L // HALF):
-                    nc.vector.tensor_reduce(
-                        out=neg_maxes[:, h : h + 1], in_=tiles["s_ps", i, h][:], axis=AX.X, op=ALU.max, negate=True
-                    )
                 tiles["neg_maxes", i] = neg_maxes
+            nc.vector.tensor_reduce(
+                out=tiles["neg_maxes", i][:, h : h + 1], in_=tiles["s_ps", i, h][:], axis=AX.X, op=ALU.max, negate=True
+            )
 
         def join_max(i):
             if kind(i) != VECTOR:
@@ -345,9 +363,12 @@ def tile_relativepositionmultiheadattention_pa_kernel(tc, q, k, x, w_v, rel_w, r
                 )
                 tiles["neg_max", i] = neg_max
 
-        def exponent(i):
-            e = work.tile([P, L], BF16)
-            row_sum = late.tile([P, 2], F32)
+        def exponent(i, h=0):
+            if h == 0:
+                e = work.tile([P, L], BF16)
+                tiles["e", i] = e
+            e = tiles["e", i]
+            row_sum = row_sums[:, i, :]
             if kind(i) == VECTOR:
                 nc.scalar.activation(
                     out=e[:],
@@ -358,7 +379,7 @@ def tile_relativepositionmultiheadattention_pa_kernel(tc, q, k, x, w_v, rel_w, r
                     accum_out=row_sum[:, 0:1],
                 )
             else:
-                for h in range(L // HALF):
+                if True:
                     nc.scalar.activation(
                         out=e[:, HALF * h : HALF * (h + 1)],
                         in_=tiles["s_ps", i, h][:],
@@ -367,15 +388,6 @@ def tile_relativepositionmultiheadattention_pa_kernel(tc, q, k, x, w_v, rel_w, r
                         scale=SCALE,
                         accum_out=row_sum[:, h : h + 1],
                     )
-            tiles["e", i] = e
-            tiles["row_sum", i] = row_sum
-
-        def join_sum(i):
-            if kind(i) != VECTOR:
-                row_sum = tiles["row_sum", i]
-                whole = late.tile([P, 1], F32)
-                nc.gpsimd.tensor_tensor(out=whole[:], in0=row_sum[:, 0:1], in1=row_sum[:, 1:2], op=ALU.add)
-                tiles["row_sum", i] = whole
 
         def turn_e(i):
             e_ps = psum_t.tile([P, NT // 2, P], F32, tag="turned")
@@ -406,25 +418,34 @@ def tile_relativepositionmultiheadattention_pa_kernel(tc, q, k, x, w_v, rel_w, r
             tiles["e_codes", i] = e_codes
             tiles["e_scales", i] = e_scales
 
-        def weigh_values(i):
+        def weigh_values(i, o_ps):
             n = i // NT
-            o_ps = psum_o.tile([P, D], F32, tag="turned")
             for g in range(NG):
                 nc.tensor.matmul_mx(
-                    out=o_ps[:],
+                    out=o_ps,
                     lhsT=tiles["e_codes", i][:, g, :].bitcast(FP8X4),
                     lhsT_scale=tiles["e_scales", i][:, g, :],
-                    rhs=v_codes[:, n, g, :].bitcast(FP8X4),
-                    rhs_scale=v_scales[:, n, g, :],
+                    rhs=v_codes[:, g, n, :].bitcast(FP8X4),
+                    rhs_scale=v_scales[:, g, n, :],
                     start=(g == 0),
                     stop=(g == NG - 1),
                 )
             tiles["o_ps", i] = o_ps
 
-        def invert_sum(i):
-            inv_sum = late.tile([P, 1], F32)
-            nc.vector.reciprocal(out=inv_sum[:], in_=tiles["row_sum", i][:, 0:1])
-            tiles["inv_sum", i] = inv_sum
+        def add_sums(i, j):
+            total = late.tile([P, 2, 1], F32)
+            lo = min(i, j)
+            step = abs(i - j)
+            nc.vector.tensor_reduce(
+                out=total[:, :, 0], in_=row_sums[:, lo : lo + step + 1 : step, :], axis=AX.X, op=ALU.add
+            )
+            tiles["total", i] = total
+
+        def invert_sums(i, j):
+            inverse = late.tile([P, 2], F32)
+            nc.vector.reciprocal(out=inverse[:], in_=tiles["total", i][:, :, 0])
+            tiles["inv_sum", min(i, j)] = inverse[:, 0:1]
+            tiles["inv_sum", max(i, j)] = inverse[:, 1:2]
 
         out_rows = out.rearrange("b h w c -> (b h w) c")
 
@@ -433,54 +454,124 @@ def tile_relativepositionmultiheadattention_pa_kernel(tc, q, k, x, w_v, rel_w, r
             t = i % NT
             o_sb = work.tile([P, D], F32)
             nc.scalar.activation(
-                out=o_sb[:], in_=tiles["o_ps", i][:], func=ACT.Copy, scale=tiles["inv_sum", i][:, 0:1]
+                out=o_sb[:], in_=tiles["o_ps", i], func=ACT.Copy, scale=tiles["inv_sum", i]
             )
             nc.sync.dma_start(out=out_rows[P * t : P * (t + 1), D * n : D * (n + 1)], in_=o_sb[:])
 
-        def if_tile(stage, j):
-            if 0 <= j < TILES:
-                stage(ORDER[j])
 
-        turn_head(0)
-        for j in range(4):
-            gather_bias(ORDER[j])
-        for c in range(-1, TILES + 8):
-            if c + 4 >= 4:
-                if_tile(gather_bias, c + 4)
-            if_tile(join_sum, c - 3)
-            if_tile(turn_bias, c + 2)
-            if_tile(scores, c + 1)
-            if_tile(weigh_values, c - 6)
-            if_tile(turn_e, c - 2)
-            if_tile(row_max, c - 1)
-            if_tile(quantise_e, c - 4)
-            if_tile(join_max, c - 1)
-            if_tile(add_bias, c + 0)
-            if_tile(invert_sum, c - 6)
-            if_tile(low_half, c + 3)
-            if_tile(take_bias, c + 2)
-            if_tile(exponent, c - 1)
-            if_tile(normalise_and_store, c - 6)
-            if_tile(group_e, c - 2)
-            if c == 0:
+        def biased(k):
+            return NT * (k // 4) + 4 + k % 4
+
+        def plain(k):
+            return NT * (k // 4) + k % 4
+
+        extras = {1: [("v", 0, 0), ("v", 0, 1)], 2: [("k", 1, 0), ("q", 1, 0)], 3: [("v", 1, 0), ("v", 1, 1)]}
+        for n in range(2, NH):
+            for s, extra in enumerate([("k", n, 0), ("q", n, 0), ("v", n, 0), ("v", n, 1)]):
+                extras[4 * n - 4 + s] = [extra]
+
+        def start_extra(what, n, g):
+            if what == "k":
+                turn_rows(n, k_sb)
+            if what == "q":
+                turn_rows(n, q_sb)
+            if what == "v":
+                project_values(n, g)
+
+        def take_extra(what, n, g):
+            if what == "k":
+                take_rows(n, kT)
+            if what == "q":
+                take_rows(n, qT)
+            if what == "v":
+                take_values(n, g)
+
+        turn_rows(0, k_sb)
+        take_rows(0, kT)
+        turn_rows(0, q_sb)
+        take_rows(0, qT)
+        for k in range(-3, PAIRS + 5):
+            if 0 <= k + 3 < PAIRS:
+                gather_bias(biased(k + 3))
+                low_half(biased(k + 3))
+            if 0 <= k + 1 < PAIRS:
+                gather_bias(plain(k + 1))
+            if 0 <= k < PAIRS:
+                scores(biased(k), 0)
+            if 0 <= k - 1 < PAIRS:
+                join_max(biased(k - 1))
+            if 0 <= k - 1 < PAIRS:
+                add_bias(plain(k - 1), 1)
+            if 0 <= k - 1 < PAIRS:
+                exponent(biased(k - 1), 0)
+            if 0 <= k - 2 < PAIRS:
+                quantise_e(biased(k - 2))
+            if 0 <= k - 2 < PAIRS:
+                add_sums(biased(k - 2), plain(k - 2))
+            if 0 <= k - 2 < PAIRS:
+                turn_e(plain(k - 2))
+            mine = extras.get(k, [])
+            for extra in mine[:1]:
+                start_extra(*extra)
+            if 0 <= k - 1 < PAIRS:
+                row_max(plain(k - 1))
+            if 0 <= k - 1 < PAIRS:
+                exponent(biased(k - 1), 1)
+            if 0 <= k < PAIRS:
+                scores(biased(k), 1)
+            if 0 <= k - 2 < PAIRS:
+                invert_sums(biased(k - 2), plain(k - 2))
+            if 0 <= k - 3 < PAIRS:
+                normalise_and_store(biased(k - 3))
+            if 0 <= k - 4 < PAIRS:
+                normalise_and_store(plain(k - 4))
+            if 0 <= k + 1 < PAIRS:
+                take_bias(biased(k + 1))
+            if 0 <= k + 1 < PAIRS:
+                widen_bias(biased(k + 1))
+            for extra in mine[:1]:
+                take_extra(*extra)
+            for extra in mine[1:]:
+                start_extra(*extra)
+                take_extra(*extra)
+            for what, n, g in extras.get(k - 1, []):
+                if what == "v":
+                    quantise_v(n, g)
+            if 0 <= k - 3 < PAIRS:
+                quantise_e(plain(k - 3))
+            if 0 <= k < PAIRS:
+                scores(plain(k), 0)
+            if 0 <= k < PAIRS:
+                half_max(biased(k), 0)
+            if 0 <= k - 1 < PAIRS:
+                exponent(plain(k - 1))
+            if 0 <= k - 1 < PAIRS:
+                turn_e(biased(k - 1))
+            if 0 <= k < PAIRS:
+                add_bias(plain(k), 0)
+            if 2 <= k < PAIRS + 3:
+                o_ps = psum_o.tile([P, 2, D], F32, tag="out", bufs=1)
+            if 0 <= k - 2 < PAIRS:
+                weigh_values(biased(k - 2), o_ps[:, 0, :])
+            if 0 <= k - 3 < PAIRS:
+                weigh_values(plain(k - 3), o_ps[:, 1, :])
+            if 0 <= k < PAIRS:
+                half_max(biased(k), 1)
+            if 0 <= k - 1 < PAIRS:
+                group_e(biased(k - 1))
+            if 0 <= k + 2 < PAIRS:
+                turn_bias(biased(k + 2))
+            if 0 <= k < PAIRS:
+                scores(plain(k), 1)
+            if 0 <= k - 2 < PAIRS:
+                group_e(plain(k - 2))
+            if k == -1:
+                group_w()
+                quantise_w()
                 turn_x(0)
                 turn_x(1)
-                group_w()
-            if c == 1:
+                quantise_x(0)
+            if k == 0:
                 turn_x(2)
                 turn_x(3)
-            if c == 2:
-                quantise_w()
-                quantise_x(0)
-            if c == 3:
                 quantise_x(1)
-            if c == 4:
-                project_values(0)
-            if c == 5:
-                quantise_v(0)
-            if c % NT == 0 and 1 <= c // NT < NH and c > 5:
-                project_values(c // NT)
-            if c % NT == 1 and 1 <= c // NT < NH and c > 5:
-                quantise_v(c // NT)
-            if c % NT == 3 and c // NT + 1 < NH:
-                turn_head(c // NT + 1)

@@ -31,7 +31,9 @@ FLOPS = 2 * L * C * C + 2 * 2 * NH * L * L * D
 TILES = NH * NT
 COLS = P // (HALF // GRID)
 VECTOR, MATMUL, TURN = range(3)
-KINDS = [VECTOR] * 4 + [MATMUL] + [TURN] * 3
+VECTORS = 4
+TURNS = 4
+MATMULS = (4, 5, NT + 4, 2 * NT + 4)
 PAIRS = TILES // 2
 
 
@@ -42,15 +44,22 @@ def tile_relativepositionmultiheadattention_pa_kernel(tc, q, k, x, w_v, rel_w, r
         keep = ctx.enter_context(tc.tile_pool(name="keep", bufs=1))
         bias = ctx.enter_context(tc.tile_pool(name="bias", bufs=4))
         work = ctx.enter_context(tc.tile_pool(name="work", bufs=4))
-        late = ctx.enter_context(tc.tile_pool(name="late", bufs=8))
+        late = ctx.enter_context(tc.tile_pool(name="late", bufs=18))
         psum_s = ctx.enter_context(tc.psum_pool(name="psum_s", bufs=2))
         psum_t = ctx.enter_context(tc.psum_pool(name="psum_t", bufs=2))
-        psum_o = psum_t
+
+        def bank(role, shape, dtype):
+            return psum_t.tile(shape, dtype, name=role, tag=role, bufs=2 if role == "turned" else 1)
+
 
         ident_bf = keep.tile([P, P], BF16)
         make_identity(nc, ident_bf[:])
         ident_f32 = keep.tile([P, P], F32)
         make_identity(nc, ident_f32[:])
+        swap = keep.tile([P, P], F32)
+        nc.vector.tensor_copy(
+            out=swap[:].rearrange("p (r g) -> p r g", g=COLS), in_=ident_f32[:].rearrange("p (g r) -> p r g", g=COLS)
+        )
         wrap = keep.tile([P, 2 * GRID], BF16)
         nc.gpsimd.tensor_tensor(
             out=wrap[:], in0=ident_bf[:, 0 : 2 * GRID], in1=ident_bf[:, 2 * GRID : 4 * GRID], op=ALU.add
@@ -77,14 +86,19 @@ def tile_relativepositionmultiheadattention_pa_kernel(tc, q, k, x, w_v, rel_w, r
         rh = rh.rearrange("a (r j) -> a r j", j=skew)[:, :, 0:GRID]
         rh = rh.rearrange("(n c) (t rl) j -> n rl c t j", c=GRID, rl=ROWS)
 
-        def load_bias(queue, n):
+        def load_cols(queue, n):
             of_head = slice(NT * n, NT * (n + 1))
             for rl in range(ROWS):
                 rows = slice(GRID * rl, GRID * (rl + 1))
                 queue.dma_start(out=col_bias[rows, of_head, :], in_=rw[rl][:, of_head, :])
+
+        def load_rows(queue, n):
+            of_head = slice(NT * n, NT * (n + 1))
+            for rl in range(ROWS):
+                rows = slice(GRID * rl, GRID * (rl + 1))
                 queue.dma_start(out=row_bias[rows, of_head, :], in_=rh[n, rl])
 
-        load_bias(nc.scalar, 0)
+        load_cols(nc.scalar, 0)
         q_rows = q.rearrange("b n (t p) d -> (b n) p t d", p=P)
         k_rows = k.rearrange("b n (t p) d -> (b n) p t d", p=P)
         q_sb = []
@@ -97,29 +111,32 @@ def tile_relativepositionmultiheadattention_pa_kernel(tc, q, k, x, w_v, rel_w, r
         x_in = x_sb[:].rearrange("p (u k) -> p u k", k=2 * C)
         x_rows = x.rearrange("b h w c -> (b h w) c").rearrange("(u p e) c -> p u (e c)", p=P, e=2)
         nc.sync.dma_start(out=k_sb[0][:], in_=k_rows[0])
+        nc.sync.dma_start(out=q_sb[0][:], in_=q_rows[0])
+        load_rows(nc.sync, 0)
         nc.sync.dma_start(
             out=w_sb[:].rearrange("p (u e) c -> p u (e c)", e=2),
             in_=w_v.rearrange("(u p e) c -> p u (e c)", u=2, e=2),
         )
-        nc.sync.dma_start(out=q_sb[0][:], in_=q_rows[0])
         for half in range(2):
             nc.sync.dma_start(out=x_in[:, 2 * half : 2 * half + 2, :], in_=x_rows[:, 2 * half : 2 * half + 2, :])
-        for n in range(1, NH):
-            load_bias(nc.sync, n)
+        def load_head(n):
             nc.sync.dma_start(out=k_sb[n][:], in_=k_rows[n])
             nc.sync.dma_start(out=q_sb[n][:], in_=q_rows[n])
+            load_cols(nc.sync, n)
+            load_rows(nc.sync, n)
 
         qT = keep.tile([P, NH, L], BF16)
         kT = keep.tile([P, NH, L], BF16)
 
-        def turn_rows(n, rows_sb):
-            r_ps = psum_t.tile([P, NT, P], BF16, tag="turned")
+        def turn_rows(n, rows_sb, role):
+            r_ps = bank(role, [P, NT, P], BF16)
             for t in range(NT):
                 nc.tensor.transpose(out=r_ps[:, t, :], in_=rows_sb[n][:, t, :], identity=ident_bf[:])
-            tiles["r_ps"] = r_ps
+            tiles["r_ps", n, rows_sb is k_sb] = r_ps
 
         def take_rows(n, turned):
-            nc.scalar.copy(out=turned[:, n, :], in_=tiles["r_ps"][:].rearrange("p t l -> p (t l)"))
+            r_ps = tiles["r_ps", n, turned is kT]
+            nc.scalar.copy(out=turned[:, n, :], in_=r_ps[:].rearrange("p t l -> p (t l)"))
 
         tiles = {}
 
@@ -132,16 +149,20 @@ def tile_relativepositionmultiheadattention_pa_kernel(tc, q, k, x, w_v, rel_w, r
         x_grouped = keep.tile([P, L * PACK], BF16, align_bytes=64)
         w_grouped = keep.tile([P, C, PACK], BF16, align_bytes=64)
 
-        def turn_x(b):
+        def turn_x(b, role):
             x_words = x_sb[:].bitcast(F32)
-            x_grouped_words = x_grouped[:].bitcast(F32).rearrange("p (l u) -> p l u", u=2)
-            x_ps = psum_o.tile([P, 2, 2, P], F32, tag="turned")
+            x_ps = bank(role, [P, 2, 2, P], F32)
             for tt in range(2):
                 for u in range(2):
                     first = (C // 2) * (2 * b + tt) + P * u
                     nc.tensor.transpose(
                         out=x_ps[:, tt, u, :], in_=x_words[:, first : first + P], identity=ident_f32[:]
                     )
+            tiles["x_ps", b] = x_ps
+
+        def take_x(b):
+            x_grouped_words = x_grouped[:].bitcast(F32).rearrange("p (l u) -> p l u", u=2)
+            x_ps = tiles["x_ps", b]
             grouped = x_grouped_words[:, 2 * P * b : 2 * P * (b + 1), :].rearrange("p (t l) u -> p t l u", t=2)
             if b % 2 == 0:
                 nc.vector.tensor_copy(out=grouped, in_=x_ps[:].rearrange("p t u l -> p t l u"))
@@ -166,8 +187,8 @@ def tile_relativepositionmultiheadattention_pa_kernel(tc, q, k, x, w_v, rel_w, r
 
         v_grouped = keep.tile([P, NH, NG, D, PACK], BF16, align_bytes=64)
 
-        def project_values(n, g):
-            v_ps = psum_o.tile([P, PACK, D], F32, tag="turned")
+        def project_values(n, g, role):
+            v_ps = bank(role, [P, PACK, D], F32)
             for j in range(PACK):
                 rows = slice(P * (PACK * g + j), P * (PACK * g + j + 1))
                 cols = slice(D * n, D * (n + 1))
@@ -180,12 +201,15 @@ def tile_relativepositionmultiheadattention_pa_kernel(tc, q, k, x, w_v, rel_w, r
                     start=True,
                     stop=True,
                 )
-            tiles["v_ps"] = v_ps
+            tiles["v_ps", n, g] = v_ps
 
         def take_values(n, g):
             grouped = v_grouped[:, n, g, :, :]
-            by_keys = tiles["v_ps"][:].rearrange("p j d -> p d j")
-            nc.scalar.copy(out=grouped, in_=by_keys)
+            by_keys = tiles["v_ps", n, g][:].rearrange("p j d -> p d j")
+            if g == 0:
+                nc.scalar.copy(out=grouped, in_=by_keys)
+            else:
+                nc.vector.tensor_copy(out=grouped, in_=by_keys)
 
         def quantise_v(n, g):
             nc.vector.quantize_mx(
@@ -196,87 +220,81 @@ def tile_relativepositionmultiheadattention_pa_kernel(tc, q, k, x, w_v, rel_w, r
 
 
         def kind(i):
-            return KINDS[i % NT]
+            if i % NT < VECTORS:
+                return VECTOR
+            return MATMUL if i in MATMULS else TURN
 
         def build_pos(i):
             pos = bias.tile([P, L], F32)
-            nc.gpsimd.tensor_tensor(
-                out=pos[:].rearrange("p (a b) -> p a b", b=GRID),
-                in0=col_bias[:, i, :].unsqueeze(1).to_broadcast([P, GRID, GRID]),
-                in1=row_bias[:, i, :].unsqueeze(2).to_broadcast([P, GRID, GRID]),
-                op=ALU.add,
-            )
+            part = GRID // 4
+            for r in range(0, GRID, part):
+                nc.gpsimd.tensor_tensor(
+                    out=pos[:, GRID * r : GRID * (r + part)].rearrange("p (a b) -> p a b", b=GRID),
+                    in0=col_bias[:, i, :].unsqueeze(1).to_broadcast([P, part, GRID]),
+                    in1=row_bias[:, i, r : r + part].unsqueeze(2).to_broadcast([P, part, GRID]),
+                    op=ALU.add,
+                )
             tiles["pos", i] = pos
 
-        def gather_bias(i):
-            if kind(i) == VECTOR:
-                build_pos(i)
-            elif kind(i) == MATMUL:
-                halves = bias.tile([P, 2, 2 * GRID], BF16)
-                rel = bias_in[:, i, :, :].rearrange("p k j -> p (k j)")
-                nc.gpsimd.tensor_scalar(out=halves[:, 0, :], in0=rel, scalar1=ROOT, scalar2=0.0, op0=ALU.mult, op1=ALU.add)
-                tiles["halves", i] = halves
-            else:
-                flat = bias.tile([P, 3, P], BF16)
-                nc.gpsimd.tensor_scalar(
-                    out=flat[:, 0, :].rearrange("p (a b) -> p a b", b=GRID),
-                    in0=col_bias[:, i, :].unsqueeze(1).to_broadcast([P, ROWS, GRID]),
-                    scalar1=1.0, scalar2=0.0, op0=ALU.mult, op1=ALU.add,
-                )
-                nc.gpsimd.tensor_scalar(
-                    out=flat[:, 1:3, :].rearrange("p h (a b) -> p (h a) b", b=COLS),
-                    in0=row_bias[:, i, :].unsqueeze(2).to_broadcast([P, GRID, COLS]),
-                    scalar1=1.0, scalar2=0.0, op0=ALU.mult, op1=ALU.add,
-                )
-                tiles["flat", i] = flat[:].rearrange("p k j -> p (k j)")
+        def split_bias(i):
+            halves = bias.tile([P, 2, 2 * GRID], BF16)
+            rel = bias_in[:, i, :, :].rearrange("p k j -> p (k j)")
+            nc.gpsimd.tensor_scalar(out=halves[:, 0, :], in0=rel, scalar1=ROOT, scalar2=0.0, op0=ALU.mult, op1=ALU.add)
+            tiles["halves", i] = halves
 
         def low_half(i):
-            if kind(i) == MATMUL:
-                halves = tiles["halves", i]
-                rel = bias_in[:, i, :, :].rearrange("p k j -> p (k j)")
-                nc.vector.scalar_tensor_tensor(
-                    out=halves[:, 1, :], in0=rel, scalar=ROOT, in1=halves[:, 0, :], op0=ALU.mult, op1=ALU.subtract
-                )
-                tiles["flat", i] = halves[:].rearrange("p k j -> p (k j)")
+            halves = tiles["halves", i]
+            rel = bias_in[:, i, :, :].rearrange("p k j -> p (k j)")
+            nc.vector.scalar_tensor_tensor(
+                out=halves[:, 1, :], in0=rel, scalar=ROOT, in1=halves[:, 0, :], op0=ALU.mult, op1=ALU.subtract
+            )
 
         def turn_bias(i):
-            if kind(i) == VECTOR:
-                return
-            flat = tiles["flat", i]
-            pieces = 1 if kind(i) == MATMUL else 3
-            b_ps = psum_t.tile([P, pieces, P], BF16, tag="bias", bufs=1)
-            for b in range(pieces):
-                nc.tensor.transpose(out=b_ps[:, b, :], in_=flat[:, P * b : P * (b + 1)], identity=ident_bf[:])
+            b_ps = bank("turned", [P, P], BF16)
+            flat = tiles["halves", i][:].rearrange("p k j -> p (k j)")
+            nc.tensor.transpose(out=b_ps[:], in_=flat, identity=ident_bf[:])
             tiles["b_ps", i] = b_ps
 
         def take_bias(i):
-            if kind(i) == VECTOR:
-                return
-            b_ps = tiles["b_ps", i]
-            if kind(i) == MATMUL:
-                turned = bias.tile([P, P], BF16)
-                nc.scalar.copy(out=turned[:], in_=b_ps[:, 0, :])
-                tiles["turned", i] = turned
-            else:
-                thin = bias.tile([P, 3, P], BF16)
-                nc.scalar.copy(out=thin[:], in_=b_ps[:])
-                tiles["thin", i] = thin
+            turned = bias.tile([P, P], BF16)
+            nc.scalar.copy(out=turned[:], in_=tiles["b_ps", i][:])
+            tiles["turned", i] = turned
 
-        def widen_bias(i):
-            if kind(i) == TURN:
-                thin = tiles["thin", i]
-                turned = bias.tile([P, 3, P], F32)
-                nc.gpsimd.tensor_scalar(
-                    out=turned[:], in0=thin[:], scalar1=ROOT, scalar2=0.0, op0=ALU.mult, op1=ALU.add
-                )
-                tiles["turned", i] = turned
+        out_rows = out.rearrange("b h w c -> (b h w) c")
+        park = [out_rows[2 * P * n : 2 * P * (n + 1), D * (NH - 1) : D * NH] for n in range(NH)]
+
+        def turn_head_bias(n):
+            b_ps = bank("turned", [P, 2, P], BF16)
+            for s in range(2):
+                first = NT * n + VECTORS + 2 * s
+                rel = bias_in[:, first : first + 2, :, :].rearrange("p t k j -> p (t k j)")
+                nc.tensor.transpose(out=b_ps[:, s, :], in_=rel, identity=ident_bf[:])
+            tiles["head_bias", n] = b_ps
+
+        def take_head_bias(n):
+            tall = keep.tile([P, 2, P], F32, name="tall%d" % n)
+            nc.vector.tensor_scalar(
+                out=tall[:], in0=tiles["head_bias", n][:], scalar1=ROOT, scalar2=0.0, op0=ALU.mult, op1=ALU.add
+            )
+            nc.sync.dma_start(out=park[n].rearrange("(s p) q -> p s q", p=P), in_=tall[:])
+            wide = keep.tile([P, 3, TURNS, P], F32, name="wide%d" % n)
+            by_kind = park[n].rearrange("(t k j) q -> k j t q", t=NT - VECTORS, k=2)
+            for g in range(ROWS):
+                nc.sync.dma_start(out=wide[GRID * g : GRID * (g + 1), 0, :, :], in_=by_kind[0])
+            half = HALF // GRID
+            for h in range(2):
+                for g in range(COLS):
+                    nc.sync.dma_start(
+                        out=wide[half * g : half * (g + 1), 1 + h, :, :], in_=by_kind[1, half * h : half * (h + 1)]
+                    )
+            tiles["wide", n] = wide
 
         def scores(i, h):
             n = i // NT
             t = i % NT
             if True:
                 if kind(i) == VECTOR:
-                    s_ps = psum_s.tile([P, HALF], F32, tag="logits", bufs=1)
+                    s_ps = psum_s.tile([P, HALF], F32, tag="logits", bufs=2)
                 else:
                     s_ps = psum_s.tile([P, HALF], F32, tag="biased", bufs=3)
                 nc.tensor.matmul(
@@ -295,11 +313,12 @@ def tile_relativepositionmultiheadattention_pa_kernel(tc, q, k, x, w_v, rel_w, r
                         stop=True,
                     )
                 if kind(i) == TURN:
-                    turned = tiles["turned", i]
+                    wide = tiles["wide", n]
+                    te = t - VECTORS
                     for b in range(HALF // P):
                         nc.tensor.matmul(
                             out=s_ps[:, P * b : P * (b + 1)],
-                            lhsT=turned[:, 0, :],
+                            lhsT=wide[:, 0, te, :],
                             rhs=ident_f32[:],
                             start=False,
                             stop=False,
@@ -309,8 +328,8 @@ def tile_relativepositionmultiheadattention_pa_kernel(tc, q, k, x, w_v, rel_w, r
                     for b in range(HALF // P):
                         nc.tensor.matmul(
                             out=by_cols[:, b, :, :],
-                            lhsT=turned[:, 1 + h, :],
-                            rhs=ident_f32[:],
+                            lhsT=wide[:, 1 + h, te, :],
+                            rhs=swap[:],
                             start=False,
                             stop=b == HALF // P - 1,
                             is_transpose=True,
@@ -447,8 +466,6 @@ def tile_relativepositionmultiheadattention_pa_kernel(tc, q, k, x, w_v, rel_w, r
             tiles["inv_sum", min(i, j)] = inverse[:, 0:1]
             tiles["inv_sum", max(i, j)] = inverse[:, 1:2]
 
-        out_rows = out.rearrange("b h w c -> (b h w) c")
-
         def normalise_and_store(i):
             n = i // NT
             t = i % NT
@@ -459,119 +476,143 @@ def tile_relativepositionmultiheadattention_pa_kernel(tc, q, k, x, w_v, rel_w, r
             nc.sync.dma_start(out=out_rows[P * t : P * (t + 1), D * n : D * (n + 1)], in_=o_sb[:])
 
 
-        def biased(k):
-            return NT * (k // 4) + 4 + k % 4
+        def biased(p):
+            return NT * (p // VECTORS) + VECTORS + p % VECTORS
 
-        def plain(k):
-            return NT * (k // 4) + k % 4
+        def plain(p):
+            return NT * (p // VECTORS) + p % VECTORS
 
-        extras = {1: [("v", 0, 0), ("v", 0, 1)], 2: [("k", 1, 0), ("q", 1, 0)], 3: [("v", 1, 0), ("v", 1, 1)]}
-        for n in range(2, NH):
-            for s, extra in enumerate([("k", n, 0), ("q", n, 0), ("v", n, 0), ("v", n, 1)]):
-                extras[4 * n - 4 + s] = [extra]
+        pieces = {
+            0: [("k", 1, 0)],
+            1: [("q", 1, 0)],
+            2: [("x", 0, 0), ("x", 1, 0)],
+            3: [("x", 2, 0), ("x", 3, 0)],
+            4: [("v", 0, 0), ("k", 2, 0)],
+            5: [("v", 0, 1), ("q", 2, 0)],
+            6: [("v", 1, 0)],
+            7: [("v", 1, 1)],
+            8: [("v", 2, 0)],
+            9: [("k", 3, 0), ("v", 2, 1)],
+            10: [("q", 3, 0)],
+            11: [("v", 3, 0)],
+            12: [("v", 3, 1)],
+        }
 
-        def start_extra(what, n, g):
+        weigh_at = {}
+        pair = 0
+        for k in range(7, PAIRS + 3):
+            for step in range(2):
+                if pair <= min(k - 2, PAIRS - 1):
+                    weigh_at.setdefault(k, []).extend([biased(pair), plain(pair)])
+                    pair += 1
+
+        def start_piece(what, n, half, role):
             if what == "k":
-                turn_rows(n, k_sb)
+                turn_rows(n, k_sb, role)
             if what == "q":
-                turn_rows(n, q_sb)
+                turn_rows(n, q_sb, role)
             if what == "v":
-                project_values(n, g)
+                project_values(n, half, role)
+            if what == "x":
+                turn_x(n, role)
 
-        def take_extra(what, n, g):
+        def take_piece(what, n, half):
             if what == "k":
                 take_rows(n, kT)
             if what == "q":
                 take_rows(n, qT)
             if what == "v":
-                take_values(n, g)
+                take_values(n, half)
+            if what == "x":
+                take_x(n)
 
-        turn_rows(0, k_sb)
-        take_rows(0, kT)
-        turn_rows(0, q_sb)
-        take_rows(0, qT)
-        for k in range(-3, PAIRS + 5):
-            if 0 <= k + 3 < PAIRS:
-                gather_bias(biased(k + 3))
-                low_half(biased(k + 3))
-            if 0 <= k + 1 < PAIRS:
-                gather_bias(plain(k + 1))
-            if 0 <= k < PAIRS:
-                scores(biased(k), 0)
-            if 0 <= k - 1 < PAIRS:
-                join_max(biased(k - 1))
-            if 0 <= k - 1 < PAIRS:
-                add_bias(plain(k - 1), 1)
-            if 0 <= k - 1 < PAIRS:
-                exponent(biased(k - 1), 0)
-            if 0 <= k - 2 < PAIRS:
-                quantise_e(biased(k - 2))
-            if 0 <= k - 2 < PAIRS:
-                add_sums(biased(k - 2), plain(k - 2))
-            if 0 <= k - 2 < PAIRS:
-                turn_e(plain(k - 2))
-            mine = extras.get(k, [])
-            for extra in mine[:1]:
-                start_extra(*extra)
-            if 0 <= k - 1 < PAIRS:
-                row_max(plain(k - 1))
-            if 0 <= k - 1 < PAIRS:
-                exponent(biased(k - 1), 1)
-            if 0 <= k < PAIRS:
-                scores(biased(k), 1)
-            if 0 <= k - 2 < PAIRS:
-                invert_sums(biased(k - 2), plain(k - 2))
-            if 0 <= k - 3 < PAIRS:
-                normalise_and_store(biased(k - 3))
-            if 0 <= k - 4 < PAIRS:
-                normalise_and_store(plain(k - 4))
-            if 0 <= k + 1 < PAIRS:
-                take_bias(biased(k + 1))
-            if 0 <= k + 1 < PAIRS:
-                widen_bias(biased(k + 1))
-            for extra in mine[:1]:
-                take_extra(*extra)
-            for extra in mine[1:]:
-                start_extra(*extra)
-                take_extra(*extra)
-            for what, n, g in extras.get(k - 1, []):
-                if what == "v":
-                    quantise_v(n, g)
-            if 0 <= k - 3 < PAIRS:
-                quantise_e(plain(k - 3))
-            if 0 <= k < PAIRS:
-                scores(plain(k), 0)
-            if 0 <= k < PAIRS:
-                half_max(biased(k), 0)
-            if 0 <= k - 1 < PAIRS:
-                exponent(plain(k - 1))
-            if 0 <= k - 1 < PAIRS:
-                turn_e(biased(k - 1))
-            if 0 <= k < PAIRS:
-                add_bias(plain(k), 0)
-            if 2 <= k < PAIRS + 3:
-                o_ps = psum_o.tile([P, 2, D], F32, tag="out", bufs=1)
-            if 0 <= k - 2 < PAIRS:
-                weigh_values(biased(k - 2), o_ps[:, 0, :])
-            if 0 <= k - 3 < PAIRS:
-                weigh_values(plain(k - 3), o_ps[:, 1, :])
-            if 0 <= k < PAIRS:
-                half_max(biased(k), 1)
-            if 0 <= k - 1 < PAIRS:
-                group_e(biased(k - 1))
-            if 0 <= k + 2 < PAIRS:
-                turn_bias(biased(k + 2))
-            if 0 <= k < PAIRS:
-                scores(plain(k), 1)
-            if 0 <= k - 2 < PAIRS:
-                group_e(plain(k - 2))
-            if k == -1:
+        def finish_piece(what, n, half):
+            if what == "v":
+                quantise_v(n, half)
+            if what == "x" and n % 2 == 1:
+                quantise_x(n // 2)
+
+        def head_at(k):
+            if k == -3:
+                return 0
+            return k // 4 + 1 if k % 4 == 0 and 0 < k // 4 + 1 < NH else None
+
+        def matmul_tile(p):
+            return biased(p) if 0 <= p < PAIRS and kind(biased(p)) == MATMUL else None
+
+        def start_pieces(k):
+            for piece, role in zip(pieces.get(k, []), ("turned", "out")):
+                start_piece(*piece, role)
+            if head_at(k) is not None:
+                turn_head_bias(head_at(k))
+            if matmul_tile(k + 3) is not None:
+                turn_bias(matmul_tile(k + 3))
+
+        def take_pieces(k):
+            if matmul_tile(k + 3) is not None:
+                take_bias(matmul_tile(k + 3))
+            for piece in pieces.get(k, []):
+                take_piece(*piece)
+
+        def finish_pieces(k):
+            if k == 1:
                 group_w()
+            if k == 2:
                 quantise_w()
-                turn_x(0)
-                turn_x(1)
-                quantise_x(0)
-            if k == 0:
-                turn_x(2)
-                turn_x(3)
-                quantise_x(1)
+            if head_at(k) is not None:
+                take_head_bias(head_at(k))
+            for piece in pieces.get(k - 1, []):
+                finish_piece(*piece)
+
+        def weigh(k):
+            if k in weigh_at:
+                o_ps = bank("out", [P, 4, D], F32)
+                for slot, i in enumerate(weigh_at[k]):
+                    weigh_values(i, o_ps[:, slot, :])
+
+        def normalise(k):
+            for i in weigh_at.get(k, []):
+                normalise_and_store(i)
+
+        def on(p, stage, *args):
+            if 0 <= p < PAIRS:
+                stage(*[a(p) if a in (biased, plain) else a for a in args])
+
+        turn_rows(0, k_sb, "turned")
+        take_rows(0, kT)
+        turn_rows(0, q_sb, "turned")
+        take_rows(0, qT)
+        for k in range(-5, PAIRS + 3):
+            if 0 < k + 5 < NH:
+                load_head(k + 5)
+            on(k + 1, build_pos, plain)
+            if matmul_tile(k + 4) is not None:
+                split_bias(matmul_tile(k + 4))
+            on(k, join_max, biased)
+            on(k + 1, scores, plain, 0)
+            on(k + 1, scores, plain, 1)
+            on(k, row_max, plain)
+            on(k, exponent, biased, 0)
+            start_pieces(k)
+            weigh(k)
+            on(k, exponent, biased, 1)
+            on(k - 1, invert_sums, biased, plain)
+            on(k + 1, half_max, biased, 0)
+            on(k + 1, scores, biased, 1)
+            take_pieces(k)
+            on(k, exponent, plain)
+            on(k - 1, quantise_e, biased)
+            on(k - 1, quantise_e, plain)
+            finish_pieces(k)
+            on(k + 1, add_bias, plain, 0)
+            on(k, turn_e, biased)
+            on(k + 1, add_bias, plain, 1)
+            on(k, turn_e, plain)
+            on(k, group_e, biased)
+            normalise(k)
+            on(k + 1, half_max, biased, 1)
+            on(k + 2, scores, biased, 0)
+            on(k, group_e, plain)
+            on(k, add_sums, biased, plain)
+            if matmul_tile(k + 4) is not None:
+                low_half(matmul_tile(k + 4))

@@ -33,7 +33,7 @@ COLS = P // (HALF // GRID)
 VECTOR, MATMUL, TURN = range(3)
 VECTORS = 4
 TURNS = 4
-MATMULS = (4, 5, NT + 4, 2 * NT + 4)
+MATMULS = (4, 5, 6, 7)
 PAIRS = TILES // 2
 
 
@@ -408,8 +408,18 @@ def tile_relativepositionmultiheadattention_pa_kernel(tc, q, k, x, w_v, rel_w, r
                         accum_out=row_sum[:, h : h + 1],
                     )
 
-        def turn_e(i):
+        def turn_e(i, paced=False):
             e_ps = psum_t.tile([P, NT // 2, P], F32, tag="turned")
+            if paced:
+                nc.tensor.matmul_mx(
+                    out=e_ps[:].rearrange("p b m -> p (b m)"),
+                    lhsT=x_codes[:, 0:P].bitcast(FP8X4),
+                    lhsT_scale=x_scales[:, 0:P],
+                    rhs=w_codes[:].bitcast(FP8X4),
+                    rhs_scale=w_scales[:],
+                    start=True,
+                    stop=True,
+                )
             e_words = tiles["e", i][:].bitcast(F32)
             for b in range(NT // 2):
                 nc.tensor.transpose(
@@ -607,7 +617,7 @@ def tile_relativepositionmultiheadattention_pa_kernel(tc, q, k, x, w_v, rel_w, r
             on(k + 1, add_bias, plain, 0)
             on(k, turn_e, biased)
             on(k + 1, add_bias, plain, 1)
-            on(k, turn_e, plain)
+            on(k, turn_e, plain, k >= 5)
             on(k, group_e, biased)
             normalise(k)
             on(k + 1, half_max, biased, 1)

@@ -170,7 +170,9 @@ def tile_relativepositionmultiheadattention_pa_kernel(tc, q, k, x, w_v, rel_w, r
                 nc.scalar.copy(out=grouped, in_=x_ps[:].rearrange("p t u l -> p t l u"))
 
         def group_w():
-            nc.vector.tensor_copy(out=w_grouped[:], in_=w_sb[:].rearrange("p t c -> p c t"))
+            nc.gpsimd.tensor_scalar(
+                out=w_grouped[:], in0=w_sb[:].rearrange("p t c -> p c t"), scalar1=1.0, scalar2=0.0, op0=ALU.mult, op1=ALU.add
+            )
 
         def quantise_x(half):
             cols = slice(HALF * half, HALF * (half + 1))
@@ -236,29 +238,22 @@ def tile_relativepositionmultiheadattention_pa_kernel(tc, q, k, x, w_v, rel_w, r
                 )
             tiles["pos", i] = pos
 
-        def split_bias(i):
-            halves = bias.tile([P, 2, 2 * GRID], BF16)
-            rel = bias_in[:, i, :, :].rearrange("p k j -> p (k j)")
-            nc.gpsimd.tensor_scalar(out=halves[:, 0, :], in0=rel, scalar1=ROOT, scalar2=0.0, op0=ALU.mult, op1=ALU.add)
-            tiles["halves", i] = halves
+        halves = keep.tile([P, VECTORS, 2, 2 * GRID], BF16)
+        turned = keep.tile([P, VECTORS, P], BF16)
 
-        def low_half(i):
-            halves = tiles["halves", i]
-            rel = bias_in[:, i, :, :].rearrange("p k j -> p (k j)")
+        def turn_matmul_bias():
+            first = MATMULS[0]
+            rel = bias_in[:, first : first + VECTORS, :, :].rearrange("p t k j -> p t (k j)")
+            high = halves[:, :, 0, :]
+            nc.gpsimd.tensor_scalar(out=high, in0=rel, scalar1=ROOT, scalar2=0.0, op0=ALU.mult, op1=ALU.add)
             nc.vector.scalar_tensor_tensor(
-                out=halves[:, 1, :], in0=rel, scalar=ROOT, in1=halves[:, 0, :], op0=ALU.mult, op1=ALU.subtract
+                out=halves[:, :, 1, :], in0=rel, scalar=ROOT, in1=high, op0=ALU.mult, op1=ALU.subtract
             )
-
-        def turn_bias(i):
-            b_ps = bank("turned", [P, P], BF16)
-            flat = tiles["halves", i][:].rearrange("p k j -> p (k j)")
-            nc.tensor.transpose(out=b_ps[:], in_=flat, identity=ident_bf[:])
-            tiles["b_ps", i] = b_ps
-
-        def take_bias(i):
-            turned = bias.tile([P, P], BF16)
-            nc.scalar.copy(out=turned[:], in_=tiles["b_ps", i][:])
-            tiles["turned", i] = turned
+            b_ps = bank("out", [P, VECTORS, P], BF16)
+            for s in range(VECTORS):
+                flat = halves[:, s, :, :].rearrange("p h j -> p (h j)")
+                nc.tensor.transpose(out=b_ps[:, s, :], in_=flat, identity=ident_bf[:])
+            nc.scalar.copy(out=turned[:], in_=b_ps[:])
 
         out_rows = out.rearrange("b h w c -> (b h w) c")
         park = [out_rows[2 * P * n : 2 * P * (n + 1), D * (NH - 1) : D * NH] for n in range(NH)]
@@ -307,7 +302,7 @@ def tile_relativepositionmultiheadattention_pa_kernel(tc, q, k, x, w_v, rel_w, r
                 if kind(i) == MATMUL:
                     nc.tensor.matmul(
                         out=s_ps[:],
-                        lhsT=tiles["turned", i][:],
+                        lhsT=turned[:, i - MATMULS[0], :],
                         rhs=spread[:, HALF * h : HALF * (h + 1)],
                         start=False,
                         stop=True,
@@ -411,10 +406,11 @@ def tile_relativepositionmultiheadattention_pa_kernel(tc, q, k, x, w_v, rel_w, r
         def turn_e(i, paced=False):
             e_ps = psum_t.tile([P, NT // 2, P], F32, tag="turned")
             if paced:
-                nc.tensor.matmul_mx(
+                for again in range(2):
+                  nc.tensor.matmul_mx(
                     out=e_ps[:].rearrange("p b m -> p (b m)"),
-                    lhsT=x_codes[:, 0:P].bitcast(FP8X4),
-                    lhsT_scale=x_scales[:, 0:P],
+                    lhsT=w_codes[:, 0:P].bitcast(FP8X4),
+                    lhsT_scale=w_scales[:, 0:P],
                     rhs=w_codes[:].bitcast(FP8X4),
                     rhs_scale=w_scales[:],
                     start=True,
@@ -547,27 +543,28 @@ def tile_relativepositionmultiheadattention_pa_kernel(tc, q, k, x, w_v, rel_w, r
                 return 0
             return k // 4 + 1 if k % 4 == 0 and 0 < k // 4 + 1 < NH else None
 
-        def matmul_tile(p):
-            return biased(p) if 0 <= p < PAIRS and kind(biased(p)) == MATMUL else None
-
         def start_pieces(k):
-            for piece, role in zip(pieces.get(k, []), ("turned", "out")):
-                start_piece(*piece, role)
+            for piece in pieces.get(k, []):
+                start_piece(*piece, "out" if piece in last_piece(k) else "turned")
             if head_at(k) is not None:
                 turn_head_bias(head_at(k))
-            if matmul_tile(k + 3) is not None:
-                turn_bias(matmul_tile(k + 3))
 
         def take_pieces(k):
-            if matmul_tile(k + 3) is not None:
-                take_bias(matmul_tile(k + 3))
             for piece in pieces.get(k, []):
+                if piece not in last_piece(k):
+                    take_piece(*piece)
+
+        def last_piece(k):
+            return pieces.get(k, [])[-1:] if k < 7 else []
+
+        def take_last_piece(k):
+            for piece in last_piece(k):
                 take_piece(*piece)
 
         def finish_pieces(k):
-            if k == 1:
+            if k == -1:
                 group_w()
-            if k == 2:
+            if k == 0:
                 quantise_w()
             if head_at(k) is not None:
                 take_head_bias(head_at(k))
@@ -592,12 +589,11 @@ def tile_relativepositionmultiheadattention_pa_kernel(tc, q, k, x, w_v, rel_w, r
         take_rows(0, kT)
         turn_rows(0, q_sb, "turned")
         take_rows(0, qT)
+        turn_matmul_bias()
         for k in range(-5, PAIRS + 3):
             if 0 < k + 5 < NH:
                 load_head(k + 5)
             on(k + 1, build_pos, plain)
-            if matmul_tile(k + 4) is not None:
-                split_bias(matmul_tile(k + 4))
             on(k, join_max, biased)
             on(k + 1, scores, plain, 0)
             on(k + 1, scores, plain, 1)
@@ -617,12 +613,11 @@ def tile_relativepositionmultiheadattention_pa_kernel(tc, q, k, x, w_v, rel_w, r
             on(k + 1, add_bias, plain, 0)
             on(k, turn_e, biased)
             on(k + 1, add_bias, plain, 1)
-            on(k, turn_e, plain, k >= 5)
+            on(k, turn_e, plain, 0 <= k < PAIRS - 1)
             on(k, group_e, biased)
+            take_last_piece(k)
             normalise(k)
             on(k + 1, half_max, biased, 1)
             on(k + 2, scores, biased, 0)
             on(k, group_e, plain)
             on(k, add_sums, biased, plain)
-            if matmul_tile(k + 4) is not None:
-                low_half(matmul_tile(k + 4))

@@ -607,16 +607,16 @@ def tile_relativepositionmultiheadattention_pa_kernel(tc, q, k, x, w_v, rel_w, r
             on(k + 1, scores, biased, 1)
             take_pieces(k)
             on(k, exponent, plain)
+            normalise(k)
             on(k - 1, quantise_e, biased)
             on(k - 1, quantise_e, plain)
             finish_pieces(k)
             on(k + 1, add_bias, plain, 0)
             on(k, turn_e, biased)
             on(k + 1, add_bias, plain, 1)
-            on(k, turn_e, plain, 0 <= k < PAIRS - 1)
+            on(k, turn_e, plain)
             on(k, group_e, biased)
             take_last_piece(k)
-            normalise(k)
             on(k + 1, half_max, biased, 1)
             on(k + 2, scores, biased, 0)
             on(k, group_e, plain)

@@ -24,17 +24,16 @@ NG = L // (P * PACK)
 HALF = 512
 REL = 2 * GRID - 1
 ROWS = P // GRID
+BANK_ROWS = HALF // GRID
+COLS = P // BANK_ROWS
 SCALE = 1.0 / (D ** 0.5)
 ROOT = D ** 0.5
 
 FLOPS = 2 * L * C * C + 2 * 2 * NH * L * L * D
 TILES = NH * NT
-COLS = P // (HALF // GRID)
-VECTOR, MATMUL, TURN = range(3)
-VECTORS = 4
-TURNS = 4
-MATMULS = (4, 5, 6, 7)
-PAIRS = TILES // 2
+PER_HEAD = NT // 2
+PAIRS = NH * PER_HEAD
+FIRST_WEIGH = 7
 
 
 def tile_relativepositionmultiheadattention_pa_kernel(tc, q, k, x, w_v, rel_w, rel_h, out):
@@ -42,15 +41,14 @@ def tile_relativepositionmultiheadattention_pa_kernel(tc, q, k, x, w_v, rel_w, r
     with ExitStack() as ctx:
         ctx.enter_context(tc.manual_schedule())
         keep = ctx.enter_context(tc.tile_pool(name="keep", bufs=1))
-        bias = ctx.enter_context(tc.tile_pool(name="bias", bufs=4))
         work = ctx.enter_context(tc.tile_pool(name="work", bufs=4))
         late = ctx.enter_context(tc.tile_pool(name="late", bufs=18))
-        psum_s = ctx.enter_context(tc.psum_pool(name="psum_s", bufs=2))
-        psum_t = ctx.enter_context(tc.psum_pool(name="psum_t", bufs=2))
+        psum = ctx.enter_context(tc.psum_pool(name="psum", bufs=1))
 
-        def bank(role, shape, dtype):
-            return psum_t.tile(shape, dtype, name=role, tag=role, bufs=2 if role == "turned" else 1)
+        banks = {"biased": 3, "plain": 2, "turned": 2, "out": 1}
 
+        def bank(use, shape, dtype):
+            return psum.tile(shape, dtype, name=use, tag=use, bufs=banks[use])
 
         ident_bf = keep.tile([P, P], BF16)
         make_identity(nc, ident_bf[:])
@@ -71,13 +69,11 @@ def tile_relativepositionmultiheadattention_pa_kernel(tc, q, k, x, w_v, rel_w, r
             in1=wrap[:, GRID : 2 * GRID].unsqueeze(2).to_broadcast([P, GRID, GRID]),
             op=ALU.add,
         )
-
         row_sums = keep.tile([P, TILES, 2], F32)
         nc.gpsimd.memset(row_sums[:], 0.0)
 
-        bias_in = keep.tile([P, TILES, 2, GRID], BF16)
-        col_bias = bias_in[:, :, 0, :]
-        row_bias = bias_in[:, :, 1, :]
+        col_bias = keep.tile([P, TILES, GRID], BF16)
+        row_bias = keep.tile([P, TILES, GRID], BF16)
         skew = REL - 1
         rw = rel_w.rearrange("b n r c m -> (b n r) (c m)")[:, GRID - 1 : GRID - 1 + skew * GRID]
         rw = rw.rearrange("a (c j) -> a c j", j=skew)[:, :, 0:GRID]
@@ -86,19 +82,17 @@ def tile_relativepositionmultiheadattention_pa_kernel(tc, q, k, x, w_v, rel_w, r
         rh = rh.rearrange("a (r j) -> a r j", j=skew)[:, :, 0:GRID]
         rh = rh.rearrange("(n c) (t rl) j -> n rl c t j", c=GRID, rl=ROWS)
 
-        def load_cols(queue, n):
-            of_head = slice(NT * n, NT * (n + 1))
+        def load_cols(queue, first, last):
             for rl in range(ROWS):
                 rows = slice(GRID * rl, GRID * (rl + 1))
-                queue.dma_start(out=col_bias[rows, of_head, :], in_=rw[rl][:, of_head, :])
+                queue.dma_start(out=col_bias[rows, first:last, :], in_=rw[rl][:, first:last, :])
 
-        def load_rows(queue, n):
-            of_head = slice(NT * n, NT * (n + 1))
+        def load_rows(n):
             for rl in range(ROWS):
                 rows = slice(GRID * rl, GRID * (rl + 1))
-                queue.dma_start(out=row_bias[rows, of_head, :], in_=rh[n, rl])
+                nc.sync.dma_start(out=row_bias[rows, NT * n : NT * (n + 1), :], in_=rh[n, rl])
 
-        load_cols(nc.scalar, 0)
+        load_cols(nc.scalar, 0, NT)
         q_rows = q.rearrange("b n (t p) d -> (b n) p t d", p=P)
         k_rows = k.rearrange("b n (t p) d -> (b n) p t d", p=P)
         q_sb = []
@@ -106,39 +100,43 @@ def tile_relativepositionmultiheadattention_pa_kernel(tc, q, k, x, w_v, rel_w, r
         for n in range(NH):
             k_sb.append(keep.tile([P, NT, D], BF16, name="k_sb%d" % n))
             q_sb.append(keep.tile([P, NT, D], BF16, name="q_sb%d" % n))
+
+        def load_head(n):
+            nc.sync.dma_start(out=k_sb[n][:], in_=k_rows[n])
+            nc.sync.dma_start(out=q_sb[n][:], in_=q_rows[n])
+            load_rows(n)
+
+        load_head(0)
         w_sb = keep.tile([P, PACK, C], BF16)
-        x_sb = keep.tile([P, NT * C], BF16)
-        x_in = x_sb[:].rearrange("p (u k) -> p u k", k=2 * C)
-        x_rows = x.rearrange("b h w c -> (b h w) c").rearrange("(u p e) c -> p u (e c)", p=P, e=2)
-        nc.sync.dma_start(out=k_sb[0][:], in_=k_rows[0])
-        nc.sync.dma_start(out=q_sb[0][:], in_=q_rows[0])
-        load_rows(nc.sync, 0)
         nc.sync.dma_start(
             out=w_sb[:].rearrange("p (u e) c -> p u (e c)", e=2),
             in_=w_v.rearrange("(u p e) c -> p u (e c)", u=2, e=2),
         )
+        x_sb = keep.tile([P, NT * C], BF16)
+        x_in = x_sb[:].rearrange("p (u k) -> p u k", k=2 * C)
+        x_rows = x.rearrange("b h w c -> (b h w) c").rearrange("(u p e) c -> p u (e c)", p=P, e=2)
         for half in range(2):
             nc.sync.dma_start(out=x_in[:, 2 * half : 2 * half + 2, :], in_=x_rows[:, 2 * half : 2 * half + 2, :])
-        def load_head(n):
-            nc.sync.dma_start(out=k_sb[n][:], in_=k_rows[n])
-            nc.sync.dma_start(out=q_sb[n][:], in_=q_rows[n])
-            load_cols(nc.sync, n)
-            load_rows(nc.sync, n)
+        load_head(1)
+        load_cols(nc.sync, NT, TILES)
+        load_head(2)
+        load_head(3)
+
+        tiles = {}
 
         qT = keep.tile([P, NH, L], BF16)
         kT = keep.tile([P, NH, L], BF16)
 
-        def turn_rows(n, rows_sb, role):
-            r_ps = bank(role, [P, NT, P], BF16)
+        def turn_rows(what, n, use):
+            rows_sb = (k_sb if what == "k" else q_sb)[n]
+            turned = bank(use, [P, NT, P], BF16)
             for t in range(NT):
-                nc.tensor.transpose(out=r_ps[:, t, :], in_=rows_sb[n][:, t, :], identity=ident_bf[:])
-            tiles["r_ps", n, rows_sb is k_sb] = r_ps
+                nc.tensor.transpose(out=turned[:, t, :], in_=rows_sb[:, t, :], identity=ident_bf[:])
+            tiles[what, n] = turned
 
-        def take_rows(n, turned):
-            r_ps = tiles["r_ps", n, turned is kT]
-            nc.scalar.copy(out=turned[:, n, :], in_=r_ps[:].rearrange("p t l -> p (t l)"))
-
-        tiles = {}
+        def take_rows(what, n):
+            target = kT if what == "k" else qT
+            nc.scalar.copy(out=target[:, n, :], in_=tiles[what, n][:].rearrange("p t l -> p (t l)"))
 
         x_codes = keep.tile([P, L], U32, align_bytes=64)
         x_scales = keep.tile([P, L], U8, align_bytes=64)
@@ -148,31 +146,42 @@ def tile_relativepositionmultiheadattention_pa_kernel(tc, q, k, x, w_v, rel_w, r
         v_scales = keep.tile([P, NG, NH, D], U8, align_bytes=64)
         x_grouped = keep.tile([P, L * PACK], BF16, align_bytes=64)
         w_grouped = keep.tile([P, C, PACK], BF16, align_bytes=64)
+        v_grouped = keep.tile([P, NH, NG, D, PACK], BF16, align_bytes=64)
 
-        def turn_x(b, role):
+        def group_w():
+            nc.gpsimd.tensor_scalar(
+                out=w_grouped[:],
+                in0=w_sb[:].rearrange("p t c -> p c t"),
+                scalar1=1.0,
+                scalar2=0.0,
+                op0=ALU.mult,
+                op1=ALU.add,
+            )
+
+        def quantise_w():
+            nc.vector.quantize_mx(
+                out=w_codes[:].bitcast(FP8X4), scales=w_scales[:], in_=w_grouped[:].rearrange("p c t -> p (c t)")
+            )
+
+        def turn_x(b, use):
             x_words = x_sb[:].bitcast(F32)
-            x_ps = bank(role, [P, 2, 2, P], F32)
+            turned = bank(use, [P, 2, 2, P], F32)
             for tt in range(2):
                 for u in range(2):
                     first = (C // 2) * (2 * b + tt) + P * u
                     nc.tensor.transpose(
-                        out=x_ps[:, tt, u, :], in_=x_words[:, first : first + P], identity=ident_f32[:]
+                        out=turned[:, tt, u, :], in_=x_words[:, first : first + P], identity=ident_f32[:]
                     )
-            tiles["x_ps", b] = x_ps
+            tiles["x", b] = turned
 
         def take_x(b):
-            x_grouped_words = x_grouped[:].bitcast(F32).rearrange("p (l u) -> p l u", u=2)
-            x_ps = tiles["x_ps", b]
-            grouped = x_grouped_words[:, 2 * P * b : 2 * P * (b + 1), :].rearrange("p (t l) u -> p t l u", t=2)
+            grouped_words = x_grouped[:].bitcast(F32).rearrange("p (l u) -> p l u", u=2)
+            grouped = grouped_words[:, 2 * P * b : 2 * P * (b + 1), :].rearrange("p (t l) u -> p t l u", t=2)
+            words = tiles["x", b][:].rearrange("p t u l -> p t l u")
             if b % 2 == 0:
-                nc.vector.tensor_copy(out=grouped, in_=x_ps[:].rearrange("p t u l -> p t l u"))
+                nc.vector.tensor_copy(out=grouped, in_=words)
             else:
-                nc.scalar.copy(out=grouped, in_=x_ps[:].rearrange("p t u l -> p t l u"))
-
-        def group_w():
-            nc.gpsimd.tensor_scalar(
-                out=w_grouped[:], in0=w_sb[:].rearrange("p t c -> p c t"), scalar1=1.0, scalar2=0.0, op0=ALU.mult, op1=ALU.add
-            )
+                nc.scalar.copy(out=grouped, in_=words)
 
         def quantise_x(half):
             cols = slice(HALF * half, HALF * (half + 1))
@@ -182,15 +191,8 @@ def tile_relativepositionmultiheadattention_pa_kernel(tc, q, k, x, w_v, rel_w, r
                 in_=x_grouped[:, PACK * HALF * half : PACK * HALF * (half + 1)],
             )
 
-        def quantise_w():
-            nc.vector.quantize_mx(
-                out=w_codes[:].bitcast(FP8X4), scales=w_scales[:], in_=w_grouped[:].rearrange("p c t -> p (c t)")
-            )
-
-        v_grouped = keep.tile([P, NH, NG, D, PACK], BF16, align_bytes=64)
-
-        def project_values(n, g, role):
-            v_ps = bank(role, [P, PACK, D], F32)
+        def project_values(n, g, use):
+            v_ps = bank(use, [P, PACK, D], F32)
             for j in range(PACK):
                 rows = slice(P * (PACK * g + j), P * (PACK * g + j + 1))
                 cols = slice(D * n, D * (n + 1))
@@ -203,11 +205,11 @@ def tile_relativepositionmultiheadattention_pa_kernel(tc, q, k, x, w_v, rel_w, r
                     start=True,
                     stop=True,
                 )
-            tiles["v_ps", n, g] = v_ps
+            tiles["v", n, g] = v_ps
 
         def take_values(n, g):
             grouped = v_grouped[:, n, g, :, :]
-            by_keys = tiles["v_ps", n, g][:].rearrange("p j d -> p d j")
+            by_keys = tiles["v", n, g][:].rearrange("p j d -> p d j")
             if g == 0:
                 nc.scalar.copy(out=grouped, in_=by_keys)
             else:
@@ -220,14 +222,61 @@ def tile_relativepositionmultiheadattention_pa_kernel(tc, q, k, x, w_v, rel_w, r
                 in_=v_grouped[:, n, g, :, :].rearrange("p d j -> p (d j)"),
             )
 
+        halves = keep.tile([P, PER_HEAD, 2, 2, GRID], BF16)
+        head0_bias = keep.tile([P, PER_HEAD, P], BF16)
 
-        def kind(i):
-            if i % NT < VECTORS:
-                return VECTOR
-            return MATMUL if i in MATMULS else TURN
+        def split_head0_bias():
+            for kind, rel in enumerate((col_bias, row_bias)):
+                rel = rel[:, PER_HEAD:NT, :]
+                high = halves[:, :, 0, kind, :]
+                nc.gpsimd.tensor_scalar(out=high, in0=rel, scalar1=ROOT, scalar2=0.0, op0=ALU.mult, op1=ALU.add)
+                nc.vector.scalar_tensor_tensor(
+                    out=halves[:, :, 1, kind, :], in0=rel, scalar=ROOT, in1=high, op0=ALU.mult, op1=ALU.subtract
+                )
+            turned = bank("out", [P, PER_HEAD, P], BF16)
+            for t in range(PER_HEAD):
+                flat = halves[:, t, :, :, :].rearrange("p h k j -> p (h k j)")
+                nc.tensor.transpose(out=turned[:, t, :], in_=flat, identity=ident_bf[:])
+            nc.scalar.copy(out=head0_bias[:], in_=turned[:])
+
+        out_rows = out.rearrange("b h w c -> (b h w) c")
+        park = [out_rows[2 * P * n : 2 * P * (n + 1), D * (NH - 1) : D * NH] for n in range(NH)]
+
+        def turn_bias(n):
+            turned = bank("turned", [P, 2, P], BF16)
+            for kind, rel in enumerate((col_bias, row_bias)):
+                flat = rel[:, NT * n + PER_HEAD : NT * (n + 1), :].rearrange("p t j -> p (t j)")
+                nc.tensor.transpose(out=turned[:, kind, :], in_=flat, identity=ident_bf[:])
+            tiles["turned_bias", n] = turned
+
+        def take_bias(n):
+            tall = keep.tile([P, 2, P], F32, name="tall%d" % n)
+            nc.vector.tensor_scalar(
+                out=tall[:], in0=tiles["turned_bias", n][:], scalar1=ROOT, scalar2=0.0, op0=ALU.mult, op1=ALU.add
+            )
+            nc.sync.dma_start(out=park[n].rearrange("(k p) q -> p k q", p=P), in_=tall[:])
+            wide_cols = keep.tile([P, PER_HEAD, P], F32, name="wide_cols%d" % n)
+            for rl in range(ROWS):
+                nc.sync.dma_start(
+                    out=wide_cols[GRID * rl : GRID * (rl + 1), :, :],
+                    in_=park[n][0:P, :].rearrange("(t j) q -> j t q", j=GRID),
+                )
+            wide_rows = keep.tile([P, PER_HEAD, 2, P], F32, name="wide_rows%d" % n)
+            for g in range(COLS):
+                nc.sync.dma_start(
+                    out=wide_rows[BANK_ROWS * g : BANK_ROWS * (g + 1), :, :, :].rearrange("r t h q -> r (t h) q"),
+                    in_=park[n][P : 2 * P, :].rearrange("(th r) q -> r th q", r=BANK_ROWS),
+                )
+            tiles["wide", n] = (wide_cols, wide_rows)
+
+        def biased(p):
+            return NT * (p // PER_HEAD) + PER_HEAD + p % PER_HEAD
+
+        def plain(p):
+            return NT * (p // PER_HEAD) + p % PER_HEAD
 
         def build_pos(i):
-            pos = bias.tile([P, L], F32)
+            pos = work.tile([P, L], F32)
             part = GRID // 4
             for r in range(0, GRID, part):
                 nc.gpsimd.tensor_tensor(
@@ -238,122 +287,70 @@ def tile_relativepositionmultiheadattention_pa_kernel(tc, q, k, x, w_v, rel_w, r
                 )
             tiles["pos", i] = pos
 
-        halves = keep.tile([P, VECTORS, 2, 2 * GRID], BF16)
-        turned = keep.tile([P, VECTORS, P], BF16)
-
-        def turn_matmul_bias():
-            first = MATMULS[0]
-            rel = bias_in[:, first : first + VECTORS, :, :].rearrange("p t k j -> p t (k j)")
-            high = halves[:, :, 0, :]
-            nc.gpsimd.tensor_scalar(out=high, in0=rel, scalar1=ROOT, scalar2=0.0, op0=ALU.mult, op1=ALU.add)
-            nc.vector.scalar_tensor_tensor(
-                out=halves[:, :, 1, :], in0=rel, scalar=ROOT, in1=high, op0=ALU.mult, op1=ALU.subtract
-            )
-            b_ps = bank("out", [P, VECTORS, P], BF16)
-            for s in range(VECTORS):
-                flat = halves[:, s, :, :].rearrange("p h j -> p (h j)")
-                nc.tensor.transpose(out=b_ps[:, s, :], in_=flat, identity=ident_bf[:])
-            nc.scalar.copy(out=turned[:], in_=b_ps[:])
-
-        out_rows = out.rearrange("b h w c -> (b h w) c")
-        park = [out_rows[2 * P * n : 2 * P * (n + 1), D * (NH - 1) : D * NH] for n in range(NH)]
-
-        def turn_head_bias(n):
-            b_ps = bank("turned", [P, 2, P], BF16)
-            for s in range(2):
-                first = NT * n + VECTORS + 2 * s
-                rel = bias_in[:, first : first + 2, :, :].rearrange("p t k j -> p (t k j)")
-                nc.tensor.transpose(out=b_ps[:, s, :], in_=rel, identity=ident_bf[:])
-            tiles["head_bias", n] = b_ps
-
-        def take_head_bias(n):
-            tall = keep.tile([P, 2, P], F32, name="tall%d" % n)
-            nc.vector.tensor_scalar(
-                out=tall[:], in0=tiles["head_bias", n][:], scalar1=ROOT, scalar2=0.0, op0=ALU.mult, op1=ALU.add
-            )
-            nc.sync.dma_start(out=park[n].rearrange("(s p) q -> p s q", p=P), in_=tall[:])
-            wide = keep.tile([P, 3, TURNS, P], F32, name="wide%d" % n)
-            by_kind = park[n].rearrange("(t k j) q -> k j t q", t=NT - VECTORS, k=2)
-            for g in range(ROWS):
-                nc.sync.dma_start(out=wide[GRID * g : GRID * (g + 1), 0, :, :], in_=by_kind[0])
-            half = HALF // GRID
-            for h in range(2):
-                for g in range(COLS):
-                    nc.sync.dma_start(
-                        out=wide[half * g : half * (g + 1), 1 + h, :, :], in_=by_kind[1, half * h : half * (h + 1)]
-                    )
-            tiles["wide", n] = wide
-
         def scores(i, h):
             n = i // NT
             t = i % NT
-            if True:
-                if kind(i) == VECTOR:
-                    s_ps = psum_s.tile([P, HALF], F32, tag="logits", bufs=2)
-                else:
-                    s_ps = psum_s.tile([P, HALF], F32, tag="biased", bufs=3)
+            s_ps = bank("plain" if t < PER_HEAD else "biased", [P, HALF], F32)
+            tiles["s_ps", i, h] = s_ps
+            nc.tensor.matmul(
+                out=s_ps[:],
+                lhsT=qT[:, n, P * t : P * (t + 1)],
+                rhs=kT[:, n, HALF * h : HALF * (h + 1)],
+                start=True,
+                stop=t < PER_HEAD,
+            )
+            if t < PER_HEAD:
+                return
+            t -= PER_HEAD
+            if n == 0:
                 nc.tensor.matmul(
                     out=s_ps[:],
-                    lhsT=qT[:, n, P * t : P * (t + 1)],
-                    rhs=kT[:, n, HALF * h : HALF * (h + 1)],
-                    start=True,
-                    stop=kind(i) == VECTOR,
+                    lhsT=head0_bias[:, t, :],
+                    rhs=spread[:, HALF * h : HALF * (h + 1)],
+                    start=False,
+                    stop=True,
                 )
-                if kind(i) == MATMUL:
-                    nc.tensor.matmul(
-                        out=s_ps[:],
-                        lhsT=turned[:, i - MATMULS[0], :],
-                        rhs=spread[:, HALF * h : HALF * (h + 1)],
-                        start=False,
-                        stop=True,
-                    )
-                if kind(i) == TURN:
-                    wide = tiles["wide", n]
-                    te = t - VECTORS
-                    for b in range(HALF // P):
-                        nc.tensor.matmul(
-                            out=s_ps[:, P * b : P * (b + 1)],
-                            lhsT=wide[:, 0, te, :],
-                            rhs=ident_f32[:],
-                            start=False,
-                            stop=False,
-                            is_transpose=True,
-                        )
-                    by_cols = s_ps[:].rearrange("p (a b c) -> p b a c", b=HALF // P, c=COLS)
-                    for b in range(HALF // P):
-                        nc.tensor.matmul(
-                            out=by_cols[:, b, :, :],
-                            lhsT=wide[:, 1 + h, te, :],
-                            rhs=swap[:],
-                            start=False,
-                            stop=b == HALF // P - 1,
-                            is_transpose=True,
-                        )
-                tiles["s_ps", i, h] = s_ps
+                return
+            wide_cols, wide_rows = tiles["wide", n]
+            blocks = HALF // P
+            for b in range(blocks):
+                nc.tensor.matmul(
+                    out=s_ps[:, P * b : P * (b + 1)],
+                    lhsT=wide_cols[:, t, :],
+                    rhs=ident_f32[:],
+                    start=False,
+                    stop=False,
+                    is_transpose=True,
+                )
+            by_cols = s_ps[:].rearrange("p (r b g) -> p b r g", b=blocks, g=COLS)
+            for b in range(blocks):
+                nc.tensor.matmul(
+                    out=by_cols[:, b, :, :],
+                    lhsT=wide_rows[:, t, h, :],
+                    rhs=swap[:],
+                    start=False,
+                    stop=b == blocks - 1,
+                    is_transpose=True,
+                )
 
         def add_bias(i, h):
-            if kind(i) != VECTOR:
-                return
             if h == 0:
                 s = work.tile([P, L], F32)
                 tiles["s", i] = s
-            s = tiles["s", i]
-            if True:
-                cols = slice(HALF * h, HALF * (h + 1))
-                nc.vector.scalar_tensor_tensor(
-                    out=s[:, cols],
-                    in0=tiles["s_ps", i, h][:],
-                    scalar=SCALE,
-                    in1=tiles["pos", i][:, cols],
-                    op0=ALU.mult,
-                    op1=ALU.add,
-                )
+            cols = slice(HALF * h, HALF * (h + 1))
+            nc.vector.scalar_tensor_tensor(
+                out=tiles["s", i][:, cols],
+                in0=tiles["s_ps", i, h][:],
+                scalar=SCALE,
+                in1=tiles["pos", i][:, cols],
+                op0=ALU.mult,
+                op1=ALU.add,
+            )
 
-        def row_max(i):
-            if kind(i) == VECTOR:
-                neg_max = late.tile([P, 1], F32)
-                nc.vector.tensor_reduce(out=neg_max[:], in_=tiles["s", i][:], axis=AX.X, op=ALU.max, negate=True)
-                tiles["neg_max", i] = neg_max
+        def plain_max(i):
+            neg_max = late.tile([P, 1], F32)
+            nc.vector.tensor_reduce(out=neg_max[:], in_=tiles["s", i][:], axis=AX.X, op=ALU.max, negate=True)
+            tiles["neg_max", i] = neg_max
 
         def half_max(i, h):
             if h == 0:
@@ -363,72 +360,57 @@ def tile_relativepositionmultiheadattention_pa_kernel(tc, q, k, x, w_v, rel_w, r
                 out=tiles["neg_maxes", i][:, h : h + 1], in_=tiles["s_ps", i, h][:], axis=AX.X, op=ALU.max, negate=True
             )
 
-        def join_max(i):
-            if kind(i) != VECTOR:
-                neg_max = late.tile([P, 1], F32)
-                neg_maxes = tiles["neg_maxes", i]
-                nc.vector.tensor_scalar(
-                    out=neg_max[:],
-                    in0=neg_maxes[:, 0:1],
-                    scalar1=neg_maxes[:, 1:2],
-                    scalar2=SCALE,
-                    op0=ALU.min,
-                    op1=ALU.mult,
-                )
-                tiles["neg_max", i] = neg_max
+        def biased_max(i):
+            neg_max = late.tile([P, 1], F32)
+            neg_maxes = tiles["neg_maxes", i]
+            nc.vector.tensor_scalar(
+                out=neg_max[:],
+                in0=neg_maxes[:, 0:1],
+                scalar1=neg_maxes[:, 1:2],
+                scalar2=SCALE,
+                op0=ALU.min,
+                op1=ALU.mult,
+            )
+            tiles["neg_max", i] = neg_max
 
-        def exponent(i, h=0):
+        def plain_exp(i):
+            e = work.tile([P, L], BF16)
+            nc.scalar.activation(
+                out=e[:],
+                in_=tiles["s", i][:],
+                func=ACT.Exp,
+                bias=tiles["neg_max", i][:, 0:1],
+                scale=1.0,
+                accum_out=row_sums[:, i, 0:1],
+            )
+            tiles["e", i] = e
+
+        def half_exp(i, h):
             if h == 0:
                 e = work.tile([P, L], BF16)
                 tiles["e", i] = e
-            e = tiles["e", i]
-            row_sum = row_sums[:, i, :]
-            if kind(i) == VECTOR:
-                nc.scalar.activation(
-                    out=e[:],
-                    in_=tiles["s", i][:],
-                    func=ACT.Exp,
-                    bias=tiles["neg_max", i][:, 0:1],
-                    scale=1.0,
-                    accum_out=row_sum[:, 0:1],
-                )
-            else:
-                if True:
-                    nc.scalar.activation(
-                        out=e[:, HALF * h : HALF * (h + 1)],
-                        in_=tiles["s_ps", i, h][:],
-                        func=ACT.Exp,
-                        bias=tiles["neg_max", i][:, 0:1],
-                        scale=SCALE,
-                        accum_out=row_sum[:, h : h + 1],
-                    )
+            nc.scalar.activation(
+                out=tiles["e", i][:, HALF * h : HALF * (h + 1)],
+                in_=tiles["s_ps", i, h][:],
+                func=ACT.Exp,
+                bias=tiles["neg_max", i][:, 0:1],
+                scale=SCALE,
+                accum_out=row_sums[:, i, h : h + 1],
+            )
 
-        def turn_e(i, paced=False):
-            e_ps = psum_t.tile([P, NT // 2, P], F32, tag="turned")
-            if paced:
-                for again in range(2):
-                  nc.tensor.matmul_mx(
-                    out=e_ps[:].rearrange("p b m -> p (b m)"),
-                    lhsT=w_codes[:, 0:P].bitcast(FP8X4),
-                    lhsT_scale=w_scales[:, 0:P],
-                    rhs=w_codes[:].bitcast(FP8X4),
-                    rhs_scale=w_scales[:],
-                    start=True,
-                    stop=True,
-                )
+        def turn_e(i):
+            turned = bank("turned", [P, NT // 2, P], F32)
             e_words = tiles["e", i][:].bitcast(F32)
             for b in range(NT // 2):
-                nc.tensor.transpose(
-                    out=e_ps[:, b, :], in_=e_words[:, P * b : P * (b + 1)], identity=ident_f32[:]
-                )
-            tiles["e_ps", i] = e_ps
+                nc.tensor.transpose(out=turned[:, b, :], in_=e_words[:, P * b : P * (b + 1)], identity=ident_f32[:])
+            tiles["turned_e", i] = turned
 
         def group_e(i):
             e_grouped = work.tile([P, NG, P, PACK], BF16, align_bytes=64)
             grouped_words = e_grouped[:].rearrange("p g m j -> p (g m j)").bitcast(F32)
             nc.scalar.copy(
                 out=grouped_words.rearrange("p (g m u) -> p g m u", g=NG, u=2),
-                in_=tiles["e_ps", i][:].rearrange("p (g u) m -> p g m u", g=NG),
+                in_=tiles["turned_e", i][:].rearrange("p (g u) m -> p g m u", g=NG),
             )
             tiles["e_grouped", i] = e_grouped
 
@@ -440,184 +422,157 @@ def tile_relativepositionmultiheadattention_pa_kernel(tc, q, k, x, w_v, rel_w, r
                 scales=e_scales[:].rearrange("p g m -> p (g m)"),
                 in_=tiles["e_grouped", i][:].rearrange("p g m j -> p (g m j)"),
             )
-            tiles["e_codes", i] = e_codes
-            tiles["e_scales", i] = e_scales
+            tiles["e_codes", i] = (e_codes, e_scales)
 
         def weigh_values(i, o_ps):
             n = i // NT
+            e_codes, e_scales = tiles["e_codes", i]
             for g in range(NG):
                 nc.tensor.matmul_mx(
                     out=o_ps,
-                    lhsT=tiles["e_codes", i][:, g, :].bitcast(FP8X4),
-                    lhsT_scale=tiles["e_scales", i][:, g, :],
+                    lhsT=e_codes[:, g, :].bitcast(FP8X4),
+                    lhsT_scale=e_scales[:, g, :],
                     rhs=v_codes[:, g, n, :].bitcast(FP8X4),
                     rhs_scale=v_scales[:, g, n, :],
                     start=(g == 0),
                     stop=(g == NG - 1),
                 )
-            tiles["o_ps", i] = o_ps
 
-        def add_sums(i, j):
-            total = late.tile([P, 2, 1], F32)
-            lo = min(i, j)
-            step = abs(i - j)
-            nc.vector.tensor_reduce(
-                out=total[:, :, 0], in_=row_sums[:, lo : lo + step + 1 : step, :], axis=AX.X, op=ALU.add
-            )
-            tiles["total", i] = total
+        def both(p):
+            return slice(plain(p), biased(p) + 1, PER_HEAD)
 
-        def invert_sums(i, j):
+        def add_sums(p):
+            total = late.tile([P, 2], F32)
+            nc.vector.tensor_reduce(out=total[:], in_=row_sums[:, both(p), :], axis=AX.X, op=ALU.add)
+            tiles["total", p] = total
+
+        def invert_sums(p):
             inverse = late.tile([P, 2], F32)
-            nc.vector.reciprocal(out=inverse[:], in_=tiles["total", i][:, :, 0])
-            tiles["inv_sum", min(i, j)] = inverse[:, 0:1]
-            tiles["inv_sum", max(i, j)] = inverse[:, 1:2]
+            nc.vector.reciprocal(out=inverse[:], in_=tiles["total", p][:])
+            tiles["inverse", p] = inverse
 
-        def normalise_and_store(i):
-            n = i // NT
-            t = i % NT
-            o_sb = work.tile([P, D], F32)
-            nc.scalar.activation(
-                out=o_sb[:], in_=tiles["o_ps", i], func=ACT.Copy, scale=tiles["inv_sum", i]
-            )
-            nc.sync.dma_start(out=out_rows[P * t : P * (t + 1), D * n : D * (n + 1)], in_=o_sb[:])
+        paired_rows = out_rows.rearrange("(s t p) c -> t p s c", s=2, p=P)
 
-
-        def biased(p):
-            return NT * (p // VECTORS) + VECTORS + p % VECTORS
-
-        def plain(p):
-            return NT * (p // VECTORS) + p % VECTORS
+        def normalise_and_store(p, o_ps):
+            n = p // PER_HEAD
+            o_sb = work.tile([P, 2, D], F32)
+            for s in range(2):
+                nc.scalar.activation(
+                    out=o_sb[:, s, :], in_=o_ps[:, s, :], func=ACT.Copy, scale=tiles["inverse", p][:, s : s + 1]
+                )
+            nc.sync.dma_start(out=paired_rows[p % PER_HEAD][:, :, D * n : D * (n + 1)], in_=o_sb[:])
 
         pieces = {
-            0: [("k", 1, 0)],
-            1: [("q", 1, 0)],
-            2: [("x", 0, 0), ("x", 1, 0)],
-            3: [("x", 2, 0), ("x", 3, 0)],
-            4: [("v", 0, 0), ("k", 2, 0)],
-            5: [("v", 0, 1), ("q", 2, 0)],
+            0: [("k", 1)],
+            1: [("q", 1)],
+            2: [("x", 0), ("x", 1)],
+            3: [("x", 2), ("x", 3)],
+            4: [("v", 0, 0), ("k", 2)],
+            5: [("v", 0, 1), ("q", 2)],
             6: [("v", 1, 0)],
             7: [("v", 1, 1)],
             8: [("v", 2, 0)],
-            9: [("k", 3, 0), ("v", 2, 1)],
-            10: [("q", 3, 0)],
+            9: [("k", 3), ("v", 2, 1)],
+            10: [("q", 3)],
             11: [("v", 3, 0)],
             12: [("v", 3, 1)],
         }
 
+        def start_piece(piece, use):
+            if piece[0] in ("k", "q"):
+                turn_rows(*piece, use)
+            elif piece[0] == "x":
+                turn_x(piece[1], use)
+            else:
+                project_values(*piece[1:], use)
+
+        def take_piece(piece):
+            if piece[0] in ("k", "q"):
+                take_rows(*piece)
+            elif piece[0] == "x":
+                take_x(piece[1])
+            else:
+                take_values(*piece[1:])
+
+        def finish_piece(piece):
+            if piece[0] == "v":
+                quantise_v(*piece[1:])
+            elif piece[0] == "x" and piece[1] % 2 == 1:
+                quantise_x(piece[1] // 2)
+
+        def split_pieces(k):
+            todo = pieces.get(k, [])
+            return (todo[:-1], todo[-1:]) if k < FIRST_WEIGH else (todo, [])
+
+        def bias_head(k):
+            return k // PER_HEAD + 1 if k % PER_HEAD == 0 and 0 <= k < PAIRS - PER_HEAD else None
+
         weigh_at = {}
-        pair = 0
-        for k in range(7, PAIRS + 3):
+        p = 0
+        for k in range(FIRST_WEIGH, PAIRS + 3):
             for step in range(2):
-                if pair <= min(k - 2, PAIRS - 1):
-                    weigh_at.setdefault(k, []).extend([biased(pair), plain(pair)])
-                    pair += 1
+                if p <= min(k - 2, PAIRS - 1):
+                    weigh_at.setdefault(k, []).append(p)
+                    p += 1
 
-        def start_piece(what, n, half, role):
-            if what == "k":
-                turn_rows(n, k_sb, role)
-            if what == "q":
-                turn_rows(n, q_sb, role)
-            if what == "v":
-                project_values(n, half, role)
-            if what == "x":
-                turn_x(n, role)
+        def weigh(k):
+            if k in weigh_at:
+                o_ps = bank("out", [P, 2, 2, D], F32)
+                for slot, p in enumerate(weigh_at[k]):
+                    weigh_values(plain(p), o_ps[:, slot, 0, :])
+                    weigh_values(biased(p), o_ps[:, slot, 1, :])
+                tiles["o_ps", k] = o_ps
 
-        def take_piece(what, n, half):
-            if what == "k":
-                take_rows(n, kT)
-            if what == "q":
-                take_rows(n, qT)
-            if what == "v":
-                take_values(n, half)
-            if what == "x":
-                take_x(n)
+        def on(p, stage, tile_of=None, *half):
+            if 0 <= p < PAIRS:
+                stage(p if tile_of is None else tile_of(p), *half)
 
-        def finish_piece(what, n, half):
-            if what == "v":
-                quantise_v(n, half)
-            if what == "x" and n % 2 == 1:
-                quantise_x(n // 2)
-
-        def head_at(k):
-            if k == -3:
-                return 0
-            return k // 4 + 1 if k % 4 == 0 and 0 < k // 4 + 1 < NH else None
-
-        def start_pieces(k):
-            for piece in pieces.get(k, []):
-                start_piece(*piece, "out" if piece in last_piece(k) else "turned")
-            if head_at(k) is not None:
-                turn_head_bias(head_at(k))
-
-        def take_pieces(k):
-            for piece in pieces.get(k, []):
-                if piece not in last_piece(k):
-                    take_piece(*piece)
-
-        def last_piece(k):
-            return pieces.get(k, [])[-1:] if k < 7 else []
-
-        def take_last_piece(k):
-            for piece in last_piece(k):
-                take_piece(*piece)
-
-        def finish_pieces(k):
+        for what in ("k", "q"):
+            turn_rows(what, 0, "turned")
+            take_rows(what, 0)
+        split_head0_bias()
+        for k in range(-2, PAIRS + 3):
+            early, last = split_pieces(k)
+            on(k + 1, build_pos, plain)
+            on(k - 1, invert_sums)
+            on(k, biased_max, biased)
+            on(k + 1, scores, plain, 0)
+            on(k + 1, scores, plain, 1)
+            on(k, plain_max, plain)
+            on(k, half_exp, biased, 0)
+            for piece in early:
+                start_piece(piece, "turned")
+            for piece in last:
+                start_piece(piece, "out")
+            if bias_head(k) is not None:
+                turn_bias(bias_head(k))
+            weigh(k)
+            on(k, half_exp, biased, 1)
+            on(k + 1, half_max, biased, 0)
+            on(k + 1, scores, biased, 1)
+            for piece in early:
+                take_piece(piece)
+            on(k, plain_exp, plain)
+            for slot, p in enumerate(weigh_at.get(k, [])):
+                normalise_and_store(p, tiles["o_ps", k][:, slot, :, :])
+            on(k - 1, quantise_e, biased)
+            on(k - 1, quantise_e, plain)
             if k == -1:
                 group_w()
             if k == 0:
                 quantise_w()
-            if head_at(k) is not None:
-                take_head_bias(head_at(k))
+            if bias_head(k) is not None:
+                take_bias(bias_head(k))
             for piece in pieces.get(k - 1, []):
-                finish_piece(*piece)
-
-        def weigh(k):
-            if k in weigh_at:
-                o_ps = bank("out", [P, 4, D], F32)
-                for slot, i in enumerate(weigh_at[k]):
-                    weigh_values(i, o_ps[:, slot, :])
-
-        def normalise(k):
-            for i in weigh_at.get(k, []):
-                normalise_and_store(i)
-
-        def on(p, stage, *args):
-            if 0 <= p < PAIRS:
-                stage(*[a(p) if a in (biased, plain) else a for a in args])
-
-        turn_rows(0, k_sb, "turned")
-        take_rows(0, kT)
-        turn_rows(0, q_sb, "turned")
-        take_rows(0, qT)
-        turn_matmul_bias()
-        for k in range(-5, PAIRS + 3):
-            if 0 < k + 5 < NH:
-                load_head(k + 5)
-            on(k + 1, build_pos, plain)
-            on(k, join_max, biased)
-            on(k + 1, scores, plain, 0)
-            on(k + 1, scores, plain, 1)
-            on(k, row_max, plain)
-            on(k, exponent, biased, 0)
-            start_pieces(k)
-            weigh(k)
-            on(k, exponent, biased, 1)
-            on(k - 1, invert_sums, biased, plain)
-            on(k + 1, half_max, biased, 0)
-            on(k + 1, scores, biased, 1)
-            take_pieces(k)
-            on(k, exponent, plain)
-            normalise(k)
-            on(k - 1, quantise_e, biased)
-            on(k - 1, quantise_e, plain)
-            finish_pieces(k)
+                finish_piece(piece)
             on(k + 1, add_bias, plain, 0)
             on(k, turn_e, biased)
             on(k + 1, add_bias, plain, 1)
             on(k, turn_e, plain)
             on(k, group_e, biased)
-            take_last_piece(k)
+            for piece in last:
+                take_piece(piece)
             on(k + 1, half_max, biased, 1)
             on(k + 2, scores, biased, 0)
             on(k, group_e, plain)
-            on(k, add_sums, biased, plain)
+            on(k, add_sums)

@@ -101,26 +101,35 @@ def tile_relativepositionmultiheadattention_pa_kernel(tc, q, k, x, w_v, rel_w, r
             k_sb.append(keep.tile([P, NT, D], BF16, name="k_sb%d" % n))
             q_sb.append(keep.tile([P, NT, D], BF16, name="q_sb%d" % n))
 
-        def load_head(n):
+        def load_k(n):
             nc.sync.dma_start(out=k_sb[n][:], in_=k_rows[n])
-            nc.sync.dma_start(out=q_sb[n][:], in_=q_rows[n])
-            load_rows(n)
 
-        load_head(0)
+        def load_q(n):
+            nc.sync.dma_start(out=q_sb[n][:], in_=q_rows[n])
+
+        load_k(0)
+        load_q(0)
+        load_rows(0)
+        load_k(1)
+        load_rows(1)
+        load_cols(nc.sync, NT, 2 * NT)
         w_sb = keep.tile([P, PACK, C], BF16)
         nc.sync.dma_start(
             out=w_sb[:].rearrange("p (u e) c -> p u (e c)", e=2),
             in_=w_v.rearrange("(u p e) c -> p u (e c)", u=2, e=2),
         )
+        load_q(1)
         x_sb = keep.tile([P, NT * C], BF16)
         x_in = x_sb[:].rearrange("p (u k) -> p u k", k=2 * C)
         x_rows = x.rearrange("b h w c -> (b h w) c").rearrange("(u p e) c -> p u (e c)", p=P, e=2)
         for half in range(2):
             nc.sync.dma_start(out=x_in[:, 2 * half : 2 * half + 2, :], in_=x_rows[:, 2 * half : 2 * half + 2, :])
-        load_head(1)
-        load_cols(nc.sync, NT, TILES)
-        load_head(2)
-        load_head(3)
+
+        def load_late_head(n):
+            load_cols(nc.sync, NT * n, NT * (n + 1))
+            load_rows(n)
+            load_k(n)
+            load_q(n)
 
         tiles = {}
 
@@ -178,10 +187,7 @@ def tile_relativepositionmultiheadattention_pa_kernel(tc, q, k, x, w_v, rel_w, r
             grouped_words = x_grouped[:].bitcast(F32).rearrange("p (l u) -> p l u", u=2)
             grouped = grouped_words[:, 2 * P * b : 2 * P * (b + 1), :].rearrange("p (t l) u -> p t l u", t=2)
             words = tiles["x", b][:].rearrange("p t u l -> p t l u")
-            if b % 2 == 0:
-                nc.vector.tensor_copy(out=grouped, in_=words)
-            else:
-                nc.scalar.copy(out=grouped, in_=words)
+            nc.scalar.copy(out=grouped, in_=words)
 
         def quantise_x(half):
             cols = slice(HALF * half, HALF * (half + 1))
@@ -210,10 +216,7 @@ def tile_relativepositionmultiheadattention_pa_kernel(tc, q, k, x, w_v, rel_w, r
         def take_values(n, g):
             grouped = v_grouped[:, n, g, :, :]
             by_keys = tiles["v", n, g][:].rearrange("p j d -> p d j")
-            if g == 0:
-                nc.scalar.copy(out=grouped, in_=by_keys)
-            else:
-                nc.vector.tensor_copy(out=grouped, in_=by_keys)
+            nc.scalar.copy(out=grouped, in_=by_keys)
 
         def quantise_v(n, g):
             nc.vector.quantize_mx(
@@ -276,7 +279,7 @@ def tile_relativepositionmultiheadattention_pa_kernel(tc, q, k, x, w_v, rel_w, r
             return NT * (p // PER_HEAD) + p % PER_HEAD
 
         def build_pos(i):
-            pos = work.tile([P, L], F32)
+            pos = work.tile([P, L], F32, name="pos", tag="pos", bufs=2)
             part = GRID // 4
             for r in range(0, GRID, part):
                 nc.gpsimd.tensor_tensor(
@@ -533,8 +536,11 @@ def tile_relativepositionmultiheadattention_pa_kernel(tc, q, k, x, w_v, rel_w, r
         split_head0_bias()
         for k in range(-2, PAIRS + 3):
             early, last = split_pieces(k)
+            if k == 1:
+                load_late_head(2)
+            if k == 3:
+                load_late_head(3)
             on(k + 1, build_pos, plain)
-            on(k - 1, invert_sums)
             on(k, biased_max, biased)
             on(k + 1, scores, plain, 0)
             on(k + 1, scores, plain, 1)
@@ -555,11 +561,13 @@ def tile_relativepositionmultiheadattention_pa_kernel(tc, q, k, x, w_v, rel_w, r
             on(k, plain_exp, plain)
             for slot, p in enumerate(weigh_at.get(k, [])):
                 normalise_and_store(p, tiles["o_ps", k][:, slot, :, :])
+            on(k - 1, add_sums)
             on(k - 1, quantise_e, biased)
             on(k - 1, quantise_e, plain)
-            if k == -1:
+            on(k - 1, invert_sums)
+            if k == 1:
                 group_w()
-            if k == 0:
+            if k == 3:
                 quantise_w()
             if bias_head(k) is not None:
                 take_bias(bias_head(k))
@@ -575,4 +583,3 @@ def tile_relativepositionmultiheadattention_pa_kernel(tc, q, k, x, w_v, rel_w, r
             on(k + 1, half_max, biased, 1)
             on(k + 2, scores, biased, 0)
             on(k, group_e, plain)
-            on(k, add_sums)

@@ -33,7 +33,7 @@ FLOPS = 2 * L * C * C + 2 * 2 * NH * L * L * D
 TILES = NH * NT
 PER_HEAD = NT // 2
 PAIRS = NH * PER_HEAD
-FIRST_WEIGH = 7
+FIRST_WEIGH = 8
 
 
 def tile_relativepositionmultiheadattention_pa_kernel(tc, q, k, x, w_v, rel_w, rel_h, out):
@@ -295,17 +295,45 @@ def tile_relativepositionmultiheadattention_pa_kernel(tc, q, k, x, w_v, rel_w, r
             t = i % NT
             s_ps = bank("plain" if t < PER_HEAD else "biased", [P, HALF], F32)
             tiles["s_ps", i, h] = s_ps
-            nc.tensor.matmul(
-                out=s_ps[:],
-                lhsT=qT[:, n, P * t : P * (t + 1)],
-                rhs=kT[:, n, HALF * h : HALF * (h + 1)],
-                start=True,
-                stop=t < PER_HEAD,
-            )
-            if t < PER_HEAD:
-                return
             t -= PER_HEAD
-            if n == 0:
+            turns_first = n > 0 and t >= 0 and h == 0
+
+            def multiply():
+                nc.tensor.matmul(
+                    out=s_ps[:],
+                    lhsT=qT[:, n, P * (i % NT) : P * (i % NT + 1)],
+                    rhs=kT[:, n, HALF * h : HALF * (h + 1)],
+                    start=not turns_first,
+                    stop=t < 0 or turns_first,
+                )
+
+            def turn():
+                wide_cols, wide_rows = tiles["wide", n]
+                blocks = HALF // P
+                for b in range(blocks):
+                    nc.tensor.matmul(
+                        out=s_ps[:, P * b : P * (b + 1)],
+                        lhsT=wide_cols[:, t, :],
+                        rhs=ident_f32[:],
+                        start=turns_first and b == 0,
+                        stop=False,
+                        is_transpose=True,
+                    )
+                by_cols = s_ps[:].rearrange("p (r b g) -> p b r g", b=blocks, g=COLS)
+                for b in range(blocks):
+                    nc.tensor.matmul(
+                        out=by_cols[:, b, :, :],
+                        lhsT=wide_rows[:, t, h, :],
+                        rhs=swap[:],
+                        start=False,
+                        stop=not turns_first and b == blocks - 1,
+                        is_transpose=True,
+                    )
+
+            if turns_first:
+                turn()
+            multiply()
+            if t >= 0 and n == 0:
                 nc.tensor.matmul(
                     out=s_ps[:],
                     lhsT=head0_bias[:, t, :],
@@ -313,28 +341,8 @@ def tile_relativepositionmultiheadattention_pa_kernel(tc, q, k, x, w_v, rel_w, r
                     start=False,
                     stop=True,
                 )
-                return
-            wide_cols, wide_rows = tiles["wide", n]
-            blocks = HALF // P
-            for b in range(blocks):
-                nc.tensor.matmul(
-                    out=s_ps[:, P * b : P * (b + 1)],
-                    lhsT=wide_cols[:, t, :],
-                    rhs=ident_f32[:],
-                    start=False,
-                    stop=False,
-                    is_transpose=True,
-                )
-            by_cols = s_ps[:].rearrange("p (r b g) -> p b r g", b=blocks, g=COLS)
-            for b in range(blocks):
-                nc.tensor.matmul(
-                    out=by_cols[:, b, :, :],
-                    lhsT=wide_rows[:, t, h, :],
-                    rhs=swap[:],
-                    start=False,
-                    stop=b == blocks - 1,
-                    is_transpose=True,
-                )
+            elif t >= 0 and not turns_first:
+                turn()
 
         def add_bias(i, h):
             if h == 0:
@@ -467,16 +475,16 @@ def tile_relativepositionmultiheadattention_pa_kernel(tc, q, k, x, w_v, rel_w, r
 
         pieces = {
             0: [("k", 1)],
-            1: [("q", 1)],
-            2: [("x", 0), ("x", 1)],
-            3: [("x", 2), ("x", 3)],
+            1: [("q", 1), ("x", 0)],
+            2: [("x", 1), ("x", 2)],
+            3: [("x", 3)],
             4: [("v", 0, 0), ("k", 2)],
-            5: [("v", 0, 1), ("q", 2)],
-            6: [("v", 1, 0)],
+            5: [("v", 0, 1)],
+            6: [("q", 2), ("v", 1, 0)],
             7: [("v", 1, 1)],
-            8: [("v", 2, 0)],
-            9: [("k", 3), ("v", 2, 1)],
-            10: [("q", 3)],
+            8: [("k", 3)],
+            9: [("v", 2, 0)],
+            10: [("q", 3), ("v", 2, 1)],
             11: [("v", 3, 0)],
             12: [("v", 3, 1)],
         }
@@ -556,9 +564,9 @@ def tile_relativepositionmultiheadattention_pa_kernel(tc, q, k, x, w_v, rel_w, r
             on(k, half_exp, biased, 1)
             on(k + 1, half_max, biased, 0)
             on(k + 1, scores, biased, 1)
+            on(k, plain_exp, plain)
             for piece in early:
                 take_piece(piece)
-            on(k, plain_exp, plain)
             for slot, p in enumerate(weigh_at.get(k, [])):
                 normalise_and_store(p, tiles["o_ps", k][:, slot, :, :])
             on(k - 1, add_sums)

@@ -111,6 +111,7 @@ def tile_relativepositionmultiheadattention_pa_kernel(tc, q, k, x, w_v, rel_w, r
         load_q(0)
         load_rows(0)
         load_k(1)
+        load_q(1)
         load_rows(1)
         load_cols(nc.sync, NT, 2 * NT)
         w_sb = keep.tile([P, PACK, C], BF16)
@@ -118,7 +119,6 @@ def tile_relativepositionmultiheadattention_pa_kernel(tc, q, k, x, w_v, rel_w, r
             out=w_sb[:].rearrange("p (u e) c -> p u (e c)", e=2),
             in_=w_v.rearrange("(u p e) c -> p u (e c)", u=2, e=2),
         )
-        load_q(1)
         x_sb = keep.tile([P, NT * C], BF16)
         x_in = x_sb[:].rearrange("p (u k) -> p u k", k=2 * C)
         x_rows = x.rearrange("b h w c -> (b h w) c").rearrange("(u p e) c -> p u (e c)", p=P, e=2)
@@ -454,7 +454,9 @@ def tile_relativepositionmultiheadattention_pa_kernel(tc, q, k, x, w_v, rel_w, r
 
         def add_sums(p):
             total = late.tile([P, 2], F32)
-            nc.vector.tensor_reduce(out=total[:], in_=row_sums[:, both(p), :], axis=AX.X, op=ALU.add)
+            nc.gpsimd.tensor_tensor(
+                out=total[:], in0=row_sums[:, both(p), 0], in1=row_sums[:, both(p), 1], op=ALU.add
+            )
             tiles["total", p] = total
 
         def invert_sums(p):
@@ -474,13 +476,14 @@ def tile_relativepositionmultiheadattention_pa_kernel(tc, q, k, x, w_v, rel_w, r
             nc.sync.dma_start(out=paired_rows[p % PER_HEAD][:, :, D * n : D * (n + 1)], in_=o_sb[:])
 
         pieces = {
-            0: [("k", 1)],
-            1: [("q", 1), ("x", 0)],
-            2: [("x", 1), ("x", 2)],
-            3: [("x", 3)],
-            4: [("v", 0, 0), ("k", 2)],
-            5: [("v", 0, 1)],
-            6: [("q", 2), ("v", 1, 0)],
+            -1: [("k", 1), ("q", 1)],
+            0: [("x", 0)],
+            1: [("x", 1), ("x", 2)],
+            2: [("x", 3)],
+            3: [("v", 0, 0)],
+            4: [("k", 2), ("v", 0, 1)],
+            5: [("q", 2)],
+            6: [("v", 1, 0)],
             7: [("v", 1, 1)],
             8: [("k", 3)],
             9: [("v", 2, 0)],
@@ -548,6 +551,7 @@ def tile_relativepositionmultiheadattention_pa_kernel(tc, q, k, x, w_v, rel_w, r
                 load_late_head(2)
             if k == 3:
                 load_late_head(3)
+            on(k - 1, add_sums)
             on(k + 1, build_pos, plain)
             on(k, biased_max, biased)
             on(k + 1, scores, plain, 0)
@@ -567,15 +571,14 @@ def tile_relativepositionmultiheadattention_pa_kernel(tc, q, k, x, w_v, rel_w, r
             on(k, plain_exp, plain)
             for piece in early:
                 take_piece(piece)
-            for slot, p in enumerate(weigh_at.get(k, [])):
-                normalise_and_store(p, tiles["o_ps", k][:, slot, :, :])
-            on(k - 1, add_sums)
             on(k - 1, quantise_e, biased)
             on(k - 1, quantise_e, plain)
-            on(k - 1, invert_sums)
-            if k == 1:
+            on(k - 2, invert_sums)
+            for slot, p in enumerate(weigh_at.get(k, [])):
+                normalise_and_store(p, tiles["o_ps", k][:, slot, :, :])
+            if k == 0:
                 group_w()
-            if k == 3:
+            if k == 2:
                 quantise_w()
             if bias_head(k) is not None:
                 take_bias(bias_head(k))

@@ -295,45 +295,17 @@ def tile_relativepositionmultiheadattention_pa_kernel(tc, q, k, x, w_v, rel_w, r
             t = i % NT
             s_ps = bank("plain" if t < PER_HEAD else "biased", [P, HALF], F32)
             tiles["s_ps", i, h] = s_ps
+            nc.tensor.matmul(
+                out=s_ps[:],
+                lhsT=qT[:, n, P * t : P * (t + 1)],
+                rhs=kT[:, n, HALF * h : HALF * (h + 1)],
+                start=True,
+                stop=t < PER_HEAD,
+            )
+            if t < PER_HEAD:
+                return
             t -= PER_HEAD
-            turns_first = n > 0 and t >= 0 and h == 0
-
-            def multiply():
-                nc.tensor.matmul(
-                    out=s_ps[:],
-                    lhsT=qT[:, n, P * (i % NT) : P * (i % NT + 1)],
-                    rhs=kT[:, n, HALF * h : HALF * (h + 1)],
-                    start=not turns_first,
-                    stop=t < 0 or turns_first,
-                )
-
-            def turn():
-                wide_cols, wide_rows = tiles["wide", n]
-                blocks = HALF // P
-                for b in range(blocks):
-                    nc.tensor.matmul(
-                        out=s_ps[:, P * b : P * (b + 1)],
-                        lhsT=wide_cols[:, t, :],
-                        rhs=ident_f32[:],
-                        start=turns_first and b == 0,
-                        stop=False,
-                        is_transpose=True,
-                    )
-                by_cols = s_ps[:].rearrange("p (r b g) -> p b r g", b=blocks, g=COLS)
-                for b in range(blocks):
-                    nc.tensor.matmul(
-                        out=by_cols[:, b, :, :],
-                        lhsT=wide_rows[:, t, h, :],
-                        rhs=swap[:],
-                        start=False,
-                        stop=not turns_first and b == blocks - 1,
-                        is_transpose=True,
-                    )
-
-            if turns_first:
-                turn()
-            multiply()
-            if t >= 0 and n == 0:
+            if n == 0:
                 nc.tensor.matmul(
                     out=s_ps[:],
                     lhsT=head0_bias[:, t, :],
@@ -341,8 +313,28 @@ def tile_relativepositionmultiheadattention_pa_kernel(tc, q, k, x, w_v, rel_w, r
                     start=False,
                     stop=True,
                 )
-            elif t >= 0 and not turns_first:
-                turn()
+                return
+            wide_cols, wide_rows = tiles["wide", n]
+            blocks = HALF // P
+            for b in range(blocks):
+                nc.tensor.matmul(
+                    out=s_ps[:, P * b : P * (b + 1)],
+                    lhsT=wide_cols[:, t, :],
+                    rhs=ident_f32[:],
+                    start=False,
+                    stop=False,
+                    is_transpose=True,
+                )
+            by_cols = s_ps[:].rearrange("p (r b g) -> p b r g", b=blocks, g=COLS)
+            for b in range(blocks):
+                nc.tensor.matmul(
+                    out=by_cols[:, b, :, :],
+                    lhsT=wide_rows[:, t, h, :],
+                    rhs=swap[:],
+                    start=False,
+                    stop=b == blocks - 1,
+                    is_transpose=True,
+                )
 
         def add_bias(i, h):
             if h == 0:
@@ -476,7 +468,6 @@ def tile_relativepositionmultiheadattention_pa_kernel(tc, q, k, x, w_v, rel_w, r
             nc.sync.dma_start(out=paired_rows[p % PER_HEAD][:, :, D * n : D * (n + 1)], in_=o_sb[:])
 
         pieces = {
-            -1: [("k", 1), ("q", 1)],
             0: [("x", 0)],
             1: [("x", 1), ("x", 2)],
             2: [("x", 3)],
@@ -593,4 +584,8 @@ def tile_relativepositionmultiheadattention_pa_kernel(tc, q, k, x, w_v, rel_w, r
                 take_piece(piece)
             on(k + 1, half_max, biased, 1)
             on(k + 2, scores, biased, 0)
+            if k == -1:
+                for what in ("k", "q"):
+                    turn_rows(what, 1, "turned")
+                    take_rows(what, 1)
             on(k, group_e, plain)

from contextlib import ExitStack

import concourse.mybir as mybir
from concourse.masks import make_identity

F32 = mybir.dt.float32
BF16 = mybir.dt.bfloat16
U32 = mybir.dt.uint32
U8 = mybir.dt.uint8
FP8X4 = mybir.dt.float8_e4m3fn_x4
ALU = mybir.AluOpType
ACT = mybir.ActivationFunctionType
AX = mybir.AxisListType

P = 128
PACK = 4
GRID = 32
L = GRID * GRID
C = 512
NH = 4
D = 128
NT = L // P
NG = L // (P * PACK)
HALF = 512
REL = 2 * GRID - 1
ROWS = P // GRID
BANK_ROWS = HALF // GRID
COLS = P // BANK_ROWS
SCALE = 1.0 / (D ** 0.5)
ROOT = D ** 0.5

FLOPS = 2 * L * C * C + 2 * 2 * NH * L * L * D
TILES = NH * NT
PER_HEAD = NT // 2
PAIRS = NH * PER_HEAD
FIRST_WEIGH = 8


def tile_relativepositionmultiheadattention_pa_kernel(tc, q, k, x, w_v, rel_w, rel_h, out):
    nc = tc.nc
    with ExitStack() as ctx:
        ctx.enter_context(tc.manual_schedule())
        keep = ctx.enter_context(tc.tile_pool(name="keep", bufs=1))
        work = ctx.enter_context(tc.tile_pool(name="work", bufs=4))
        late = ctx.enter_context(tc.tile_pool(name="late", bufs=18))
        psum = ctx.enter_context(tc.psum_pool(name="psum", bufs=1))

        banks = {"biased": 3, "plain": 2, "turned": 2, "out": 1}

        def bank(use, shape, dtype):
            return psum.tile(shape, dtype, name=use, tag=use, bufs=banks[use])

        ident_bf = keep.tile([P, P], BF16)
        make_identity(nc, ident_bf[:])
        ident_f32 = keep.tile([P, P], F32)
        make_identity(nc, ident_f32[:])
        swap = keep.tile([P, P], F32)
        nc.vector.tensor_copy(
            out=swap[:].rearrange("p (r g) -> p r g", g=COLS), in_=ident_f32[:].rearrange("p (g r) -> p r g", g=COLS)
        )
        wrap = keep.tile([P, 2 * GRID], BF16)
        nc.gpsimd.tensor_tensor(
            out=wrap[:], in0=ident_bf[:, 0 : 2 * GRID], in1=ident_bf[:, 2 * GRID : 4 * GRID], op=ALU.add
        )
        spread = keep.tile([P, L], BF16)
        nc.gpsimd.tensor_tensor(
            out=spread[:].rearrange("p (a b) -> p a b", b=GRID),
            in0=wrap[:, 0:GRID].unsqueeze(1).to_broadcast([P, GRID, GRID]),
            in1=wrap[:, GRID : 2 * GRID].unsqueeze(2).to_broadcast([P, GRID, GRID]),
            op=ALU.add,
        )
        row_sums = keep.tile([P, TILES, 2], F32)
        nc.gpsimd.memset(row_sums[:], 0.0)

        col_bias = keep.tile([P, TILES, GRID], BF16)
        row_bias = keep.tile([P, TILES, GRID], BF16)
        skew = REL - 1
        rw = rel_w.rearrange("b n r c m -> (b n r) (c m)")[:, GRID - 1 : GRID - 1 + skew * GRID]
        rw = rw.rearrange("a (c j) -> a c j", j=skew)[:, :, 0:GRID]
        rw = rw.rearrange("(i rl) c j -> rl c i j", rl=ROWS)
        rh = rel_h.rearrange("b n c r m -> (b n c) (r m)")[:, GRID - 1 : GRID - 1 + skew * GRID]
        rh = rh.rearrange("a (r j) -> a r j", j=skew)[:, :, 0:GRID]
        rh = rh.rearrange("(n c) (t rl) j -> n rl c t j", c=GRID, rl=ROWS)

        def load_cols(queue, first, last):
            for rl in range(ROWS):
                rows = slice(GRID * rl, GRID * (rl + 1))
                queue.dma_start(out=col_bias[rows, first:last, :], in_=rw[rl][:, first:last, :])

        def load_rows(n):
            for rl in range(ROWS):
                rows = slice(GRID * rl, GRID * (rl + 1))
                nc.sync.dma_start(out=row_bias[rows, NT * n : NT * (n + 1), :], in_=rh[n, rl])

        load_cols(nc.scalar, 0, NT)
        q_rows = q.rearrange("b n (t p) d -> (b n) p t d", p=P)
        k_rows = k.rearrange("b n (t p) d -> (b n) p t d", p=P)
        q_sb = []
        k_sb = []
        for n in range(NH):
            k_sb.append(keep.tile([P, NT, D], BF16, name="k_sb%d" % n))
            q_sb.append(keep.tile([P, NT, D], BF16, name="q_sb%d" % n))

        def load_k(n):
            nc.sync.dma_start(out=k_sb[n][:], in_=k_rows[n])

        def load_q(n):
            nc.sync.dma_start(out=q_sb[n][:], in_=q_rows[n])

        load_k(0)
        load_q(0)
        load_rows(0)
        load_k(1)
        load_q(1)
        load_rows(1)
        load_cols(nc.sync, NT, 2 * NT)
        w_sb = keep.tile([P, PACK, C], BF16)
        nc.sync.dma_start(
            out=w_sb[:].rearrange("p (u e) c -> p u (e c)", e=2),
            in_=w_v.rearrange("(u p e) c -> p u (e c)", u=2, e=2),
        )
        x_sb = keep.tile([P, NT * C], BF16)
        x_in = x_sb[:].rearrange("p (u k) -> p u k", k=2 * C)
        x_rows = x.rearrange("b h w c -> (b h w) c").rearrange("(u p e) c -> p u (e c)", p=P, e=2)
        for half in range(2):
            nc.sync.dma_start(out=x_in[:, 2 * half : 2 * half + 2, :], in_=x_rows[:, 2 * half : 2 * half + 2, :])

        def load_late_head(n):
            load_cols(nc.sync, NT * n, NT * (n + 1))
            load_rows(n)
            load_k(n)
            load_q(n)

        tiles = {}

        qT = keep.tile([P, NH, L], BF16)
        kT = keep.tile([P, NH, L], BF16)

        def turn_rows(what, n, use):
            rows_sb = (k_sb if what == "k" else q_sb)[n]
            turned = bank(use, [P, NT, P], BF16)
            for t in range(NT):
                nc.tensor.transpose(out=turned[:, t, :], in_=rows_sb[:, t, :], identity=ident_bf[:])
            tiles[what, n] = turned

        def take_rows(what, n):
            target = kT if what == "k" else qT
            nc.scalar.copy(out=target[:, n, :], in_=tiles[what, n][:].rearrange("p t l -> p (t l)"))

        x_codes = keep.tile([P, L], U32, align_bytes=64)
        x_scales = keep.tile([P, L], U8, align_bytes=64)
        w_codes = keep.tile([P, C], U32, align_bytes=64)
        w_scales = keep.tile([P, C], U8, align_bytes=64)
        v_codes = keep.tile([P, NG, NH, D], U32, align_bytes=64)
        v_scales = keep.tile([P, NG, NH, D], U8, align_bytes=64)
        x_grouped = keep.tile([P, L * PACK], BF16, align_bytes=64)
        w_grouped = keep.tile([P, C, PACK], BF16, align_bytes=64)
        v_grouped = keep.tile([P, NH, NG, D, PACK], BF16, align_bytes=64)

        def group_w():
            nc.gpsimd.tensor_scalar(
                out=w_grouped[:],
                in0=w_sb[:].rearrange("p t c -> p c t"),
                scalar1=1.0,
                scalar2=0.0,
                op0=ALU.mult,
                op1=ALU.add,
            )

        def quantise_w():
            nc.vector.quantize_mx(
                out=w_codes[:].bitcast(FP8X4), scales=w_scales[:], in_=w_grouped[:].rearrange("p c t -> p (c t)")
            )

        def turn_x(b, use):
            x_words = x_sb[:].bitcast(F32)
            turned = bank(use, [P, 2, 2, P], F32)
            for tt in range(2):
                for u in range(2):
                    first = (C // 2) * (2 * b + tt) + P * u
                    nc.tensor.transpose(
                        out=turned[:, tt, u, :], in_=x_words[:, first : first + P], identity=ident_f32[:]
                    )
            tiles["x", b] = turned

        def take_x(b):
            grouped_words = x_grouped[:].bitcast(F32).rearrange("p (l u) -> p l u", u=2)
            grouped = grouped_words[:, 2 * P * b : 2 * P * (b + 1), :].rearrange("p (t l) u -> p t l u", t=2)
            words = tiles["x", b][:].rearrange("p t u l -> p t l u")
            nc.scalar.copy(out=grouped, in_=words)

        def quantise_x(half):
            cols = slice(HALF * half, HALF * (half + 1))
            nc.vector.quantize_mx(
                out=x_codes[:, cols].bitcast(FP8X4),
                scales=x_scales[:, cols],
                in_=x_grouped[:, PACK * HALF * half : PACK * HALF * (half + 1)],
            )

        def project_values(n, g, use):
            v_ps = bank(use, [P, PACK, D], F32)
            for j in range(PACK):
                rows = slice(P * (PACK * g + j), P * (PACK * g + j + 1))
                cols = slice(D * n, D * (n + 1))
                nc.tensor.matmul_mx(
                    out=v_ps[:, j, :],
                    lhsT=x_codes[:, rows].bitcast(FP8X4),
                    lhsT_scale=x_scales[:, rows],
                    rhs=w_codes[:, cols].bitcast(FP8X4),
                    rhs_scale=w_scales[:, cols],
                    start=True,
                    stop=True,
                )
            tiles["v", n, g] = v_ps

        def take_values(n, g):
            grouped = v_grouped[:, n, g, :, :]
            by_keys = tiles["v", n, g][:].rearrange("p j d -> p d j")
            nc.scalar.copy(out=grouped, in_=by_keys)

        def quantise_v(n, g):
            nc.vector.quantize_mx(
                out=v_codes[:, g, n, :].bitcast(FP8X4),
                scales=v_scales[:, g, n, :],
                in_=v_grouped[:, n, g, :, :].rearrange("p d j -> p (d j)"),
            )

        halves = keep.tile([P, PER_HEAD, 2, 2, GRID], BF16)
        head0_bias = keep.tile([P, PER_HEAD, P], BF16)

        def split_head0_bias():
            for kind, rel in enumerate((col_bias, row_bias)):
                rel = rel[:, PER_HEAD:NT, :]
                high = halves[:, :, 0, kind, :]
                nc.gpsimd.tensor_scalar(out=high, in0=rel, scalar1=ROOT, scalar2=0.0, op0=ALU.mult, op1=ALU.add)
                nc.vector.scalar_tensor_tensor(
                    out=halves[:, :, 1, kind, :], in0=rel, scalar=ROOT, in1=high, op0=ALU.mult, op1=ALU.subtract
                )
            turned = bank("out", [P, PER_HEAD, P], BF16)
            for t in range(PER_HEAD):
                flat = halves[:, t, :, :, :].rearrange("p h k j -> p (h k j)")
                nc.tensor.transpose(out=turned[:, t, :], in_=flat, identity=ident_bf[:])
            nc.scalar.copy(out=head0_bias[:], in_=turned[:])

        out_rows = out.rearrange("b h w c -> (b h w) c")
        park = [out_rows[2 * P * n : 2 * P * (n + 1), D * (NH - 1) : D * NH] for n in range(NH)]

        def turn_bias(n):
            turned = bank("turned", [P, 2, P], BF16)
            for kind, rel in enumerate((col_bias, row_bias)):
                flat = rel[:, NT * n + PER_HEAD : NT * (n + 1), :].rearrange("p t j -> p (t j)")
                nc.tensor.transpose(out=turned[:, kind, :], in_=flat, identity=ident_bf[:])
            tiles["turned_bias", n] = turned

        def take_bias(n):
            tall = keep.tile([P, 2, P], F32, name="tall%d" % n)
            nc.vector.tensor_scalar(
                out=tall[:], in0=tiles["turned_bias", n][:], scalar1=ROOT, scalar2=0.0, op0=ALU.mult, op1=ALU.add
            )
            nc.sync.dma_start(out=park[n].rearrange("(k p) q -> p k q", p=P), in_=tall[:])
            wide_cols = keep.tile([P, PER_HEAD, P], F32, name="wide_cols%d" % n)
            for rl in range(ROWS):
                nc.sync.dma_start(
                    out=wide_cols[GRID * rl : GRID * (rl + 1), :, :],
                    in_=park[n][0:P, :].rearrange("(t j) q -> j t q", j=GRID),
                )
            wide_rows = keep.tile([P, PER_HEAD, 2, P], F32, name="wide_rows%d" % n)
            for g in range(COLS):
                nc.sync.dma_start(
                    out=wide_rows[BANK_ROWS * g : BANK_ROWS * (g + 1), :, :, :].rearrange("r t h q -> r (t h) q"),
                    in_=park[n][P : 2 * P, :].rearrange("(th r) q -> r th q", r=BANK_ROWS),
                )
            tiles["wide", n] = (wide_cols, wide_rows)

        def biased(p):
            return NT * (p // PER_HEAD) + PER_HEAD + p % PER_HEAD

        def plain(p):
            return NT * (p // PER_HEAD) + p % PER_HEAD

        def build_pos(i):
            pos = work.tile([P, L], F32, name="pos", tag="pos", bufs=2)
            part = GRID // 4
            for r in range(0, GRID, part):
                nc.gpsimd.tensor_tensor(
                    out=pos[:, GRID * r : GRID * (r + part)].rearrange("p (a b) -> p a b", b=GRID),
                    in0=col_bias[:, i, :].unsqueeze(1).to_broadcast([P, part, GRID]),
                    in1=row_bias[:, i, r : r + part].unsqueeze(2).to_broadcast([P, part, GRID]),
                    op=ALU.add,
                )
            tiles["pos", i] = pos

        def scores(i, h):
            n = i // NT
            t = i % NT
            s_ps = bank("plain" if t < PER_HEAD else "biased", [P, HALF], F32)
            tiles["s_ps", i, h] = s_ps
            nc.tensor.matmul(
                out=s_ps[:],
                lhsT=qT[:, n, P * t : P * (t + 1)],
                rhs=kT[:, n, HALF * h : HALF * (h + 1)],
                start=True,
                stop=t < PER_HEAD,
            )
            if t < PER_HEAD:
                return
            t -= PER_HEAD
            if n == 0:
                nc.tensor.matmul(
                    out=s_ps[:],
                    lhsT=head0_bias[:, t, :],
                    rhs=spread[:, HALF * h : HALF * (h + 1)],
                    start=False,
                    stop=True,
                )
                return
            wide_cols, wide_rows = tiles["wide", n]
            blocks = HALF // P
            for b in range(blocks):
                nc.tensor.matmul(
                    out=s_ps[:, P * b : P * (b + 1)],
                    lhsT=wide_cols[:, t, :],
                    rhs=ident_f32[:],
                    start=False,
                    stop=False,
                    is_transpose=True,
                )
            by_cols = s_ps[:].rearrange("p (r b g) -> p b r g", b=blocks, g=COLS)
            for b in range(blocks):
                nc.tensor.matmul(
                    out=by_cols[:, b, :, :],
                    lhsT=wide_rows[:, t, h, :],
                    rhs=swap[:],
                    start=False,
                    stop=b == blocks - 1,
                    is_transpose=True,
                )

        def add_bias(i, h):
            if h == 0:
                s = work.tile([P, L], F32)
                tiles["s", i] = s
            cols = slice(HALF * h, HALF * (h + 1))
            nc.vector.scalar_tensor_tensor(
                out=tiles["s", i][:, cols],
                in0=tiles["s_ps", i, h][:],
                scalar=SCALE,
                in1=tiles["pos", i][:, cols],
                op0=ALU.mult,
                op1=ALU.add,
            )

        def plain_max(i):
            neg_max = late.tile([P, 1], F32)
            nc.vector.tensor_reduce(out=neg_max[:], in_=tiles["s", i][:], axis=AX.X, op=ALU.max, negate=True)
            tiles["neg_max", i] = neg_max

        def half_max(i, h):
            if h == 0:
                neg_maxes = late.tile([P, 2], F32)
                tiles["neg_maxes", i] = neg_maxes
            nc.vector.tensor_reduce(
                out=tiles["neg_maxes", i][:, h : h + 1], in_=tiles["s_ps", i, h][:], axis=AX.X, op=ALU.max, negate=True
            )

        def biased_max(i):
            neg_max = late.tile([P, 1], F32)
            neg_maxes = tiles["neg_maxes", i]
            nc.vector.tensor_scalar(
                out=neg_max[:],
                in0=neg_maxes[:, 0:1],
                scalar1=neg_maxes[:, 1:2],
                scalar2=SCALE,
                op0=ALU.min,
                op1=ALU.mult,
            )
            tiles["neg_max", i] = neg_max

        def plain_exp(i):
            e = work.tile([P, L], BF16)
            nc.scalar.activation(
                out=e[:],
                in_=tiles["s", i][:],
                func=ACT.Exp,
                bias=tiles["neg_max", i][:, 0:1],
                scale=1.0,
                accum_out=row_sums[:, i, 0:1],
            )
            tiles["e", i] = e

        def half_exp(i, h):
            if h == 0:
                e = work.tile([P, L], BF16)
                tiles["e", i] = e
            nc.scalar.activation(
                out=tiles["e", i][:, HALF * h : HALF * (h + 1)],
                in_=tiles["s_ps", i, h][:],
                func=ACT.Exp,
                bias=tiles["neg_max", i][:, 0:1],
                scale=SCALE,
                accum_out=row_sums[:, i, h : h + 1],
            )

        def turn_e(i):
            turned = bank("turned", [P, NT // 2, P], F32)
            e_words = tiles["e", i][:].bitcast(F32)
            for b in range(NT // 2):
                nc.tensor.transpose(out=turned[:, b, :], in_=e_words[:, P * b : P * (b + 1)], identity=ident_f32[:])
            tiles["turned_e", i] = turned

        def group_e(i):
            e_grouped = work.tile([P, NG, P, PACK], BF16, align_bytes=64)
            grouped_words = e_grouped[:].rearrange("p g m j -> p (g m j)").bitcast(F32)
            nc.scalar.copy(
                out=grouped_words.rearrange("p (g m u) -> p g m u", g=NG, u=2),
                in_=tiles["turned_e", i][:].rearrange("p (g u) m -> p g m u", g=NG),
            )
            tiles["e_grouped", i] = e_grouped

        def quantise_e(i):
            e_codes = late.tile([P, NG, P], U32, align_bytes=64)
            e_scales = late.tile([P, NG, P], U8, align_bytes=64)
            nc.vector.quantize_mx(
                out=e_codes[:].rearrange("p g m -> p (g m)").bitcast(FP8X4),
                scales=e_scales[:].rearrange("p g m -> p (g m)"),
                in_=tiles["e_grouped", i][:].rearrange("p g m j -> p (g m j)"),
            )
            tiles["e_codes", i] = (e_codes, e_scales)

        def weigh_values(i, o_ps):
            n = i // NT
            e_codes, e_scales = tiles["e_codes", i]
            for g in range(NG):
                nc.tensor.matmul_mx(
                    out=o_ps,
                    lhsT=e_codes[:, g, :].bitcast(FP8X4),
                    lhsT_scale=e_scales[:, g, :],
                    rhs=v_codes[:, g, n, :].bitcast(FP8X4),
                    rhs_scale=v_scales[:, g, n, :],
                    start=(g == 0),
                    stop=(g == NG - 1),
                )

        def both(p):
            return slice(plain(p), biased(p) + 1, PER_HEAD)

        def add_sums(p):
            total = late.tile([P, 2], F32)
            nc.gpsimd.tensor_tensor(
                out=total[:], in0=row_sums[:, both(p), 0], in1=row_sums[:, both(p), 1], op=ALU.add
            )
            tiles["total", p] = total

        def invert_sums(p):
            inverse = late.tile([P, 2], F32)
            nc.vector.reciprocal(out=inverse[:], in_=tiles["total", p][:])
            tiles["inverse", p] = inverse

        paired_rows = out_rows.rearrange("(s t p) c -> t p s c", s=2, p=P)

        def normalise_and_store(p, o_ps):
            n = p // PER_HEAD
            o_sb = work.tile([P, 2, D], F32)
            for s in range(2):
                nc.scalar.activation(
                    out=o_sb[:, s, :], in_=o_ps[:, s, :], func=ACT.Copy, scale=tiles["inverse", p][:, s : s + 1]
                )
            nc.sync.dma_start(out=paired_rows[p % PER_HEAD][:, :, D * n : D * (n + 1)], in_=o_sb[:])

        pieces = {
            0: [("x", 0)],
            1: [("x", 1), ("x", 2)],
            2: [("x", 3)],
            3: [("v", 0, 0)],
            4: [("k", 2), ("v", 0, 1)],
            5: [("q", 2)],
            6: [("v", 1, 0)],
            7: [("v", 1, 1)],
            8: [("k", 3)],
            9: [("v", 2, 0)],
            10: [("q", 3), ("v", 2, 1)],
            11: [("v", 3, 0)],
            12: [("v", 3, 1)],
        }

        def start_piece(piece, use):
            if piece[0] in ("k", "q"):
                turn_rows(*piece, use)
            elif piece[0] == "x":
                turn_x(piece[1], use)
            else:
                project_values(*piece[1:], use)

        def take_piece(piece):
            if piece[0] in ("k", "q"):
                take_rows(*piece)
            elif piece[0] == "x":
                take_x(piece[1])
            else:
                take_values(*piece[1:])

        def finish_piece(piece):
            if piece[0] == "v":
                quantise_v(*piece[1:])
            elif piece[0] == "x" and piece[1] % 2 == 1:
                quantise_x(piece[1] // 2)

        def split_pieces(k):
            todo = pieces.get(k, [])
            return (todo[:-1], todo[-1:]) if k < FIRST_WEIGH else (todo, [])

        def bias_head(k):
            return k // PER_HEAD + 1 if k % PER_HEAD == 0 and 0 <= k < PAIRS - PER_HEAD else None

        weigh_at = {}
        p = 0
        for k in range(FIRST_WEIGH, PAIRS + 3):
            for step in range(2):
                if p <= min(k - 2, PAIRS - 1):
                    weigh_at.setdefault(k, []).append(p)
                    p += 1

        def weigh(k):
            if k in weigh_at:
                o_ps = bank("out", [P, 2, 2, D], F32)
                for slot, p in enumerate(weigh_at[k]):
                    weigh_values(plain(p), o_ps[:, slot, 0, :])
                    weigh_values(biased(p), o_ps[:, slot, 1, :])
                tiles["o_ps", k] = o_ps

        def on(p, stage, tile_of=None, *half):
            if 0 <= p < PAIRS:
                stage(p if tile_of is None else tile_of(p), *half)

        for what in ("k", "q"):
            turn_rows(what, 0, "turned")
            take_rows(what, 0)
        split_head0_bias()
        for k in range(-2, PAIRS + 3):
            early, last = split_pieces(k)
            if k == 1:
                load_late_head(2)
            if k == 3:
                load_late_head(3)
            on(k - 1, add_sums)
            on(k + 1, build_pos, plain)
            on(k, biased_max, biased)
            on(k + 1, scores, plain, 0)
            on(k + 1, scores, plain, 1)
            on(k, plain_max, plain)
            on(k, half_exp, biased, 0)
            for piece in early:
                start_piece(piece, "turned")
            for piece in last:
                start_piece(piece, "out")
            if bias_head(k) is not None:
                turn_bias(bias_head(k))
            weigh(k)
            on(k, half_exp, biased, 1)
            on(k + 1, half_max, biased, 0)
            on(k + 1, scores, biased, 1)
            on(k, plain_exp, plain)
            for piece in early:
                take_piece(piece)
            on(k - 1, quantise_e, biased)
            on(k - 1, quantise_e, plain)
            on(k - 2, invert_sums)
            for slot, p in enumerate(weigh_at.get(k, [])):
                normalise_and_store(p, tiles["o_ps", k][:, slot, :, :])
            if k == 0:
                group_w()
            if k == 2:
                quantise_w()
            if bias_head(k) is not None:
                take_bias(bias_head(k))
            for piece in pieces.get(k - 1, []):
                finish_piece(piece)
            on(k + 1, add_bias, plain, 0)
            on(k, turn_e, biased)
            on(k + 1, add_bias, plain, 1)
            on(k, turn_e, plain)
            on(k, group_e, biased)
            for piece in last:
                take_piece(piece)
            on(k + 1, half_max, biased, 1)
            on(k + 2, scores, biased, 0)
            if k == -1:
                for what in ("k", "q"):
                    turn_rows(what, 1, "turned")
                    take_rows(what, 1)
            on(k, group_e, plain)
